import numpy as np
import ml_dtypes


def mxq(x, axis, fmt="e4m3"):
    dtype, down = {"e4m3": (ml_dtypes.float8_e4m3fn, 7), "e5m2": (ml_dtypes.float8_e5m2, 14)}[fmt]
    v = np.moveaxis(np.asarray(x, np.float32).astype(ml_dtypes.bfloat16).astype(np.float64), axis, -1)
    blocks = v.reshape(v.shape[:-1] + (-1, 32))
    amax = np.abs(blocks).max(-1, keepdims=True)
    byte = np.maximum(np.where(amax > 0, np.frexp(amax)[1] - 1 + 127, 0) - down, 1)
    scale = np.exp2(byte - 127.0)
    codes = (blocks / scale).astype(np.float32).astype(dtype).astype(np.float64)
    return np.moveaxis((codes * scale).reshape(v.shape), -1, axis)


WIDE = False


def mx_kscale(k):
    if not WIDE:
        return np.ones(k)
    levels = np.array([10, -10, 5, -5, 0])
    a = np.random.permutation(np.resize(levels, k // 512 * 4)).reshape(k // 512, 4)
    idx = np.arange(k)
    return np.exp2(a[idx // 512, idx % 128 // 32])


BF16 = ml_dtypes.bfloat16


def bf(x):
    return np.asarray(x, np.float32).astype(BF16)


def f64(x):
    return np.asarray(x).astype(np.float64)


N, C, H, W, K, S = 16, 1024, 32, 32, 32, 3
P = H * W
M = K * (S + 1)
ALPHA = 100.0
EPS = 1e-12
SX = 0.25
LOGIT = 3.5


def softmax(v, axis):
    e = np.exp(v - v.max(axis=axis, keepdims=True))
    return e / e.sum(axis=axis, keepdims=True)


def setup_inputs():
    s = mx_kscale(C)
    s = s / s.min()
    gain = 1.0 + 0.1 * np.random.standard_normal((K, S + 1, 1))
    x = np.random.standard_normal((N, C, H, W)) * SX * s[None, :, None, None]
    centroids = np.random.standard_normal((K, S + 1, C)) * gain * LOGIT / (2.0 * ALPHA * SX * np.sqrt(C)) / s
    return {"x": bf(x), "centroids": bf(centroids)}


def reference(x, centroids):
    cen = f64(centroids)
    xf = f64(x).reshape(N, C, P)
    c_flat = cen.reshape(M, C)
    w = 2.0 * ALPHA * c_flat
    b = -ALPHA * np.sqrt((c_flat ** 2).sum(axis=1))
    z = mxq(xf, 1, "e4m3").transpose(0, 2, 1) @ mxq(w, 1, "e4m3").T
    conv_out = z.transpose(0, 2, 1) + b[None, :, None]
    conv_out = conv_out.reshape(N, K, S + 1, P)
    soft_assign = softmax(conv_out, 1) * softmax(conv_out, 2)
    mult = np.prod(1.0 + soft_assign, axis=2)
    rep = cen[:, 0, :]
    out = (mxq(mult, 2, "e4m3") @ mxq(xf, 2, "e4m3").transpose(0, 2, 1)) - rep[None, :, :] * mult.sum(axis=-1)[:, :, None]
    out = out / np.maximum(np.sqrt((out ** 2).sum(axis=2, keepdims=True)), EPS)
    out = out.reshape(N, K * C)
    out = out / np.maximum(np.sqrt((out ** 2).sum(axis=1, keepdims=True)), EPS)
    return out

@@ -1,0 +1,366 @@
+from contextlib import ExitStack
+
+import concourse.mybir as mybir
+from concourse.masks import make_identity
+
+F32 = mybir.dt.float32
+BF16 = mybir.dt.bfloat16
+U32 = mybir.dt.uint32
+U8 = mybir.dt.uint8
+FP8X4 = mybir.dt.float8_e4m3fn_x4
+ALU = mybir.AluOpType
+ACT = mybir.ActivationFunctionType
+AX = mybir.AxisListType
+
+P = 128
+N_IMG = 16
+C = 1024
+PIX = 1024
+K = 32
+S4 = 4
+EPS = 1e-12
+WV = 128
+AHEAD = 2
+
+FLOPS = 2 * N_IMG * C * PIX * (K * S4) + 2 * N_IMG * K * PIX * C
+
+
+def tile_sralnet_pa_t_kernel(tc, x, centroids, out):
+    nc = tc.nc
+    tail = nc.vector
+    with ExitStack() as ctx:
+        const = ctx.enter_context(tc.tile_pool(name="const", bufs=1))
+        rawp = ctx.enter_context(tc.tile_pool(name="rawp", bufs=3))
+        g1p = ctx.enter_context(tc.tile_pool(name="g1p", bufs=2))
+        c1p = ctx.enter_context(tc.tile_pool(name="c1p", bufs=2))
+        g2p = ctx.enter_context(tc.tile_pool(name="g2p", bufs=2))
+        c2p = ctx.enter_context(tc.tile_pool(name="c2p", bufs=2))
+        zbp = ctx.enter_context(tc.tile_pool(name="zbp", bufs=3))
+        smp = ctx.enter_context(tc.tile_pool(name="smp", bufs=3))
+        epi = ctx.enter_context(tc.tile_pool(name="epi", bufs=2))
+        ps_zt = ctx.enter_context(tc.psum_pool(name="ps_zt", bufs=2))
+        ps_z = ctx.enter_context(tc.psum_pool(name="ps_z", bufs=2))
+        ps_xt = ctx.enter_context(tc.psum_pool(name="ps_xt", bufs=2))
+        ps_v = ctx.enter_context(tc.psum_pool(name="ps_v", bufs=1))
+
+        c_sb = const.tile([P, C], BF16, name="c_sb")
+        for s in range(S4):
+            nc.sync.dma_start(out=c_sb[32 * s : 32 * s + 32, :], in_=centroids[:, s, :])
+        rep4 = const.tile([P, C], BF16, name="rep4")
+        for i in range(4):
+            nc.scalar.dma_start(out=rep4[32 * i : 32 * i + 32, :], in_=centroids[:, 0, :])
+
+        warm = const.tile([P, 1], F32, name="warm")
+        nc.vector.memset(warm[:], 0.0)
+        warm2 = const.tile([P, 1], F32, name="warm2")
+        nc.scalar.activation(out=warm2[:], in_=warm[:], func=ACT.Exp)
+
+        ident_f = const.tile([P, P], F32, name="ident_f")
+        make_identity(nc, ident_f[:])
+        ident_b = const.tile([P, P], BF16, name="ident_b")
+        make_identity(nc, ident_b[:])
+        half = const.tile([P, 1], F32, name="half")
+        nc.vector.memset(half[:], 0.5)
+        ones2 = const.tile([P, 2], F32, name="ones2")
+        nc.vector.memset(ones2[:], 1.0)
+        bd = const.tile([P, P], F32, name="bd")
+        nc.vector.memset(bd[:], 0.0)
+        for i in range(4):
+            nc.vector.memset(bd[32 * i : 32 * i + 32, 32 * i : 32 * i + 32], 1.0)
+        mb = [const.tile([P, 2, P, 4], BF16, name="mb%d" % i, align_bytes=64) for i in range(4)]
+        for i in range(4):
+            nc.vector.memset(mb[i][:], 0.0)
+
+        pt = ps_xt.tile([P, 8, P], BF16, tag="xt", name="pt")
+        for r in range(8):
+            nc.tensor.transpose(pt[:, r, :], c_sb[:, P * r : P * r + P], ident_b[:])
+        wg = const.tile([P, 2, P, 4], BF16, name="wg", align_bytes=64)
+        nc.vector.tensor_scalar_mul(
+            out=wg[:], in0=pt[:].rearrange("p (g j) m -> p g m j", j=4), scalar1=200.0
+        )
+        w_codes = const.tile([P, 2 * P], U32, name="w_codes", align_bytes=64)
+        w_scales = const.tile([P, 2 * P], U8, name="w_scales", align_bytes=64)
+        nc.vector.quantize_mx(
+            out=w_codes[:].bitcast(FP8X4),
+            scales=w_scales[:],
+            in_=wg[:].rearrange("p g m j -> p (g m j)"),
+        )
+
+        junk0 = epi.tile([P, C], BF16, tag="sq", name="junk0")
+        css = const.tile([P, 1], F32, name="css")
+        nc.scalar.activation(out=junk0[:], in_=c_sb[:], func=ACT.Square, accum_out=css[:])
+        cn = const.tile([P, 1], F32, name="cn")
+        nc.gpsimd.tensor_tensor(out=cn[:], in0=css[:], in1=half[:], op=ALU.pow)
+        bvec = const.tile([P, 1], F32, name="bvec")
+        nc.vector.tensor_scalar_mul(out=bvec[:], in0=cn[:], scalar1=-100.0)
+
+        raws = {}
+        zbts = {}
+        mults = {}
+        state = {}
+
+        def stage_a(n):
+            raw = rawp.tile([P, 8, PIX], BF16, tag="raw", name="raw")
+            raws[n] = raw
+            for g in range(2):
+                nc.sync.dma_start(
+                    out=raw[:, 4 * g : 4 * g + 4, :],
+                    in_=x[n, 512 * g : 512 * g + 512].rearrange("(j p) h w -> p j (h w)", p=P),
+                )
+            c1 = c1p.tile([P, 2, PIX], U32, tag="c1", name="c1", align_bytes=64)
+            s1x = c1p.tile([P, 2, PIX], U8, tag="s1x", name="s1x", align_bytes=64)
+            for g in range(2):
+                g1 = g1p.tile([P, PIX, 4], BF16, tag="g1", name="g1", align_bytes=64)
+                if WV > 0:
+                    nc.vector.tensor_copy(
+                        out=g1[:, 0:WV, :].rearrange("p (c i) t -> p c t i", i=4),
+                        in_=raw[:, 4 * g : 4 * g + 4, 0:WV].rearrange("p t (c i) -> p c t i", i=4),
+                    )
+                nc.scalar.copy(
+                    out=g1[:, WV:PIX, :].rearrange("p (c i) t -> p c t i", i=4),
+                    in_=raw[:, 4 * g : 4 * g + 4, WV:PIX].rearrange("p t (c i) -> p c t i", i=4),
+                )
+                nc.vector.quantize_mx(
+                    out=c1[:, g, :].bitcast(FP8X4),
+                    scales=s1x[:, g, :],
+                    in_=g1[:].rearrange("p w j -> p (w j)"),
+                )
+            zbt = zbp.tile([P, PIX], F32, tag="zbt", name="zbt")
+            zbts[n] = zbt
+            for h in range(2):
+                zt = ps_zt.tile([P, 512], F32, tag="zT", name="zt")
+                for g in range(2):
+                    nc.tensor.matmul_mx(
+                        out=zt[:],
+                        lhsT=w_codes[:, P * g : P * g + P].bitcast(FP8X4),
+                        lhsT_scale=w_scales[:, P * g : P * g + P],
+                        rhs=c1[:, g, 512 * h : 512 * h + 512].bitcast(FP8X4),
+                        rhs_scale=s1x[:, g, 512 * h : 512 * h + 512],
+                        start=(g == 0),
+                        stop=(g == 1),
+                    )
+                nc.scalar.activation(
+                    out=zbt[:, 512 * h : 512 * h + 512],
+                    in_=zt[:],
+                    func=ACT.Identity,
+                    bias=bvec[:, 0:1],
+                    scale=1.0,
+                )
+
+        def stage_b(n):
+            i = n % 4
+            zbt = zbts[n]
+            z_ps = []
+            for gp in range(2):
+                zp = ps_z.tile([P, 4, S4, K], F32, tag="z", name="zp")
+                for u in range(2):
+                    for e in range(2):
+                        wb = 2 * gp + u
+                        nc.tensor.transpose(
+                            zp[:, 2 * u + e].rearrange("q s k -> q (s k)"),
+                            zbt[:, 256 * wb + e : 256 * wb + 256 : 2],
+                            ident_f[:],
+                        )
+                z_ps.append(zp)
+            msk = smp.tile([P, 8, K], F32, tag="msk", name="msk")
+            negmk = smp.tile([P, 8, S4], F32, tag="negmk", name="negmk")
+            e2 = smp.tile([P, 8, S4, K], F32, tag="e2", name="e2")
+            e1 = smp.tile([P, 8, S4, K], F32, tag="e1", name="e1")
+            s1 = smp.tile([P, 8, S4], F32, tag="s1", name="s1")
+            for gp in range(2):
+                ts = slice(4 * gp, 4 * gp + 4)
+                nc.vector.tensor_reduce(
+                    out=negmk[:, ts, :], in_=z_ps[gp][:], axis=AX.X, op=ALU.max, negate=True
+                )
+                nc.vector.tensor_reduce(
+                    out=msk[:, ts, :],
+                    in_=z_ps[gp][:].rearrange("q t s k -> q t k s"),
+                    axis=AX.X,
+                    op=ALU.max,
+                )
+                nc.vector.tensor_tensor(
+                    out=e2[:, ts],
+                    in0=z_ps[gp][:],
+                    in1=msk[:, ts, :].unsqueeze(2).to_broadcast([P, 4, S4, K]),
+                    op=ALU.subtract,
+                )
+            for t in range(8):
+                for s in range(S4):
+                    nc.scalar.activation(
+                        out=e1[:, t, s, :],
+                        in_=z_ps[t // 4][:, t % 4, s, :],
+                        func=ACT.Exp,
+                        bias=negmk[:, t, s : s + 1],
+                        scale=1.0,
+                        accum_out=s1[:, t, s : s + 1],
+                    )
+            nc.scalar.activation(out=e2[:], in_=e2[:], func=ACT.Exp)
+            s2 = smp.tile([P, 8, K], F32, tag="s2", name="s2")
+            nc.vector.tensor_reduce(
+                out=s2[:], in_=e2[:].rearrange("q t s k -> q t k s"), axis=AX.X, op=ALU.add
+            )
+            r1 = smp.tile([P, 8, S4], F32, tag="r1", name="r1")
+            nc.vector.reciprocal(out=r1[:], in_=s1[:])
+            r2 = smp.tile([P, 8, K], F32, tag="r2", name="r2")
+            nc.vector.reciprocal(out=r2[:], in_=s2[:])
+            tail.tensor_tensor(out=e1[:], in0=e1[:], in1=e2[:], op=ALU.mult)
+            tail.tensor_tensor(
+                out=e1[:].rearrange("q t s k -> q (t s) k"),
+                in0=e1[:].rearrange("q t s k -> q (t s) k"),
+                in1=r1[:].rearrange("q t s -> q (t s)").unsqueeze(2).to_broadcast([P, 32, K]),
+                op=ALU.mult,
+            )
+            tail.tensor_tensor(
+                out=e1[:],
+                in0=e1[:],
+                in1=r2[:].unsqueeze(2).to_broadcast([P, 8, S4, K]),
+                op=ALU.mult,
+            )
+            t1 = smp.tile([P, 8, 2 * K], F32, tag="t1", name="t1")
+            nc.vector.tensor_scalar_add(
+                out=t1[:], in0=e1[:, :, 2:4, :].rearrange("q t s k -> q t (s k)"), scalar1=1.0
+            )
+            uu = smp.tile([P, 8, 2 * K], F32, tag="uu", name="uu")
+            nc.vector.scalar_tensor_tensor(
+                out=uu[:],
+                in0=e1[:, :, 0:2, :].rearrange("q t s k -> q t (s k)"),
+                scalar=1.0,
+                in1=t1[:],
+                op0=ALU.add,
+                op1=ALU.mult,
+            )
+            multf = smp.tile([P, 8, K], F32, tag="multf", name="multf")
+            nc.vector.tensor_tensor(
+                out=multf[:], in0=uu[:, :, 0:K], in1=uu[:, :, K : 2 * K], op=ALU.mult
+            )
+            nc.vector.tensor_copy(
+                out=mb[i][:, :, K * i : K * i + K, :],
+                in_=multf[:].rearrange("q (g t) k -> q g k t", g=2),
+            )
+            if i == 0:
+                state["msp"] = smp.tile([P, P], F32, tag="msp", name="msp")
+            nc.vector.tensor_reduce(
+                out=state["msp"][:, K * i : K * i + K],
+                in_=multf[:].rearrange("q t k -> q k t"),
+                axis=AX.X,
+                op=ALU.add,
+            )
+            mc = smp.tile([P, 2 * P], U32, tag="mc", name="mc", align_bytes=64)
+            msc = smp.tile([P, 2 * P], U8, tag="msc", name="msc", align_bytes=64)
+            nc.vector.quantize_mx(
+                out=mc[:].bitcast(FP8X4),
+                scales=msc[:],
+                in_=mb[i][:].rearrange("q g c t -> q (g c t)"),
+            )
+            mults[n] = (mc, msc)
+
+        def stage_c(n):
+            i = n % 4
+            grp = n // 4
+            raw_w = raws[n][:].bitcast(F32)
+            c2 = c2p.tile([P, 2, C], U32, tag="c2", name="c2", align_bytes=64)
+            s2x = c2p.tile([P, 2, C], U8, tag="s2x", name="s2x", align_bytes=64)
+            for gp in range(2):
+                g2 = g2p.tile([P, 4 * C], BF16, tag="g2", name="g2", align_bytes=64)
+                g2w = g2[:].bitcast(F32).rearrange("q (c u) -> q c u", u=2)
+                for rp in range(4):
+                    xt = ps_xt.tile([P, 2, 2, P], F32, tag="xt", name="xt")
+                    for rl in range(2):
+                        for u in range(2):
+                            wb = 2 * gp + u
+                            nc.tensor.transpose(
+                                xt[:, rl, u, :],
+                                raw_w[:, 2 * rp + rl, P * wb : P * wb + P],
+                                ident_f[:],
+                            )
+                    nc.scalar.copy(
+                        out=g2w[:, 256 * rp : 256 * rp + 256, :].rearrange(
+                            "q (rl p) u -> q rl p u", rl=2
+                        ),
+                        in_=xt[:].rearrange("q rl u p -> q rl p u"),
+                    )
+                nc.vector.quantize_mx(
+                    out=c2[:, gp, :].bitcast(FP8X4), scales=s2x[:, gp, :], in_=g2[:]
+                )
+            mc, msc = mults[n]
+            if i == 0:
+                state["v"] = [
+                    ps_v.tile([P, 512], F32, tag="v%d" % hc, name="v_ps%d" % hc) for hc in range(2)
+                ]
+            v_ps = state["v"]
+            for hc in range(2):
+                for gp in range(2):
+                    nc.tensor.matmul_mx(
+                        out=v_ps[hc][:],
+                        lhsT=mc[:, P * gp : P * gp + P].bitcast(FP8X4),
+                        lhsT_scale=msc[:, P * gp : P * gp + P],
+                        rhs=c2[:, gp, 512 * hc : 512 * hc + 512].bitcast(FP8X4),
+                        rhs_scale=s2x[:, gp, 512 * hc : 512 * hc + 512],
+                        start=(i == 0 and gp == 0),
+                        stop=(i == 3 and gp == 1),
+                    )
+            if i != 3:
+                return
+            pss = ps_zt.tile([P, 512], F32, tag="zT", name="pss")
+            nc.tensor.matmul(
+                out=pss[:, 0:2], lhsT=state["msp"][:], rhs=ones2[:], start=True, stop=True
+            )
+            negms = epi.tile([P, 1], F32, tag="negms", name="negms")
+            nc.vector.tensor_scalar_mul(out=negms[:], in0=pss[:, 0:1], scalar1=-1.0)
+            v2 = epi.tile([P, C], F32, tag="v2", name="v2")
+            for hc in range(2):
+                nc.vector.scalar_tensor_tensor(
+                    out=v2[:, 512 * hc : 512 * hc + 512],
+                    in0=rep4[:, 512 * hc : 512 * hc + 512],
+                    scalar=negms[:, 0:1],
+                    in1=v_ps[hc][:],
+                    op0=ALU.mult,
+                    op1=ALU.add,
+                )
+            sq = epi.tile([P, C], BF16, tag="sq", name="sq")
+            ss = epi.tile([P, 1], F32, tag="ss", name="ss")
+            nc.scalar.activation(out=sq[:], in_=v2[:], func=ACT.Square, accum_out=ss[:])
+            n1 = epi.tile([P, 1], F32, tag="n1", name="n1")
+            nc.gpsimd.tensor_tensor(out=n1[:], in0=ss[:], in1=half[:], op=ALU.pow)
+            n1c = epi.tile([P, 1], F32, tag="n1c", name="n1c")
+            nc.vector.tensor_scalar_max(out=n1c[:], in0=n1[:], scalar1=EPS)
+            rn1 = epi.tile([P, 1], F32, tag="rn1", name="rn1")
+            nc.vector.reciprocal(out=rn1[:], in_=n1c[:])
+            q2 = epi.tile([P, 2], F32, tag="q2", name="q2")
+            nc.vector.tensor_scalar(
+                out=q2[:],
+                in0=ss[:, 0:1].to_broadcast([P, 2]),
+                scalar1=rn1[:, 0:1],
+                scalar2=rn1[:, 0:1],
+                op0=ALU.mult,
+                op1=ALU.mult,
+            )
+            nc.tensor.matmul(out=pss[:, 2:4], lhsT=bd[:], rhs=q2[:], start=True, stop=True)
+            tot = epi.tile([P, 1], F32, tag="tot", name="tot")
+            nc.vector.tensor_copy(out=tot[:], in_=pss[:, 2:3])
+            n2 = epi.tile([P, 1], F32, tag="n2", name="n2")
+            nc.gpsimd.tensor_tensor(out=n2[:], in0=tot[:], in1=half[:], op=ALU.pow)
+            den = epi.tile([P, 1], F32, tag="den", name="den")
+            nc.vector.tensor_scalar(
+                out=den[:],
+                in0=n2[:],
+                scalar1=EPS,
+                scalar2=n1c[:, 0:1],
+                op0=ALU.max,
+                op1=ALU.mult,
+            )
+            fsc = epi.tile([P, 1], F32, tag="fsc", name="fsc")
+            nc.vector.reciprocal(out=fsc[:], in_=den[:])
+            nc.vector.tensor_scalar_mul(out=v2[:], in0=v2[:], scalar1=fsc[:, 0:1])
+            nc.sync.dma_start(
+                out=out[4 * grp : 4 * grp + 4, :].rearrange("i (k c) -> (i k) c", c=C),
+                in_=v2[:],
+            )
+
+        for n in range(AHEAD):
+            stage_a(n)
+        for n in range(N_IMG):
+            stage_b(n)
+            if n + AHEAD < N_IMG:
+                stage_a(n + AHEAD)
+            stage_c(n)

@@ -19,7 +19,7 @@ PIX = 1024
 K = 32
 S4 = 4
 EPS = 1e-12
-WV = 128
+WV = 352
 AHEAD = 2
 
 FLOPS = 2 * N_IMG * C * PIX * (K * S4) + 2 * N_IMG * K * PIX * C
@@ -27,7 +27,7 @@ FLOPS = 2 * N_IMG * C * PIX * (K * S4) + 2 * N_IMG * K * PIX * C
 
 def tile_sralnet_pa_t_kernel(tc, x, centroids, out):
     nc = tc.nc
-    tail = nc.vector
+    tail = nc.gpsimd
     with ExitStack() as ctx:
         const = ctx.enter_context(tc.tile_pool(name="const", bufs=1))
         rawp = ctx.enter_context(tc.tile_pool(name="rawp", bufs=3))

@@ -19,7 +19,8 @@ PIX = 1024
 K = 32
 S4 = 4
 EPS = 1e-12
-WV = 352
+NB = 4
+WV = 672
 AHEAD = 2
 
 FLOPS = 2 * N_IMG * C * PIX * (K * S4) + 2 * N_IMG * K * PIX * C
@@ -27,20 +28,22 @@ FLOPS = 2 * N_IMG * C * PIX * (K * S4) + 2 * N_IMG * K * PIX * C
 
 def tile_sralnet_pa_t_kernel(tc, x, centroids, out):
     nc = tc.nc
-    tail = nc.gpsimd
     with ExitStack() as ctx:
         const = ctx.enter_context(tc.tile_pool(name="const", bufs=1))
-        rawp = ctx.enter_context(tc.tile_pool(name="rawp", bufs=3))
+        rap = ctx.enter_context(tc.tile_pool(name="rap", bufs=3))
+        rbp = ctx.enter_context(tc.tile_pool(name="rbp", bufs=3))
         g1p = ctx.enter_context(tc.tile_pool(name="g1p", bufs=2))
         c1p = ctx.enter_context(tc.tile_pool(name="c1p", bufs=2))
         g2p = ctx.enter_context(tc.tile_pool(name="g2p", bufs=2))
         c2p = ctx.enter_context(tc.tile_pool(name="c2p", bufs=2))
-        zbp = ctx.enter_context(tc.tile_pool(name="zbp", bufs=3))
-        smp = ctx.enter_context(tc.tile_pool(name="smp", bufs=3))
+        zbp = ctx.enter_context(tc.tile_pool(name="zbp", bufs=AHEAD + 1))
+        keep = ctx.enter_context(tc.tile_pool(name="keep", bufs=NB + 1))
+        lsp = ctx.enter_context(tc.tile_pool(name="lsp", bufs=2))
+        smp = ctx.enter_context(tc.tile_pool(name="smp", bufs=2))
         epi = ctx.enter_context(tc.tile_pool(name="epi", bufs=2))
-        ps_zt = ctx.enter_context(tc.psum_pool(name="ps_zt", bufs=2))
+        ps_zt = ctx.enter_context(tc.psum_pool(name="ps_zt", bufs=1))
         ps_z = ctx.enter_context(tc.psum_pool(name="ps_z", bufs=2))
-        ps_xt = ctx.enter_context(tc.psum_pool(name="ps_xt", bufs=2))
+        ps_xt = ctx.enter_context(tc.psum_pool(name="ps_xt", bufs=3))
         ps_v = ctx.enter_context(tc.psum_pool(name="ps_v", bufs=1))
 
         c_sb = const.tile([P, C], BF16, name="c_sb")
@@ -55,10 +58,10 @@ def tile_sralnet_pa_t_kernel(tc, x, centroids, out):
         warm2 = const.tile([P, 1], F32, name="warm2")
         nc.scalar.activation(out=warm2[:], in_=warm[:], func=ACT.Exp)
 
-        ident_f = const.tile([P, P], F32, name="ident_f")
-        make_identity(nc, ident_f[:])
         ident_b = const.tile([P, P], BF16, name="ident_b")
         make_identity(nc, ident_b[:])
+        ident_f = const.tile([P, P], F32, name="ident_f")
+        make_identity(nc, ident_f[:])
         half = const.tile([P, 1], F32, name="half")
         nc.vector.memset(half[:], 0.5)
         ones2 = const.tile([P, 2], F32, name="ones2")
@@ -94,31 +97,27 @@ def tile_sralnet_pa_t_kernel(tc, x, centroids, out):
         bvec = const.tile([P, 1], F32, name="bvec")
         nc.vector.tensor_scalar_mul(out=bvec[:], in0=cn[:], scalar1=-100.0)
 
-        raws = {}
         zbts = {}
-        mults = {}
+        kept = {}
         state = {}
 
         def stage_a(n):
-            raw = rawp.tile([P, 8, PIX], BF16, tag="raw", name="raw")
-            raws[n] = raw
-            for g in range(2):
-                nc.sync.dma_start(
-                    out=raw[:, 4 * g : 4 * g + 4, :],
-                    in_=x[n, 512 * g : 512 * g + 512].rearrange("(j p) h w -> p j (h w)", p=P),
-                )
             c1 = c1p.tile([P, 2, PIX], U32, tag="c1", name="c1", align_bytes=64)
             s1x = c1p.tile([P, 2, PIX], U8, tag="s1x", name="s1x", align_bytes=64)
             for g in range(2):
+                ra = rap.tile([P, 4, PIX], BF16, tag="ra", name="ra")
+                nc.sync.dma_start(
+                    out=ra[:],
+                    in_=x[n, 512 * g : 512 * g + 512].rearrange("(j p) h w -> p j (h w)", p=P),
+                )
                 g1 = g1p.tile([P, PIX, 4], BF16, tag="g1", name="g1", align_bytes=64)
-                if WV > 0:
-                    nc.vector.tensor_copy(
-                        out=g1[:, 0:WV, :].rearrange("p (c i) t -> p c t i", i=4),
-                        in_=raw[:, 4 * g : 4 * g + 4, 0:WV].rearrange("p t (c i) -> p c t i", i=4),
-                    )
+                nc.vector.tensor_copy(
+                    out=g1[:, 0:WV, :].rearrange("p (c i) t -> p c t i", i=4),
+                    in_=ra[:, :, 0:WV].rearrange("p t (c i) -> p c t i", i=4),
+                )
                 nc.scalar.copy(
                     out=g1[:, WV:PIX, :].rearrange("p (c i) t -> p c t i", i=4),
-                    in_=raw[:, 4 * g : 4 * g + 4, WV:PIX].rearrange("p t (c i) -> p c t i", i=4),
+                    in_=ra[:, :, WV:PIX].rearrange("p t (c i) -> p c t i", i=4),
                 )
                 nc.vector.quantize_mx(
                     out=c1[:, g, :].bitcast(FP8X4),
@@ -147,8 +146,11 @@ def tile_sralnet_pa_t_kernel(tc, x, centroids, out):
                     scale=1.0,
                 )
 
-        def stage_b(n):
-            i = n % 4
+        def stage_b1(n):
+            slot = n % NB
+            if slot == 0:
+                state["ls"] = lsp.tile([P, NB, 288], F32, tag="ls", name="ls")
+            ls = state["ls"]
             zbt = zbts[n]
             z_ps = []
             for gp in range(2):
@@ -162,11 +164,10 @@ def tile_sralnet_pa_t_kernel(tc, x, centroids, out):
                             ident_f[:],
                         )
                 z_ps.append(zp)
-            msk = smp.tile([P, 8, K], F32, tag="msk", name="msk")
-            negmk = smp.tile([P, 8, S4], F32, tag="negmk", name="negmk")
-            e2 = smp.tile([P, 8, S4, K], F32, tag="e2", name="e2")
-            e1 = smp.tile([P, 8, S4, K], F32, tag="e1", name="e1")
-            s1 = smp.tile([P, 8, S4], F32, tag="s1", name="s1")
+            msk = keep.tile([P, 8, K], F32, tag="msk", name="msk")
+            negmk = keep.tile([P, 8, S4], F32, tag="negmk", name="negmk")
+            v = keep.tile([P, S4, 8, K], F32, tag="v", name="v")
+            kept[n] = (msk, negmk, v)
             for gp in range(2):
                 ts = slice(4 * gp, 4 * gp + 4)
                 nc.vector.tensor_reduce(
@@ -179,51 +180,82 @@ def tile_sralnet_pa_t_kernel(tc, x, centroids, out):
                     op=ALU.max,
                 )
                 nc.vector.tensor_tensor(
-                    out=e2[:, ts],
-                    in0=z_ps[gp][:],
-                    in1=msk[:, ts, :].unsqueeze(2).to_broadcast([P, 4, S4, K]),
+                    out=v[:, :, ts, :],
+                    in0=z_ps[gp][:].rearrange("q t s k -> q s t k"),
+                    in1=msk[:, ts, :].unsqueeze(1).to_broadcast([P, S4, 4, K]),
                     op=ALU.subtract,
                 )
+            junk = smp.tile([P, K], F32, tag="junk", name="junk")
             for t in range(8):
                 for s in range(S4):
                     nc.scalar.activation(
-                        out=e1[:, t, s, :],
+                        out=junk[:],
                         in_=z_ps[t // 4][:, t % 4, s, :],
                         func=ACT.Exp,
                         bias=negmk[:, t, s : s + 1],
                         scale=1.0,
-                        accum_out=s1[:, t, s : s + 1],
+                        accum_out=ls[:, slot, 4 * t + s : 4 * t + s + 1],
                     )
-            nc.scalar.activation(out=e2[:], in_=e2[:], func=ACT.Exp)
-            s2 = smp.tile([P, 8, K], F32, tag="s2", name="s2")
+            e2 = smp.tile([P, S4, 8 * K], F32, tag="e2", name="e2")
+            nc.scalar.activation(
+                out=e2[:], in_=v[:].rearrange("q s t k -> q s (t k)"), func=ACT.Exp
+            )
             nc.vector.tensor_reduce(
-                out=s2[:], in_=e2[:].rearrange("q t s k -> q t k s"), axis=AX.X, op=ALU.add
+                out=ls[:, slot, 32:288],
+                in_=e2[:].rearrange("q s c -> q c s"),
+                axis=AX.X,
+                op=ALU.add,
             )
-            r1 = smp.tile([P, 8, S4], F32, tag="r1", name="r1")
-            nc.vector.reciprocal(out=r1[:], in_=s1[:])
-            r2 = smp.tile([P, 8, K], F32, tag="r2", name="r2")
-            nc.vector.reciprocal(out=r2[:], in_=s2[:])
-            tail.tensor_tensor(out=e1[:], in0=e1[:], in1=e2[:], op=ALU.mult)
-            tail.tensor_tensor(
-                out=e1[:].rearrange("q t s k -> q (t s) k"),
-                in0=e1[:].rearrange("q t s k -> q (t s) k"),
-                in1=r1[:].rearrange("q t s -> q (t s)").unsqueeze(2).to_broadcast([P, 32, K]),
-                op=ALU.mult,
+
+        def stage_ln():
+            state["lnls"] = state["ls"]
+            nc.scalar.activation(out=state["ls"][:], in_=state["ls"][:], func=ACT.Ln)
+
+        def stage_b2(n):
+            i = n % 4
+            slot = n % NB
+            lnls = state["lnls"]
+            msk, negmk, v = kept[n]
+            nb1 = smp.tile([P, 8, S4], F32, tag="nb1", name="nb1")
+            nc.vector.tensor_tensor(
+                out=nb1[:].rearrange("q t s -> q (t s)"),
+                in0=negmk[:].rearrange("q t s -> q (t s)"),
+                in1=lnls[:, slot, 0:32],
+                op=ALU.subtract,
             )
-            tail.tensor_tensor(
-                out=e1[:],
-                in0=e1[:],
-                in1=r2[:].unsqueeze(2).to_broadcast([P, 8, S4, K]),
-                op=ALU.mult,
+            c2k = smp.tile([P, 8 * K], F32, tag="c2k", name="c2k")
+            nc.vector.tensor_tensor(
+                out=c2k[:],
+                in0=msk[:].rearrange("q t k -> q (t k)"),
+                in1=lnls[:, slot, 32:288],
+                op=ALU.subtract,
             )
-            t1 = smp.tile([P, 8, 2 * K], F32, tag="t1", name="t1")
+            y = smp.tile([P, S4, 8, K], F32, tag="y", name="y")
+            nc.vector.scalar_tensor_tensor(
+                out=y[:].rearrange("q s t k -> q s (t k)"),
+                in0=v[:].rearrange("q s t k -> q s (t k)"),
+                scalar=2.0,
+                in1=c2k[:].unsqueeze(1).to_broadcast([P, S4, 8 * K]),
+                op0=ALU.mult,
+                op1=ALU.add,
+            )
+            for t in range(8):
+                for s in range(S4):
+                    nc.scalar.activation(
+                        out=y[:, s, t, :],
+                        in_=y[:, s, t, :],
+                        func=ACT.Exp,
+                        bias=nb1[:, t, s : s + 1],
+                        scale=1.0,
+                    )
+            t1 = smp.tile([P, 2, 8 * K], F32, tag="t1", name="t1")
             nc.vector.tensor_scalar_add(
-                out=t1[:], in0=e1[:, :, 2:4, :].rearrange("q t s k -> q t (s k)"), scalar1=1.0
+                out=t1[:], in0=y[:, 2:4].rearrange("q s t k -> q s (t k)"), scalar1=1.0
             )
-            uu = smp.tile([P, 8, 2 * K], F32, tag="uu", name="uu")
+            uu = smp.tile([P, 2, 8 * K], F32, tag="uu", name="uu")
             nc.vector.scalar_tensor_tensor(
                 out=uu[:],
-                in0=e1[:, :, 0:2, :].rearrange("q t s k -> q t (s k)"),
+                in0=y[:, 0:2].rearrange("q s t k -> q s (t k)"),
                 scalar=1.0,
                 in1=t1[:],
                 op0=ALU.add,
@@ -231,7 +263,10 @@ def tile_sralnet_pa_t_kernel(tc, x, centroids, out):
             )
             multf = smp.tile([P, 8, K], F32, tag="multf", name="multf")
             nc.vector.tensor_tensor(
-                out=multf[:], in0=uu[:, :, 0:K], in1=uu[:, :, K : 2 * K], op=ALU.mult
+                out=multf[:].rearrange("q t k -> q (t k)"),
+                in0=uu[:, 0, :],
+                in1=uu[:, 1, :],
+                op=ALU.mult,
             )
             nc.vector.tensor_copy(
                 out=mb[i][:, :, K * i : K * i + K, :],
@@ -252,25 +287,29 @@ def tile_sralnet_pa_t_kernel(tc, x, centroids, out):
                 scales=msc[:],
                 in_=mb[i][:].rearrange("q g c t -> q (g c t)"),
             )
-            mults[n] = (mc, msc)
+            state["mc"] = (mc, msc)
 
         def stage_c(n):
             i = n % 4
             grp = n // 4
-            raw_w = raws[n][:].bitcast(F32)
             c2 = c2p.tile([P, 2, C], U32, tag="c2", name="c2", align_bytes=64)
             s2x = c2p.tile([P, 2, C], U8, tag="s2x", name="s2x", align_bytes=64)
             for gp in range(2):
+                rb = rbp.tile([P, 8, 512], BF16, tag="rb", name="rb")
+                nc.sync.dma_start(
+                    out=rb[:],
+                    in_=x[n, :, 16 * gp : 16 * gp + 16, :].rearrange("(r p) h w -> p r (h w)", p=P),
+                )
+                rb_w = rb[:].bitcast(F32)
                 g2 = g2p.tile([P, 4 * C], BF16, tag="g2", name="g2", align_bytes=64)
                 g2w = g2[:].bitcast(F32).rearrange("q (c u) -> q c u", u=2)
                 for rp in range(4):
                     xt = ps_xt.tile([P, 2, 2, P], F32, tag="xt", name="xt")
                     for rl in range(2):
                         for u in range(2):
-                            wb = 2 * gp + u
                             nc.tensor.transpose(
                                 xt[:, rl, u, :],
-                                raw_w[:, 2 * rp + rl, P * wb : P * wb + P],
+                                rb_w[:, 2 * rp + rl, P * u : P * u + P],
                                 ident_f[:],
                             )
                     nc.scalar.copy(
@@ -282,7 +321,7 @@ def tile_sralnet_pa_t_kernel(tc, x, centroids, out):
                 nc.vector.quantize_mx(
                     out=c2[:, gp, :].bitcast(FP8X4), scales=s2x[:, gp, :], in_=g2[:]
                 )
-            mc, msc = mults[n]
+            mc, msc = state["mc"]
             if i == 0:
                 state["v"] = [
                     ps_v.tile([P, 512], F32, tag="v%d" % hc, name="v_ps%d" % hc) for hc in range(2)
@@ -359,8 +398,13 @@ def tile_sralnet_pa_t_kernel(tc, x, centroids, out):
 
         for n in range(AHEAD):
             stage_a(n)
-        for n in range(N_IMG):
-            stage_b(n)
-            if n + AHEAD < N_IMG:
-                stage_a(n + AHEAD)
-            stage_c(n)
+        for n in range(-NB, N_IMG):
+            if n + NB < N_IMG:
+                stage_b1(n + NB)
+                if n + NB + AHEAD < N_IMG:
+                    stage_a(n + NB + AHEAD)
+            if n >= 0:
+                stage_b2(n)
+                stage_c(n)
+            if (n + 1) % NB == 0 and n + NB < N_IMG:
+                stage_ln()

@@ -19,8 +19,7 @@ PIX = 1024
 K = 32
 S4 = 4
 EPS = 1e-12
-NB = 4
-WV = 672
+WV = 224
 AHEAD = 2
 
 FLOPS = 2 * N_IMG * C * PIX * (K * S4) + 2 * N_IMG * K * PIX * C
@@ -28,18 +27,16 @@ FLOPS = 2 * N_IMG * C * PIX * (K * S4) + 2 * N_IMG * K * PIX * C
 
 def tile_sralnet_pa_t_kernel(tc, x, centroids, out):
     nc = tc.nc
+    tail = nc.vector
     with ExitStack() as ctx:
         const = ctx.enter_context(tc.tile_pool(name="const", bufs=1))
-        rap = ctx.enter_context(tc.tile_pool(name="rap", bufs=3))
-        rbp = ctx.enter_context(tc.tile_pool(name="rbp", bufs=3))
+        rawp = ctx.enter_context(tc.tile_pool(name="rawp", bufs=3))
         g1p = ctx.enter_context(tc.tile_pool(name="g1p", bufs=2))
         c1p = ctx.enter_context(tc.tile_pool(name="c1p", bufs=2))
         g2p = ctx.enter_context(tc.tile_pool(name="g2p", bufs=2))
         c2p = ctx.enter_context(tc.tile_pool(name="c2p", bufs=2))
-        zbp = ctx.enter_context(tc.tile_pool(name="zbp", bufs=AHEAD + 1))
-        keep = ctx.enter_context(tc.tile_pool(name="keep", bufs=NB + 1))
-        lsp = ctx.enter_context(tc.tile_pool(name="lsp", bufs=2))
-        smp = ctx.enter_context(tc.tile_pool(name="smp", bufs=2))
+        zbp = ctx.enter_context(tc.tile_pool(name="zbp", bufs=3))
+        smp = ctx.enter_context(tc.tile_pool(name="smp", bufs=3))
         epi = ctx.enter_context(tc.tile_pool(name="epi", bufs=2))
         ps_zt = ctx.enter_context(tc.psum_pool(name="ps_zt", bufs=1))
         ps_z = ctx.enter_context(tc.psum_pool(name="ps_z", bufs=2))
@@ -58,10 +55,10 @@ def tile_sralnet_pa_t_kernel(tc, x, centroids, out):
         warm2 = const.tile([P, 1], F32, name="warm2")
         nc.scalar.activation(out=warm2[:], in_=warm[:], func=ACT.Exp)
 
-        ident_b = const.tile([P, P], BF16, name="ident_b")
-        make_identity(nc, ident_b[:])
         ident_f = const.tile([P, P], F32, name="ident_f")
         make_identity(nc, ident_f[:])
+        ident_b = const.tile([P, P], BF16, name="ident_b")
+        make_identity(nc, ident_b[:])
         half = const.tile([P, 1], F32, name="half")
         nc.vector.memset(half[:], 0.5)
         ones2 = const.tile([P, 2], F32, name="ones2")
@@ -97,28 +94,36 @@ def tile_sralnet_pa_t_kernel(tc, x, centroids, out):
         bvec = const.tile([P, 1], F32, name="bvec")
         nc.vector.tensor_scalar_mul(out=bvec[:], in0=cn[:], scalar1=-100.0)
 
+        raws = {}
         zbts = {}
-        kept = {}
+        mults = {}
         state = {}
 
         def stage_a(n):
+            raw = rawp.tile([P, 8, PIX], BF16, tag="raw", name="raw")
+            raws[n] = raw
+            for g in range(2):
+                nc.sync.dma_start(
+                    out=raw[:, 4 * g : 4 * g + 4, :],
+                    in_=x[n, 512 * g : 512 * g + 512].rearrange("(j p) h w -> p j (h w)", p=P),
+                )
             c1 = c1p.tile([P, 2, PIX], U32, tag="c1", name="c1", align_bytes=64)
             s1x = c1p.tile([P, 2, PIX], U8, tag="s1x", name="s1x", align_bytes=64)
             for g in range(2):
-                ra = rap.tile([P, 4, PIX], BF16, tag="ra", name="ra")
-                nc.sync.dma_start(
-                    out=ra[:],
-                    in_=x[n, 512 * g : 512 * g + 512].rearrange("(j p) h w -> p j (h w)", p=P),
-                )
                 g1 = g1p.tile([P, PIX, 4], BF16, tag="g1", name="g1", align_bytes=64)
+                wv = 672 if n < 2 else WV
                 nc.vector.tensor_copy(
-                    out=g1[:, 0:WV, :].rearrange("p (c i) t -> p c t i", i=4),
-                    in_=ra[:, :, 0:WV].rearrange("p t (c i) -> p c t i", i=4),
+                    out=g1[:, 0:wv, :].rearrange("p (c i) t -> p c t i", i=4),
+                    in_=raw[:, 4 * g : 4 * g + 4, 0:wv].rearrange("p t (c i) -> p c t i", i=4),
                 )
-                nc.scalar.copy(
-                    out=g1[:, WV:PIX, :].rearrange("p (c i) t -> p c t i", i=4),
-                    in_=ra[:, :, WV:PIX].rearrange("p t (c i) -> p c t i", i=4),
-                )
+                step = (PIX - wv) // 4
+                for w0 in range(wv, PIX, step):
+                    nc.scalar.copy(
+                        out=g1[:, w0 : w0 + step, :].rearrange("p (c i) t -> p c t i", i=4),
+                        in_=raw[:, 4 * g : 4 * g + 4, w0 : w0 + step].rearrange(
+                            "p t (c i) -> p c t i", i=4
+                        ),
+                    )
                 nc.vector.quantize_mx(
                     out=c1[:, g, :].bitcast(FP8X4),
                     scales=s1x[:, g, :],
@@ -146,11 +151,8 @@ def tile_sralnet_pa_t_kernel(tc, x, centroids, out):
                     scale=1.0,
                 )
 
-        def stage_b1(n):
-            slot = n % NB
-            if slot == 0:
-                state["ls"] = lsp.tile([P, NB, 288], F32, tag="ls", name="ls")
-            ls = state["ls"]
+        def stage_b(n):
+            i = n % 4
             zbt = zbts[n]
             z_ps = []
             for gp in range(2):
@@ -164,10 +166,11 @@ def tile_sralnet_pa_t_kernel(tc, x, centroids, out):
                             ident_f[:],
                         )
                 z_ps.append(zp)
-            msk = keep.tile([P, 8, K], F32, tag="msk", name="msk")
-            negmk = keep.tile([P, 8, S4], F32, tag="negmk", name="negmk")
-            v = keep.tile([P, S4, 8, K], F32, tag="v", name="v")
-            kept[n] = (msk, negmk, v)
+            msk = smp.tile([P, 8, K], F32, tag="msk", name="msk")
+            negmk = smp.tile([P, 8, S4], F32, tag="negmk", name="negmk")
+            e2 = smp.tile([P, 8, S4, K], F32, tag="e2", name="e2")
+            e1 = smp.tile([P, 8, S4, K], F32, tag="e1", name="e1")
+            s1 = smp.tile([P, 8, S4], F32, tag="s1", name="s1")
             for gp in range(2):
                 ts = slice(4 * gp, 4 * gp + 4)
                 nc.vector.tensor_reduce(
@@ -180,82 +183,51 @@ def tile_sralnet_pa_t_kernel(tc, x, centroids, out):
                     op=ALU.max,
                 )
                 nc.vector.tensor_tensor(
-                    out=v[:, :, ts, :],
-                    in0=z_ps[gp][:].rearrange("q t s k -> q s t k"),
-                    in1=msk[:, ts, :].unsqueeze(1).to_broadcast([P, S4, 4, K]),
+                    out=e2[:, ts],
+                    in0=z_ps[gp][:],
+                    in1=msk[:, ts, :].unsqueeze(2).to_broadcast([P, 4, S4, K]),
                     op=ALU.subtract,
                 )
-            junk = smp.tile([P, K], F32, tag="junk", name="junk")
             for t in range(8):
                 for s in range(S4):
                     nc.scalar.activation(
-                        out=junk[:],
+                        out=e1[:, t, s, :],
                         in_=z_ps[t // 4][:, t % 4, s, :],
                         func=ACT.Exp,
                         bias=negmk[:, t, s : s + 1],
                         scale=1.0,
-                        accum_out=ls[:, slot, 4 * t + s : 4 * t + s + 1],
+                        accum_out=s1[:, t, s : s + 1],
                     )
-            e2 = smp.tile([P, S4, 8 * K], F32, tag="e2", name="e2")
-            nc.scalar.activation(
-                out=e2[:], in_=v[:].rearrange("q s t k -> q s (t k)"), func=ACT.Exp
-            )
+            nc.scalar.activation(out=e2[:], in_=e2[:], func=ACT.Exp)
+            s2 = smp.tile([P, 8, K], F32, tag="s2", name="s2")
             nc.vector.tensor_reduce(
-                out=ls[:, slot, 32:288],
-                in_=e2[:].rearrange("q s c -> q c s"),
-                axis=AX.X,
-                op=ALU.add,
+                out=s2[:], in_=e2[:].rearrange("q t s k -> q t k s"), axis=AX.X, op=ALU.add
             )
-
-        def stage_ln():
-            state["lnls"] = state["ls"]
-            nc.scalar.activation(out=state["ls"][:], in_=state["ls"][:], func=ACT.Ln)
-
-        def stage_b2(n):
-            i = n % 4
-            slot = n % NB
-            lnls = state["lnls"]
-            msk, negmk, v = kept[n]
-            nb1 = smp.tile([P, 8, S4], F32, tag="nb1", name="nb1")
-            nc.vector.tensor_tensor(
-                out=nb1[:].rearrange("q t s -> q (t s)"),
-                in0=negmk[:].rearrange("q t s -> q (t s)"),
-                in1=lnls[:, slot, 0:32],
-                op=ALU.subtract,
+            r1 = smp.tile([P, 8, S4], F32, tag="r1", name="r1")
+            nc.vector.reciprocal(out=r1[:], in_=s1[:])
+            r2 = smp.tile([P, 8, K], F32, tag="r2", name="r2")
+            nc.vector.reciprocal(out=r2[:], in_=s2[:])
+            tail.tensor_tensor(out=e1[:], in0=e1[:], in1=e2[:], op=ALU.mult)
+            tail.tensor_tensor(
+                out=e1[:].rearrange("q t s k -> q (t s) k"),
+                in0=e1[:].rearrange("q t s k -> q (t s) k"),
+                in1=r1[:].rearrange("q t s -> q (t s)").unsqueeze(2).to_broadcast([P, 32, K]),
+                op=ALU.mult,
             )
-            c2k = smp.tile([P, 8 * K], F32, tag="c2k", name="c2k")
-            nc.vector.tensor_tensor(
-                out=c2k[:],
-                in0=msk[:].rearrange("q t k -> q (t k)"),
-                in1=lnls[:, slot, 32:288],
-                op=ALU.subtract,
+            tail.tensor_tensor(
+                out=e1[:],
+                in0=e1[:],
+                in1=r2[:].unsqueeze(2).to_broadcast([P, 8, S4, K]),
+                op=ALU.mult,
             )
-            y = smp.tile([P, S4, 8, K], F32, tag="y", name="y")
-            nc.vector.scalar_tensor_tensor(
-                out=y[:].rearrange("q s t k -> q s (t k)"),
-                in0=v[:].rearrange("q s t k -> q s (t k)"),
-                scalar=2.0,
-                in1=c2k[:].unsqueeze(1).to_broadcast([P, S4, 8 * K]),
-                op0=ALU.mult,
-                op1=ALU.add,
-            )
-            for t in range(8):
-                for s in range(S4):
-                    nc.scalar.activation(
-                        out=y[:, s, t, :],
-                        in_=y[:, s, t, :],
-                        func=ACT.Exp,
-                        bias=nb1[:, t, s : s + 1],
-                        scale=1.0,
-                    )
-            t1 = smp.tile([P, 2, 8 * K], F32, tag="t1", name="t1")
+            t1 = smp.tile([P, 8, 2 * K], F32, tag="t1", name="t1")
             nc.vector.tensor_scalar_add(
-                out=t1[:], in0=y[:, 2:4].rearrange("q s t k -> q s (t k)"), scalar1=1.0
+                out=t1[:], in0=e1[:, :, 2:4, :].rearrange("q t s k -> q t (s k)"), scalar1=1.0
             )
-            uu = smp.tile([P, 2, 8 * K], F32, tag="uu", name="uu")
+            uu = smp.tile([P, 8, 2 * K], F32, tag="uu", name="uu")
             nc.vector.scalar_tensor_tensor(
                 out=uu[:],
-                in0=y[:, 0:2].rearrange("q s t k -> q s (t k)"),
+                in0=e1[:, :, 0:2, :].rearrange("q t s k -> q t (s k)"),
                 scalar=1.0,
                 in1=t1[:],
                 op0=ALU.add,
@@ -263,10 +235,7 @@ def tile_sralnet_pa_t_kernel(tc, x, centroids, out):
             )
             multf = smp.tile([P, 8, K], F32, tag="multf", name="multf")
             nc.vector.tensor_tensor(
-                out=multf[:].rearrange("q t k -> q (t k)"),
-                in0=uu[:, 0, :],
-                in1=uu[:, 1, :],
-                op=ALU.mult,
+                out=multf[:], in0=uu[:, :, 0:K], in1=uu[:, :, K : 2 * K], op=ALU.mult
             )
             nc.vector.tensor_copy(
                 out=mb[i][:, :, K * i : K * i + K, :],
@@ -287,29 +256,25 @@ def tile_sralnet_pa_t_kernel(tc, x, centroids, out):
                 scales=msc[:],
                 in_=mb[i][:].rearrange("q g c t -> q (g c t)"),
             )
-            state["mc"] = (mc, msc)
+            mults[n] = (mc, msc)
 
         def stage_c(n):
             i = n % 4
             grp = n // 4
+            raw_w = raws[n][:].bitcast(F32)
             c2 = c2p.tile([P, 2, C], U32, tag="c2", name="c2", align_bytes=64)
             s2x = c2p.tile([P, 2, C], U8, tag="s2x", name="s2x", align_bytes=64)
             for gp in range(2):
-                rb = rbp.tile([P, 8, 512], BF16, tag="rb", name="rb")
-                nc.sync.dma_start(
-                    out=rb[:],
-                    in_=x[n, :, 16 * gp : 16 * gp + 16, :].rearrange("(r p) h w -> p r (h w)", p=P),
-                )
-                rb_w = rb[:].bitcast(F32)
                 g2 = g2p.tile([P, 4 * C], BF16, tag="g2", name="g2", align_bytes=64)
                 g2w = g2[:].bitcast(F32).rearrange("q (c u) -> q c u", u=2)
                 for rp in range(4):
                     xt = ps_xt.tile([P, 2, 2, P], F32, tag="xt", name="xt")
                     for rl in range(2):
                         for u in range(2):
+                            wb = 2 * gp + u
                             nc.tensor.transpose(
                                 xt[:, rl, u, :],
-                                rb_w[:, 2 * rp + rl, P * u : P * u + P],
+                                raw_w[:, 2 * rp + rl, P * wb : P * wb + P],
                                 ident_f[:],
                             )
                     nc.scalar.copy(
@@ -321,7 +286,7 @@ def tile_sralnet_pa_t_kernel(tc, x, centroids, out):
                 nc.vector.quantize_mx(
                     out=c2[:, gp, :].bitcast(FP8X4), scales=s2x[:, gp, :], in_=g2[:]
                 )
-            mc, msc = state["mc"]
+            mc, msc = mults[n]
             if i == 0:
                 state["v"] = [
                     ps_v.tile([P, 512], F32, tag="v%d" % hc, name="v_ps%d" % hc) for hc in range(2)
@@ -398,13 +363,11 @@ def tile_sralnet_pa_t_kernel(tc, x, centroids, out):
 
         for n in range(AHEAD):
             stage_a(n)
-        for n in range(-NB, N_IMG):
-            if n + NB < N_IMG:
-                stage_b1(n + NB)
-                if n + NB + AHEAD < N_IMG:
-                    stage_a(n + NB + AHEAD)
-            if n >= 0:
-                stage_b2(n)
+        for n in range(N_IMG):
+            stage_b(n)
+            if n + AHEAD < N_IMG:
+                stage_a(n + AHEAD)
+            if n < N_IMG - 3:
                 stage_c(n)
-            if (n + 1) % NB == 0 and n + NB < N_IMG:
-                stage_ln()
+        for n in range(N_IMG - 3, N_IMG):
+            stage_c(n)

@@ -19,24 +19,29 @@ PIX = 1024
 K = 32
 S4 = 4
 EPS = 1e-12
-WV = 224
+WV = 424
 AHEAD = 2
+LNG = 2
+LAG = 2
+GRP = 4
 
 FLOPS = 2 * N_IMG * C * PIX * (K * S4) + 2 * N_IMG * K * PIX * C
 
 
 def tile_sralnet_pa_t_kernel(tc, x, centroids, out):
     nc = tc.nc
-    tail = nc.vector
     with ExitStack() as ctx:
         const = ctx.enter_context(tc.tile_pool(name="const", bufs=1))
-        rawp = ctx.enter_context(tc.tile_pool(name="rawp", bufs=3))
+        rawp = ctx.enter_context(tc.tile_pool(name="rawp", bufs=6))
         g1p = ctx.enter_context(tc.tile_pool(name="g1p", bufs=2))
-        c1p = ctx.enter_context(tc.tile_pool(name="c1p", bufs=2))
+        c1p = ctx.enter_context(tc.tile_pool(name="c1p", bufs=3))
         g2p = ctx.enter_context(tc.tile_pool(name="g2p", bufs=2))
-        c2p = ctx.enter_context(tc.tile_pool(name="c2p", bufs=2))
-        zbp = ctx.enter_context(tc.tile_pool(name="zbp", bufs=3))
-        smp = ctx.enter_context(tc.tile_pool(name="smp", bufs=3))
+        c2p = ctx.enter_context(tc.tile_pool(name="c2p", bufs=4))
+        zbp = ctx.enter_context(tc.tile_pool(name="zbp", bufs=2))
+        smp = ctx.enter_context(tc.tile_pool(name="smp", bufs=2))
+        dp = ctx.enter_context(tc.tile_pool(name="dp", bufs=4))
+        sump = ctx.enter_context(tc.tile_pool(name="sump", bufs=3))
+        mfp = ctx.enter_context(tc.tile_pool(name="mfp", bufs=5))
         epi = ctx.enter_context(tc.tile_pool(name="epi", bufs=2))
         ps_zt = ctx.enter_context(tc.psum_pool(name="ps_zt", bufs=1))
         ps_z = ctx.enter_context(tc.psum_pool(name="ps_z", bufs=2))
@@ -63,6 +68,12 @@ def tile_sralnet_pa_t_kernel(tc, x, centroids, out):
         nc.vector.memset(half[:], 0.5)
         ones2 = const.tile([P, 2], F32, name="ones2")
         nc.vector.memset(ones2[:], 1.0)
+        sel = const.tile([P, K], F32, name="sel")
+        nc.vector.tensor_reduce(
+            out=sel[:], in_=ident_f[:].rearrange("p (b k) -> p k b", k=K), axis=AX.X, op=ALU.add
+        )
+        mhalf = const.tile([P, 1], F32, name="mhalf")
+        nc.vector.memset(mhalf[:], -0.5)
         bd = const.tile([P, P], F32, name="bd")
         nc.vector.memset(bd[:], 0.0)
         for i in range(4):
@@ -94,65 +105,73 @@ def tile_sralnet_pa_t_kernel(tc, x, centroids, out):
         bvec = const.tile([P, 1], F32, name="bvec")
         nc.vector.tensor_scalar_mul(out=bvec[:], in0=cn[:], scalar1=-100.0)
 
-        raws = {}
         zbts = {}
+        raws = {}
+        logits = {}
+        sums = {}
+        maxes = {}
         mults = {}
+        multfs = {}
+        codes2 = {}
         state = {}
 
         def stage_a(n):
-            raw = rawp.tile([P, 8, PIX], BF16, tag="raw", name="raw")
-            raws[n] = raw
-            for g in range(2):
-                nc.sync.dma_start(
-                    out=raw[:, 4 * g : 4 * g + 4, :],
-                    in_=x[n, 512 * g : 512 * g + 512].rearrange("(j p) h w -> p j (h w)", p=P),
-                )
-            c1 = c1p.tile([P, 2, PIX], U32, tag="c1", name="c1", align_bytes=64)
-            s1x = c1p.tile([P, 2, PIX], U8, tag="s1x", name="s1x", align_bytes=64)
-            for g in range(2):
-                g1 = g1p.tile([P, PIX, 4], BF16, tag="g1", name="g1", align_bytes=64)
-                wv = 672 if n < 2 else WV
-                nc.vector.tensor_copy(
-                    out=g1[:, 0:wv, :].rearrange("p (c i) t -> p c t i", i=4),
-                    in_=raw[:, 4 * g : 4 * g + 4, 0:wv].rearrange("p t (c i) -> p c t i", i=4),
-                )
-                step = (PIX - wv) // 4
-                for w0 in range(wv, PIX, step):
-                    nc.scalar.copy(
-                        out=g1[:, w0 : w0 + step, :].rearrange("p (c i) t -> p c t i", i=4),
-                        in_=raw[:, 4 * g : 4 * g + 4, w0 : w0 + step].rearrange(
-                            "p t (c i) -> p c t i", i=4
-                        ),
-                    )
-                nc.vector.quantize_mx(
-                    out=c1[:, g, :].bitcast(FP8X4),
-                    scales=s1x[:, g, :],
-                    in_=g1[:].rearrange("p w j -> p (w j)"),
-                )
             zbt = zbp.tile([P, PIX], F32, tag="zbt", name="zbt")
             zbts[n] = zbt
-            for h in range(2):
+            for gp in range(2):
+                raw = rawp.tile([P, 8, 512], BF16, tag="raw", name="raw")
+                raws[n, gp] = raw
+                nc.sync.dma_start(
+                    out=raw[:],
+                    in_=x[n, :, 16 * gp : 16 * gp + 16, :].rearrange("(r p) h w -> p r (h w)", p=P),
+                )
+                c1 = c1p.tile([P, 2, 512], U32, tag="c1", name="c1", align_bytes=64)
+                s1x = c1p.tile([P, 2, 512], U8, tag="s1x", name="s1x", align_bytes=64)
+                g1 = g1p.tile([P, 2, 512, 4], BF16, tag="g1", name="g1", align_bytes=64)
+                for g in range(2):
+                    for copy, w0, w1 in (
+                        (nc.vector.tensor_copy, 0, WV),
+                        (nc.scalar.copy, WV, 512),
+                    ):
+                        copy(
+                            out=g1[:, g, w0:w1, :].rearrange("p (c i) t -> p c t i", i=4),
+                            in_=raw[:, 4 * g : 4 * g + 4, w0:w1].rearrange(
+                                "p t (c i) -> p c t i", i=4
+                            ),
+                        )
+                nc.vector.quantize_mx(
+                    out=c1[:].rearrange("p g w -> p (g w)").bitcast(FP8X4),
+                    scales=s1x[:].rearrange("p g w -> p (g w)"),
+                    in_=g1[:].rearrange("p g w j -> p (g w j)"),
+                )
                 zt = ps_zt.tile([P, 512], F32, tag="zT", name="zt")
                 for g in range(2):
                     nc.tensor.matmul_mx(
                         out=zt[:],
                         lhsT=w_codes[:, P * g : P * g + P].bitcast(FP8X4),
                         lhsT_scale=w_scales[:, P * g : P * g + P],
-                        rhs=c1[:, g, 512 * h : 512 * h + 512].bitcast(FP8X4),
-                        rhs_scale=s1x[:, g, 512 * h : 512 * h + 512],
+                        rhs=c1[:, g, :].bitcast(FP8X4),
+                        rhs_scale=s1x[:, g, :],
                         start=(g == 0),
                         stop=(g == 1),
                     )
                 nc.scalar.activation(
-                    out=zbt[:, 512 * h : 512 * h + 512],
+                    out=zbt[:, 512 * gp : 512 * gp + 512],
                     in_=zt[:],
                     func=ACT.Identity,
                     bias=bvec[:, 0:1],
                     scale=1.0,
                 )
 
+        def over_k_and_s(tile, i):
+            return (
+                tile[:, i, 0 : 8 * S4].rearrange("q (t s) -> q t s", s=S4),
+                tile[:, i, 8 * S4 :].rearrange("q (t k) -> q t k", k=K),
+            )
+
         def stage_b(n):
-            i = n % 4
+            i = n % LNG
+            grp = n // LNG
             zbt = zbts[n]
             z_ps = []
             for gp in range(2):
@@ -166,26 +185,30 @@ def tile_sralnet_pa_t_kernel(tc, x, centroids, out):
                             ident_f[:],
                         )
                 z_ps.append(zp)
-            msk = smp.tile([P, 8, K], F32, tag="msk", name="msk")
-            negmk = smp.tile([P, 8, S4], F32, tag="negmk", name="negmk")
-            e2 = smp.tile([P, 8, S4, K], F32, tag="e2", name="e2")
-            e1 = smp.tile([P, 8, S4, K], F32, tag="e1", name="e1")
-            s1 = smp.tile([P, 8, S4], F32, tag="s1", name="s1")
+            d = dp.tile([P, S4, 8, K], F32, tag="d", name="d")
+            logits[n] = d
+            e1 = smp.tile([P, 8, S4, K], BF16, tag="e1", name="e1")
+            e2 = smp.tile([P, S4, 8, K], F32, tag="e2", name="e2")
+            if i == 0:
+                sums[grp] = sump.tile([P, LNG, 8 * S4 + 8 * K], F32, tag="sums", name="sums")
+                maxes[grp] = sump.tile([P, LNG, 8 * S4 + 8 * K], F32, tag="maxes", name="maxes")
+            sum_k, sum_s = over_k_and_s(sums[grp], i)
+            max_k, max_s = over_k_and_s(maxes[grp], i)
             for gp in range(2):
                 ts = slice(4 * gp, 4 * gp + 4)
                 nc.vector.tensor_reduce(
-                    out=negmk[:, ts, :], in_=z_ps[gp][:], axis=AX.X, op=ALU.max, negate=True
+                    out=max_k[:, ts, :], in_=z_ps[gp][:], axis=AX.X, op=ALU.max, negate=True
                 )
                 nc.vector.tensor_reduce(
-                    out=msk[:, ts, :],
+                    out=max_s[:, ts, :],
                     in_=z_ps[gp][:].rearrange("q t s k -> q t k s"),
                     axis=AX.X,
                     op=ALU.max,
                 )
                 nc.vector.tensor_tensor(
-                    out=e2[:, ts],
+                    out=d[:, :, ts, :].rearrange("q s t k -> q t s k"),
                     in0=z_ps[gp][:],
-                    in1=msk[:, ts, :].unsqueeze(2).to_broadcast([P, 4, S4, K]),
+                    in1=max_s[:, ts, :].unsqueeze(2).to_broadcast([P, 4, S4, K]),
                     op=ALU.subtract,
                 )
             for t in range(8):
@@ -194,60 +217,68 @@ def tile_sralnet_pa_t_kernel(tc, x, centroids, out):
                         out=e1[:, t, s, :],
                         in_=z_ps[t // 4][:, t % 4, s, :],
                         func=ACT.Exp,
-                        bias=negmk[:, t, s : s + 1],
+                        bias=max_k[:, t, s : s + 1],
                         scale=1.0,
-                        accum_out=s1[:, t, s : s + 1],
+                        accum_out=sum_k[:, t, s : s + 1],
                     )
-            nc.scalar.activation(out=e2[:], in_=e2[:], func=ACT.Exp)
-            s2 = smp.tile([P, 8, K], F32, tag="s2", name="s2")
-            nc.vector.tensor_reduce(
-                out=s2[:], in_=e2[:].rearrange("q t s k -> q t k s"), axis=AX.X, op=ALU.add
-            )
-            r1 = smp.tile([P, 8, S4], F32, tag="r1", name="r1")
-            nc.vector.reciprocal(out=r1[:], in_=s1[:])
-            r2 = smp.tile([P, 8, K], F32, tag="r2", name="r2")
-            nc.vector.reciprocal(out=r2[:], in_=s2[:])
-            tail.tensor_tensor(out=e1[:], in0=e1[:], in1=e2[:], op=ALU.mult)
-            tail.tensor_tensor(
-                out=e1[:].rearrange("q t s k -> q (t s) k"),
-                in0=e1[:].rearrange("q t s k -> q (t s) k"),
-                in1=r1[:].rearrange("q t s -> q (t s)").unsqueeze(2).to_broadcast([P, 32, K]),
-                op=ALU.mult,
-            )
-            tail.tensor_tensor(
-                out=e1[:],
-                in0=e1[:],
-                in1=r2[:].unsqueeze(2).to_broadcast([P, 8, S4, K]),
-                op=ALU.mult,
-            )
-            t1 = smp.tile([P, 8, 2 * K], F32, tag="t1", name="t1")
-            nc.vector.tensor_scalar_add(
-                out=t1[:], in0=e1[:, :, 2:4, :].rearrange("q t s k -> q t (s k)"), scalar1=1.0
-            )
-            uu = smp.tile([P, 8, 2 * K], F32, tag="uu", name="uu")
-            nc.vector.scalar_tensor_tensor(
-                out=uu[:],
-                in0=e1[:, :, 0:2, :].rearrange("q t s k -> q t (s k)"),
-                scalar=1.0,
-                in1=t1[:],
-                op0=ALU.add,
-                op1=ALU.mult,
-            )
-            multf = smp.tile([P, 8, K], F32, tag="multf", name="multf")
+            nc.scalar.activation(out=e2[:], in_=d[:], func=ACT.Exp)
+            half_sum = smp.tile([P, 2, 8, K], F32, tag="half_sum", name="half_sum")
             nc.vector.tensor_tensor(
-                out=multf[:], in0=uu[:, :, 0:K], in1=uu[:, :, K : 2 * K], op=ALU.mult
+                out=half_sum[:], in0=e2[:, 0:2], in1=e2[:, 2:4], op=ALU.add
             )
+            nc.vector.tensor_tensor(
+                out=sum_s, in0=half_sum[:, 0], in1=half_sum[:, 1], op=ALU.add
+            )
+
+        def log_sums(grp):
+            flat = sums[grp][:].rearrange("q i c -> q (i c)")
+            nc.scalar.activation(out=flat, in_=flat, func=ACT.Ln)
+            nc.vector.tensor_tensor(
+                out=flat,
+                in0=maxes[grp][:].rearrange("q i c -> q (i c)"),
+                in1=flat,
+                op=ALU.subtract,
+            )
+
+        def stage_d(n):
+            i = n % LNG
+            a = logits[n]
+            lse_k, lse_s = over_k_and_s(sums[n // LNG], i)
+            a_flat = a[:].rearrange("q s t k -> q s (t k)")
+            nc.vector.scalar_tensor_tensor(
+                out=a_flat,
+                in0=a_flat,
+                scalar=2.0,
+                in1=lse_s.rearrange("q t k -> q (t k)")
+                .unsqueeze(1)
+                .to_broadcast([P, S4, 8 * K]),
+                op0=ALU.mult,
+                op1=ALU.add,
+            )
+            for t in range(8):
+                for s in range(S4):
+                    nc.scalar.activation(
+                        out=a[:, s, t, :],
+                        in_=a[:, s, t, :],
+                        func=ACT.Exp,
+                        bias=lse_k[:, t, s : s + 1],
+                        scale=1.0,
+                    )
+            lo = a[:, 0:2].rearrange("q s t k -> q (s t k)")
+            hi = a[:, 2:4].rearrange("q s t k -> q (s t k)")
+            nc.vector.tensor_scalar_add(out=hi, in0=hi, scalar1=1.0)
+            nc.vector.scalar_tensor_tensor(
+                out=lo, in0=lo, scalar=1.0, in1=hi, op0=ALU.add, op1=ALU.mult
+            )
+            multf = mfp.tile([P, 8, K], F32, tag="multf", name="multf")
+            multfs[n] = multf
+            nc.vector.tensor_tensor(
+                out=multf[:], in0=a[:, 0], in1=a[:, 1], op=ALU.mult
+            )
+            i = n % GRP
             nc.vector.tensor_copy(
                 out=mb[i][:, :, K * i : K * i + K, :],
                 in_=multf[:].rearrange("q (g t) k -> q g k t", g=2),
-            )
-            if i == 0:
-                state["msp"] = smp.tile([P, P], F32, tag="msp", name="msp")
-            nc.vector.tensor_reduce(
-                out=state["msp"][:, K * i : K * i + K],
-                in_=multf[:].rearrange("q t k -> q k t"),
-                axis=AX.X,
-                op=ALU.add,
             )
             mc = smp.tile([P, 2 * P], U32, tag="mc", name="mc", align_bytes=64)
             msc = smp.tile([P, 2 * P], U8, tag="msc", name="msc", align_bytes=64)
@@ -258,23 +289,21 @@ def tile_sralnet_pa_t_kernel(tc, x, centroids, out):
             )
             mults[n] = (mc, msc)
 
-        def stage_c(n):
-            i = n % 4
-            grp = n // 4
-            raw_w = raws[n][:].bitcast(F32)
+        def stage_p(n):
             c2 = c2p.tile([P, 2, C], U32, tag="c2", name="c2", align_bytes=64)
             s2x = c2p.tile([P, 2, C], U8, tag="s2x", name="s2x", align_bytes=64)
+            codes2[n] = (c2, s2x)
             for gp in range(2):
+                raw_w = raws[n, gp][:].bitcast(F32)
                 g2 = g2p.tile([P, 4 * C], BF16, tag="g2", name="g2", align_bytes=64)
                 g2w = g2[:].bitcast(F32).rearrange("q (c u) -> q c u", u=2)
                 for rp in range(4):
                     xt = ps_xt.tile([P, 2, 2, P], F32, tag="xt", name="xt")
                     for rl in range(2):
                         for u in range(2):
-                            wb = 2 * gp + u
                             nc.tensor.transpose(
                                 xt[:, rl, u, :],
-                                raw_w[:, 2 * rp + rl, P * wb : P * wb + P],
+                                raw_w[:, 2 * rp + rl, P * u : P * u + P],
                                 ident_f[:],
                             )
                     nc.scalar.copy(
@@ -286,7 +315,12 @@ def tile_sralnet_pa_t_kernel(tc, x, centroids, out):
                 nc.vector.quantize_mx(
                     out=c2[:, gp, :].bitcast(FP8X4), scales=s2x[:, gp, :], in_=g2[:]
                 )
+
+        def stage_v(n):
+            i = n % GRP
+            grp = n // GRP
             mc, msc = mults[n]
+            c2, s2x = codes2[n]
             if i == 0:
                 state["v"] = [
                     ps_v.tile([P, 512], F32, tag="v%d" % hc, name="v_ps%d" % hc) for hc in range(2)
@@ -305,9 +339,30 @@ def tile_sralnet_pa_t_kernel(tc, x, centroids, out):
                     )
             if i != 3:
                 return
-            pss = ps_zt.tile([P, 512], F32, tag="zT", name="pss")
+            part = ps_xt.tile([P, GRP, 2], F32, tag="xt", name="part")
+            for j in range(GRP):
+                for g in range(2):
+                    nc.tensor.matmul(
+                        out=part[:, j, :],
+                        lhsT=multfs[n - 3 + j][:, 4 * g : 4 * g + 4, :].rearrange("q t k -> q (t k)"),
+                        rhs=ones2[:],
+                        start=(g == 0),
+                        stop=(g == 1),
+                    )
+            spread = epi.tile([P, GRP, K], F32, tag="spread", name="spread")
+            nc.vector.tensor_tensor(
+                out=spread[:],
+                in0=part[:, :, 0:1].to_broadcast([P, GRP, K]),
+                in1=sel[:].unsqueeze(1).to_broadcast([P, GRP, K]),
+                op=ALU.mult,
+            )
+            pss = ps_xt.tile([P, 2], F32, tag="xt", name="pss")
             nc.tensor.matmul(
-                out=pss[:, 0:2], lhsT=state["msp"][:], rhs=ones2[:], start=True, stop=True
+                out=pss[:],
+                lhsT=spread[:].rearrange("p i k -> p (i k)"),
+                rhs=ones2[:],
+                start=True,
+                stop=True,
             )
             negms = epi.tile([P, 1], F32, tag="negms", name="negms")
             nc.vector.tensor_scalar_mul(out=negms[:], in0=pss[:, 0:1], scalar1=-1.0)
@@ -324,12 +379,10 @@ def tile_sralnet_pa_t_kernel(tc, x, centroids, out):
             sq = epi.tile([P, C], BF16, tag="sq", name="sq")
             ss = epi.tile([P, 1], F32, tag="ss", name="ss")
             nc.scalar.activation(out=sq[:], in_=v2[:], func=ACT.Square, accum_out=ss[:])
-            n1 = epi.tile([P, 1], F32, tag="n1", name="n1")
-            nc.gpsimd.tensor_tensor(out=n1[:], in0=ss[:], in1=half[:], op=ALU.pow)
-            n1c = epi.tile([P, 1], F32, tag="n1c", name="n1c")
-            nc.vector.tensor_scalar_max(out=n1c[:], in0=n1[:], scalar1=EPS)
+            ssc = epi.tile([P, 1], F32, tag="ssc", name="ssc")
+            nc.vector.tensor_scalar_max(out=ssc[:], in0=ss[:], scalar1=EPS * EPS)
             rn1 = epi.tile([P, 1], F32, tag="rn1", name="rn1")
-            nc.vector.reciprocal(out=rn1[:], in_=n1c[:])
+            nc.gpsimd.tensor_tensor(out=rn1[:], in0=ssc[:], in1=mhalf[:], op=ALU.pow)
             q2 = epi.tile([P, 2], F32, tag="q2", name="q2")
             nc.vector.tensor_scalar(
                 out=q2[:],
@@ -339,23 +392,20 @@ def tile_sralnet_pa_t_kernel(tc, x, centroids, out):
                 op0=ALU.mult,
                 op1=ALU.mult,
             )
-            nc.tensor.matmul(out=pss[:, 2:4], lhsT=bd[:], rhs=q2[:], start=True, stop=True)
-            tot = epi.tile([P, 1], F32, tag="tot", name="tot")
-            nc.vector.tensor_copy(out=tot[:], in_=pss[:, 2:3])
-            n2 = epi.tile([P, 1], F32, tag="n2", name="n2")
-            nc.gpsimd.tensor_tensor(out=n2[:], in0=tot[:], in1=half[:], op=ALU.pow)
-            den = epi.tile([P, 1], F32, tag="den", name="den")
+            pst = ps_xt.tile([P, 2], F32, tag="xt", name="pst")
+            nc.tensor.matmul(out=pst[:], lhsT=bd[:], rhs=q2[:], start=True, stop=True)
+            totc = epi.tile([P, 1], F32, tag="totc", name="totc")
+            nc.vector.tensor_scalar_max(out=totc[:], in0=pst[:, 0:1], scalar1=EPS * EPS)
+            rn2 = epi.tile([P, 1], F32, tag="rn2", name="rn2")
+            nc.gpsimd.tensor_tensor(out=rn2[:], in0=totc[:], in1=mhalf[:], op=ALU.pow)
             nc.vector.tensor_scalar(
-                out=den[:],
-                in0=n2[:],
-                scalar1=EPS,
-                scalar2=n1c[:, 0:1],
-                op0=ALU.max,
+                out=v2[:],
+                in0=v2[:],
+                scalar1=rn1[:, 0:1],
+                scalar2=rn2[:, 0:1],
+                op0=ALU.mult,
                 op1=ALU.mult,
             )
-            fsc = epi.tile([P, 1], F32, tag="fsc", name="fsc")
-            nc.vector.reciprocal(out=fsc[:], in_=den[:])
-            nc.vector.tensor_scalar_mul(out=v2[:], in0=v2[:], scalar1=fsc[:, 0:1])
             nc.sync.dma_start(
                 out=out[4 * grp : 4 * grp + 4, :].rearrange("i (k c) -> (i k) c", c=C),
                 in_=v2[:],
@@ -363,11 +413,17 @@ def tile_sralnet_pa_t_kernel(tc, x, centroids, out):
 
         for n in range(AHEAD):
             stage_a(n)
-        for n in range(N_IMG):
-            stage_b(n)
+        stage_p(0)
+        for n in range(N_IMG + LAG):
+            if n < N_IMG:
+                stage_b(n)
+            if n >= LAG:
+                stage_d(n - LAG)
             if n + AHEAD < N_IMG:
                 stage_a(n + AHEAD)
-            if n < N_IMG - 3:
-                stage_c(n)
-        for n in range(N_IMG - 3, N_IMG):
-            stage_c(n)
+            if n + 1 < N_IMG:
+                stage_p(n + 1)
+            if n < N_IMG and n % LNG == LNG - 1:
+                log_sums(n // LNG)
+            if n >= LAG:
+                stage_v(n - LAG)

@@ -19,11 +19,11 @@ PIX = 1024
 K = 32
 S4 = 4
 EPS = 1e-12
-WV = 424
-AHEAD = 2
+WV0 = 344
+WV = 408
 LNG = 2
-LAG = 2
 GRP = 4
+LAST = N_IMG // GRP - 1
 
 FLOPS = 2 * N_IMG * C * PIX * (K * S4) + 2 * N_IMG * K * PIX * C
 
@@ -31,16 +31,17 @@ FLOPS = 2 * N_IMG * C * PIX * (K * S4) + 2 * N_IMG * K * PIX * C
 def tile_sralnet_pa_t_kernel(tc, x, centroids, out):
     nc = tc.nc
     with ExitStack() as ctx:
+        ctx.enter_context(tc.manual_schedule())
         const = ctx.enter_context(tc.tile_pool(name="const", bufs=1))
         rawp = ctx.enter_context(tc.tile_pool(name="rawp", bufs=6))
         g1p = ctx.enter_context(tc.tile_pool(name="g1p", bufs=2))
         c1p = ctx.enter_context(tc.tile_pool(name="c1p", bufs=3))
         g2p = ctx.enter_context(tc.tile_pool(name="g2p", bufs=2))
-        c2p = ctx.enter_context(tc.tile_pool(name="c2p", bufs=4))
+        c2p = ctx.enter_context(tc.tile_pool(name="c2p", bufs=5))
         zbp = ctx.enter_context(tc.tile_pool(name="zbp", bufs=2))
         smp = ctx.enter_context(tc.tile_pool(name="smp", bufs=2))
         dp = ctx.enter_context(tc.tile_pool(name="dp", bufs=4))
-        sump = ctx.enter_context(tc.tile_pool(name="sump", bufs=3))
+        sump = ctx.enter_context(tc.tile_pool(name="sump", bufs=2))
         mfp = ctx.enter_context(tc.tile_pool(name="mfp", bufs=5))
         epi = ctx.enter_context(tc.tile_pool(name="epi", bufs=2))
         ps_zt = ctx.enter_context(tc.psum_pool(name="ps_zt", bufs=1))
@@ -48,30 +49,51 @@ def tile_sralnet_pa_t_kernel(tc, x, centroids, out):
         ps_xt = ctx.enter_context(tc.psum_pool(name="ps_xt", bufs=3))
         ps_v = ctx.enter_context(tc.psum_pool(name="ps_v", bufs=1))
 
+        st = {}
+
+        def load(n, gp):
+            raw = rawp.tile([P, 8, 512], BF16, tag="raw", name="raw")
+            st["raw", n, gp] = raw
+            nc.sync.dma_start(
+                out=raw[:],
+                in_=x[n, :, 16 * gp : 16 * gp + 16, :].rearrange("(r p) h w -> p r (h w)", p=P),
+            )
+
+        def load_first():
+            raw = rawp.tile([P, 8, 512], BF16, tag="raw", name="raw")
+            st["raw", 0, 0] = raw
+            for g in range(2):
+                nc.sync.dma_start(
+                    out=raw[:, 4 * g : 4 * g + 4, :],
+                    in_=x[0, 512 * g : 512 * g + 512, 0:16, :].rearrange(
+                        "(r p) h w -> p r (h w)", p=P
+                    ),
+                )
+
+        load_first()
         c_sb = const.tile([P, C], BF16, name="c_sb")
         for s in range(S4):
             nc.sync.dma_start(out=c_sb[32 * s : 32 * s + 32, :], in_=centroids[:, s, :])
+        load(0, 1)
+        load(1, 0)
+        load(1, 1)
         rep4 = const.tile([P, C], BF16, name="rep4")
         for i in range(4):
-            nc.scalar.dma_start(out=rep4[32 * i : 32 * i + 32, :], in_=centroids[:, 0, :])
+            nc.sync.dma_start(out=rep4[32 * i : 32 * i + 32, :], in_=centroids[:, 0, :])
 
         warm = const.tile([P, 1], F32, name="warm")
         nc.vector.memset(warm[:], 0.0)
         warm2 = const.tile([P, 1], F32, name="warm2")
         nc.scalar.activation(out=warm2[:], in_=warm[:], func=ACT.Exp)
 
-        ident_f = const.tile([P, P], F32, name="ident_f")
-        make_identity(nc, ident_f[:])
         ident_b = const.tile([P, P], BF16, name="ident_b")
         make_identity(nc, ident_b[:])
+        ident_f = const.tile([P, P], F32, name="ident_f")
+        make_identity(nc, ident_f[:])
         half = const.tile([P, 1], F32, name="half")
         nc.vector.memset(half[:], 0.5)
         ones2 = const.tile([P, 2], F32, name="ones2")
         nc.vector.memset(ones2[:], 1.0)
-        sel = const.tile([P, K], F32, name="sel")
-        nc.vector.tensor_reduce(
-            out=sel[:], in_=ident_f[:].rearrange("p (b k) -> p k b", k=K), axis=AX.X, op=ALU.add
-        )
         mhalf = const.tile([P, 1], F32, name="mhalf")
         nc.vector.memset(mhalf[:], -0.5)
         bd = const.tile([P, P], F32, name="bd")
@@ -81,87 +103,110 @@ def tile_sralnet_pa_t_kernel(tc, x, centroids, out):
         mb = [const.tile([P, 2, P, 4], BF16, name="mb%d" % i, align_bytes=64) for i in range(4)]
         for i in range(4):
             nc.vector.memset(mb[i][:], 0.0)
-
-        pt = ps_xt.tile([P, 8, P], BF16, tag="xt", name="pt")
-        for r in range(8):
-            nc.tensor.transpose(pt[:, r, :], c_sb[:, P * r : P * r + P], ident_b[:])
-        wg = const.tile([P, 2, P, 4], BF16, name="wg", align_bytes=64)
-        nc.vector.tensor_scalar_mul(
-            out=wg[:], in0=pt[:].rearrange("p (g j) m -> p g m j", j=4), scalar1=200.0
+        sel = const.tile([P, K], F32, name="sel")
+        nc.vector.tensor_reduce(
+            out=sel[:], in_=ident_f[:].rearrange("p (b k) -> p k b", k=K), axis=AX.X, op=ALU.add
         )
+
         w_codes = const.tile([P, 2 * P], U32, name="w_codes", align_bytes=64)
         w_scales = const.tile([P, 2 * P], U8, name="w_scales", align_bytes=64)
-        nc.vector.quantize_mx(
-            out=w_codes[:].bitcast(FP8X4),
-            scales=w_scales[:],
-            in_=wg[:].rearrange("p g m j -> p (g m j)"),
-        )
-
-        junk0 = epi.tile([P, C], BF16, tag="sq", name="junk0")
-        css = const.tile([P, 1], F32, name="css")
-        nc.scalar.activation(out=junk0[:], in_=c_sb[:], func=ACT.Square, accum_out=css[:])
-        cn = const.tile([P, 1], F32, name="cn")
-        nc.gpsimd.tensor_tensor(out=cn[:], in0=css[:], in1=half[:], op=ALU.pow)
         bvec = const.tile([P, 1], F32, name="bvec")
-        nc.vector.tensor_scalar_mul(out=bvec[:], in0=cn[:], scalar1=-100.0)
 
-        zbts = {}
-        raws = {}
-        logits = {}
-        sums = {}
-        maxes = {}
-        mults = {}
-        multfs = {}
-        codes2 = {}
-        state = {}
+        def prep_w():
+            pt = ps_xt.tile([P, 8, P], BF16, tag="xt", name="pt")
+            for r in range(8):
+                nc.tensor.transpose(pt[:, r, :], c_sb[:, P * r : P * r + P], ident_b[:])
+            wg = const.tile([P, 2, P, 4], BF16, name="wg", align_bytes=64)
+            nc.vector.tensor_scalar_mul(
+                out=wg[:], in0=pt[:].rearrange("p (g j) m -> p g m j", j=4), scalar1=200.0
+            )
+            st["wg"] = wg
 
-        def stage_a(n):
-            zbt = zbp.tile([P, PIX], F32, tag="zbt", name="zbt")
-            zbts[n] = zbt
-            for gp in range(2):
-                raw = rawp.tile([P, 8, 512], BF16, tag="raw", name="raw")
-                raws[n, gp] = raw
-                nc.sync.dma_start(
-                    out=raw[:],
-                    in_=x[n, :, 16 * gp : 16 * gp + 16, :].rearrange("(r p) h w -> p r (h w)", p=P),
+        def prep_wq():
+            nc.vector.quantize_mx(
+                out=w_codes[:].bitcast(FP8X4),
+                scales=w_scales[:],
+                in_=st["wg"][:].rearrange("p g m j -> p (g m j)"),
+            )
+
+        def prep_norm():
+            junk0 = epi.tile([P, C], BF16, tag="sq", name="junk0")
+            css = const.tile([P, 1], F32, name="css")
+            nc.scalar.activation(out=junk0[:], in_=c_sb[:], func=ACT.Square, accum_out=css[:])
+            cn = const.tile([P, 1], F32, name="cn")
+            nc.gpsimd.tensor_tensor(out=cn[:], in0=css[:], in1=half[:], op=ALU.pow)
+            st["cn"] = cn
+
+        def prep_b():
+            nc.vector.tensor_scalar_mul(out=bvec[:], in0=st["cn"][:], scalar1=-100.0)
+
+        def g1_tile(n, gp):
+            st["g1", n, gp] = g1p.tile([P, 2, 512, 4], BF16, tag="g1", name="g1", align_bytes=64)
+
+        def regroup(copy, n, gp, g, w0, w1):
+            copy(
+                out=st["g1", n, gp][:, g, w0:w1, :].rearrange("p (c i) t -> p c t i", i=4),
+                in_=st["raw", n, gp][:, 4 * g : 4 * g + 4, w0:w1].rearrange(
+                    "p t (c i) -> p c t i", i=4
+                ),
+            )
+
+        def wv(n):
+            return WV0 if n < 2 else WV
+
+        def il_v(n, gp, g):
+            regroup(nc.vector.tensor_copy, n, gp, g, 0, wv(n))
+
+        def il_s(n, gp, g):
+            regroup(nc.scalar.copy, n, gp, g, wv(n), 512)
+
+        def q1(n, gp):
+            c1 = c1p.tile([P, 2, 512], U32, tag="c1", name="c1", align_bytes=64)
+            s1x = c1p.tile([P, 2, 512], U8, tag="s1x", name="s1x", align_bytes=64)
+            st["c1", n, gp] = (c1, s1x)
+            nc.vector.quantize_mx(
+                out=c1[:].rearrange("p g w -> p (g w)").bitcast(FP8X4),
+                scales=s1x[:].rearrange("p g w -> p (g w)"),
+                in_=st["g1", n, gp][:].rearrange("p g w j -> p (g w j)"),
+            )
+
+        def zmm(n, gp):
+            zt = ps_zt.tile([P, 512], F32, tag="zT", name="zt")
+            st["zt", n, gp] = zt
+            c1, s1x = st["c1", n, gp]
+            for g in range(2):
+                nc.tensor.matmul_mx(
+                    out=zt[:],
+                    lhsT=w_codes[:, P * g : P * g + P].bitcast(FP8X4),
+                    lhsT_scale=w_scales[:, P * g : P * g + P],
+                    rhs=c1[:, g, :].bitcast(FP8X4),
+                    rhs_scale=s1x[:, g, :],
+                    start=(g == 0),
+                    stop=(g == 1),
                 )
-                c1 = c1p.tile([P, 2, 512], U32, tag="c1", name="c1", align_bytes=64)
-                s1x = c1p.tile([P, 2, 512], U8, tag="s1x", name="s1x", align_bytes=64)
-                g1 = g1p.tile([P, 2, 512, 4], BF16, tag="g1", name="g1", align_bytes=64)
-                for g in range(2):
-                    for copy, w0, w1 in (
-                        (nc.vector.tensor_copy, 0, WV),
-                        (nc.scalar.copy, WV, 512),
-                    ):
-                        copy(
-                            out=g1[:, g, w0:w1, :].rearrange("p (c i) t -> p c t i", i=4),
-                            in_=raw[:, 4 * g : 4 * g + 4, w0:w1].rearrange(
-                                "p t (c i) -> p c t i", i=4
-                            ),
-                        )
-                nc.vector.quantize_mx(
-                    out=c1[:].rearrange("p g w -> p (g w)").bitcast(FP8X4),
-                    scales=s1x[:].rearrange("p g w -> p (g w)"),
-                    in_=g1[:].rearrange("p g w j -> p (g w j)"),
-                )
-                zt = ps_zt.tile([P, 512], F32, tag="zT", name="zt")
-                for g in range(2):
-                    nc.tensor.matmul_mx(
-                        out=zt[:],
-                        lhsT=w_codes[:, P * g : P * g + P].bitcast(FP8X4),
-                        lhsT_scale=w_scales[:, P * g : P * g + P],
-                        rhs=c1[:, g, :].bitcast(FP8X4),
-                        rhs_scale=s1x[:, g, :],
-                        start=(g == 0),
-                        stop=(g == 1),
+
+        def zbt(n, gp):
+            if gp == 0:
+                st["zb", n] = zbp.tile([P, PIX], F32, tag="zb", name="zb")
+            nc.scalar.activation(
+                out=st["zb", n][:, 512 * gp : 512 * gp + 512],
+                in_=st["zt", n, gp][:],
+                func=ACT.Identity,
+                bias=bvec[:, 0:1],
+                scale=1.0,
+            )
+
+        def ztr(n, gp):
+            zp = ps_z.tile([P, 4, S4, K], F32, tag="z", name="zp")
+            st["z", n, gp] = zp
+            for u in range(2):
+                for e in range(2):
+                    wb = 2 * gp + u
+                    nc.tensor.transpose(
+                        zp[:, 2 * u + e].rearrange("q s k -> q (s k)"),
+                        st["zb", n][:, 256 * wb + e : 256 * wb + 256 : 2],
+                        ident_f[:],
                     )
-                nc.scalar.activation(
-                    out=zbt[:, 512 * gp : 512 * gp + 512],
-                    in_=zt[:],
-                    func=ACT.Identity,
-                    bias=bvec[:, 0:1],
-                    scale=1.0,
-                )
 
         def over_k_and_s(tile, i):
             return (
@@ -169,261 +214,446 @@ def tile_sralnet_pa_t_kernel(tc, x, centroids, out):
                 tile[:, i, 8 * S4 :].rearrange("q (t k) -> q t k", k=K),
             )
 
-        def stage_b(n):
-            i = n % LNG
-            grp = n // LNG
-            zbt = zbts[n]
-            z_ps = []
-            for gp in range(2):
-                zp = ps_z.tile([P, 4, S4, K], F32, tag="z", name="zp")
-                for u in range(2):
-                    for e in range(2):
-                        wb = 2 * gp + u
-                        nc.tensor.transpose(
-                            zp[:, 2 * u + e].rearrange("q s k -> q (s k)"),
-                            zbt[:, 256 * wb + e : 256 * wb + 256 : 2],
-                            ident_f[:],
-                        )
-                z_ps.append(zp)
-            d = dp.tile([P, S4, 8, K], F32, tag="d", name="d")
-            logits[n] = d
-            e1 = smp.tile([P, 8, S4, K], BF16, tag="e1", name="e1")
-            e2 = smp.tile([P, S4, 8, K], F32, tag="e2", name="e2")
-            if i == 0:
-                sums[grp] = sump.tile([P, LNG, 8 * S4 + 8 * K], F32, tag="sums", name="sums")
-                maxes[grp] = sump.tile([P, LNG, 8 * S4 + 8 * K], F32, tag="maxes", name="maxes")
-            sum_k, sum_s = over_k_and_s(sums[grp], i)
-            max_k, max_s = over_k_and_s(maxes[grp], i)
-            for gp in range(2):
-                ts = slice(4 * gp, 4 * gp + 4)
-                nc.vector.tensor_reduce(
-                    out=max_k[:, ts, :], in_=z_ps[gp][:], axis=AX.X, op=ALU.max, negate=True
-                )
-                nc.vector.tensor_reduce(
-                    out=max_s[:, ts, :],
-                    in_=z_ps[gp][:].rearrange("q t s k -> q t k s"),
-                    axis=AX.X,
-                    op=ALU.max,
-                )
-                nc.vector.tensor_tensor(
-                    out=d[:, :, ts, :].rearrange("q s t k -> q t s k"),
-                    in0=z_ps[gp][:],
-                    in1=max_s[:, ts, :].unsqueeze(2).to_broadcast([P, 4, S4, K]),
-                    op=ALU.subtract,
-                )
-            for t in range(8):
-                for s in range(S4):
-                    nc.scalar.activation(
-                        out=e1[:, t, s, :],
-                        in_=z_ps[t // 4][:, t % 4, s, :],
-                        func=ACT.Exp,
-                        bias=max_k[:, t, s : s + 1],
-                        scale=1.0,
-                        accum_out=sum_k[:, t, s : s + 1],
-                    )
-            nc.scalar.activation(out=e2[:], in_=d[:], func=ACT.Exp)
-            half_sum = smp.tile([P, 2, 8, K], F32, tag="half_sum", name="half_sum")
-            nc.vector.tensor_tensor(
-                out=half_sum[:], in0=e2[:, 0:2], in1=e2[:, 2:4], op=ALU.add
-            )
-            nc.vector.tensor_tensor(
-                out=sum_s, in0=half_sum[:, 0], in1=half_sum[:, 1], op=ALU.add
+        def soft_tiles(n):
+            st["d", n] = dp.tile([P, S4, 8, K], F32, tag="d", name="d")
+            st["e1", n] = smp.tile([P, 8, S4, K], BF16, tag="e1", name="e1")
+            st["e2", n] = smp.tile([P, S4, 8, K], F32, tag="e2", name="e2")
+            lg, i = divmod(n + 1, LNG)
+            if i == 0 or n == 0:
+                for name in ("sums", "maxes"):
+                    st[name, lg] = sump.tile([P, LNG, 8 * S4 + 8 * K], F32, tag=name, name=name)
+            st["sum", n] = over_k_and_s(st["sums", lg], i)
+            st["max", n] = over_k_and_s(st["maxes", lg], i)
+
+        def max_s(n, gp):
+            nc.vector.tensor_reduce(
+                out=st["max", n][1][:, 4 * gp : 4 * gp + 4, :],
+                in_=st["z", n, gp][:].rearrange("q t s k -> q t k s"),
+                axis=AX.X,
+                op=ALU.max,
             )
 
-        def log_sums(grp):
-            flat = sums[grp][:].rearrange("q i c -> q (i c)")
-            nc.scalar.activation(out=flat, in_=flat, func=ACT.Ln)
+        def max_k(n, gp):
+            nc.vector.tensor_reduce(
+                out=st["max", n][0][:, 4 * gp : 4 * gp + 4, :],
+                in_=st["z", n, gp][:],
+                axis=AX.X,
+                op=ALU.max,
+                negate=True,
+            )
+
+        def sub_s(n, gp):
+            ts = slice(4 * gp, 4 * gp + 4)
             nc.vector.tensor_tensor(
-                out=flat,
-                in0=maxes[grp][:].rearrange("q i c -> q (i c)"),
-                in1=flat,
+                out=st["d", n][:, :, ts, :].rearrange("q s t k -> q t s k"),
+                in0=st["z", n, gp][:],
+                in1=st["max", n][1][:, ts, :].unsqueeze(2).to_broadcast([P, 4, S4, K]),
                 op=ALU.subtract,
             )
 
-        def stage_d(n):
-            i = n % LNG
-            a = logits[n]
-            lse_k, lse_s = over_k_and_s(sums[n // LNG], i)
-            a_flat = a[:].rearrange("q s t k -> q s (t k)")
+        def exp_k(n, gp):
+            for t in range(4 * gp, 4 * gp + 4):
+                for s in range(S4):
+                    nc.scalar.activation(
+                        out=st["e1", n][:, t, s, :],
+                        in_=st["z", n, gp][:, t % 4, s, :],
+                        func=ACT.Exp,
+                        bias=st["max", n][0][:, t, s : s + 1],
+                        scale=1.0,
+                        accum_out=st["sum", n][0][:, t, s : s + 1],
+                    )
+
+        def exp_s(n):
+            nc.scalar.activation(out=st["e2", n][:], in_=st["d", n][:], func=ACT.Exp)
+
+        def half_sum(n):
+            e2 = st["e2", n]
+            st["hs", n] = smp.tile([P, 2, 8, K], F32, tag="hs", name="hs")
+            nc.vector.tensor_tensor(
+                out=st["hs", n][:], in0=e2[:, 0:2], in1=e2[:, 2:4], op=ALU.add
+            )
+
+        def sum_s(n):
+            hs = st["hs", n]
+            nc.vector.tensor_tensor(
+                out=st["sum", n][1], in0=hs[:, 0], in1=hs[:, 1], op=ALU.add
+            )
+
+        def both(name, last):
+            lg, i = divmod(last + 1, LNG)
+            first = 1 if last == 0 else 0
+            return st[name, lg][:, first : i + 1, :].rearrange("q i c -> q (i c)")
+
+        def log_sums(last):
+            flat = both("sums", last)
+            nc.scalar.activation(out=flat, in_=flat, func=ACT.Ln)
+
+        def log_sum_exps(last):
+            flat = both("sums", last)
+            nc.vector.tensor_tensor(
+                out=flat, in0=both("maxes", last), in1=flat, op=ALU.subtract
+            )
+
+        def log_prod(n):
+            a_flat = st["d", n][:].rearrange("q s t k -> q s (t k)")
             nc.vector.scalar_tensor_tensor(
                 out=a_flat,
                 in0=a_flat,
                 scalar=2.0,
-                in1=lse_s.rearrange("q t k -> q (t k)")
+                in1=st["sum", n][1]
+                .rearrange("q t k -> q (t k)")
                 .unsqueeze(1)
                 .to_broadcast([P, S4, 8 * K]),
                 op0=ALU.mult,
                 op1=ALU.add,
             )
-            for t in range(8):
+
+        def exp_prod(n, gp):
+            a = st["d", n]
+            for t in range(4 * gp, 4 * gp + 4):
                 for s in range(S4):
                     nc.scalar.activation(
                         out=a[:, s, t, :],
                         in_=a[:, s, t, :],
                         func=ACT.Exp,
-                        bias=lse_k[:, t, s : s + 1],
+                        bias=st["sum", n][0][:, t, s : s + 1],
                         scale=1.0,
                     )
-            lo = a[:, 0:2].rearrange("q s t k -> q (s t k)")
-            hi = a[:, 2:4].rearrange("q s t k -> q (s t k)")
+
+        def plus_one(n):
+            hi = st["d", n][:, 2:4].rearrange("q s t k -> q (s t k)")
             nc.vector.tensor_scalar_add(out=hi, in0=hi, scalar1=1.0)
+
+        def pair_mult(n):
+            lo = st["d", n][:, 0:2].rearrange("q s t k -> q (s t k)")
+            hi = st["d", n][:, 2:4].rearrange("q s t k -> q (s t k)")
             nc.vector.scalar_tensor_tensor(
                 out=lo, in0=lo, scalar=1.0, in1=hi, op0=ALU.add, op1=ALU.mult
             )
-            multf = mfp.tile([P, 8, K], F32, tag="multf", name="multf")
-            multfs[n] = multf
+
+        def mult(n):
+            a = st["d", n]
+            st["multf", n] = mfp.tile([P, 8, K], F32, tag="multf", name="multf")
             nc.vector.tensor_tensor(
-                out=multf[:], in0=a[:, 0], in1=a[:, 1], op=ALU.mult
+                out=st["multf", n][:], in0=a[:, 0], in1=a[:, 1], op=ALU.mult
             )
+
+        def round_mult(n):
             i = n % GRP
             nc.vector.tensor_copy(
                 out=mb[i][:, :, K * i : K * i + K, :],
-                in_=multf[:].rearrange("q (g t) k -> q g k t", g=2),
+                in_=st["multf", n][:].rearrange("q (g t) k -> q g k t", g=2),
             )
+
+        def qm(n):
             mc = smp.tile([P, 2 * P], U32, tag="mc", name="mc", align_bytes=64)
             msc = smp.tile([P, 2 * P], U8, tag="msc", name="msc", align_bytes=64)
+            st["m", n] = (mc, msc)
             nc.vector.quantize_mx(
                 out=mc[:].bitcast(FP8X4),
                 scales=msc[:],
-                in_=mb[i][:].rearrange("q g c t -> q (g c t)"),
+                in_=mb[n % GRP][:].rearrange("q g c t -> q (g c t)"),
             )
-            mults[n] = (mc, msc)
 
-        def stage_p(n):
-            c2 = c2p.tile([P, 2, C], U32, tag="c2", name="c2", align_bytes=64)
-            s2x = c2p.tile([P, 2, C], U8, tag="s2x", name="s2x", align_bytes=64)
-            codes2[n] = (c2, s2x)
-            for gp in range(2):
-                raw_w = raws[n, gp][:].bitcast(F32)
-                g2 = g2p.tile([P, 4 * C], BF16, tag="g2", name="g2", align_bytes=64)
-                g2w = g2[:].bitcast(F32).rearrange("q (c u) -> q c u", u=2)
-                for rp in range(4):
-                    xt = ps_xt.tile([P, 2, 2, P], F32, tag="xt", name="xt")
-                    for rl in range(2):
-                        for u in range(2):
-                            nc.tensor.transpose(
-                                xt[:, rl, u, :],
-                                raw_w[:, 2 * rp + rl, P * u : P * u + P],
-                                ident_f[:],
-                            )
-                    nc.scalar.copy(
-                        out=g2w[:, 256 * rp : 256 * rp + 256, :].rearrange(
-                            "q (rl p) u -> q rl p u", rl=2
-                        ),
-                        in_=xt[:].rearrange("q rl u p -> q rl p u"),
+        def g2_tile(n, gp):
+            st["g2", n, gp] = g2p.tile([P, 4 * C], BF16, tag="g2", name="g2", align_bytes=64)
+
+        def xtr(n, gp, rp):
+            raw_w = st["raw", n, gp][:].bitcast(F32)
+            xt = ps_xt.tile([P, 2, 2, P], F32, tag="xt", name="xt")
+            st["xt", n, gp, rp] = xt
+            for rl in range(2):
+                for u in range(2):
+                    nc.tensor.transpose(
+                        xt[:, rl, u, :], raw_w[:, 2 * rp + rl, P * u : P * u + P], ident_f[:]
                     )
-                nc.vector.quantize_mx(
-                    out=c2[:, gp, :].bitcast(FP8X4), scales=s2x[:, gp, :], in_=g2[:]
-                )
 
-        def stage_v(n):
+        def xev(n, gp, rp):
+            g2w = st["g2", n, gp][:].bitcast(F32).rearrange("q (c u) -> q c u", u=2)
+            nc.scalar.copy(
+                out=g2w[:, 256 * rp : 256 * rp + 256, :].rearrange("q (rl p) u -> q rl p u", rl=2),
+                in_=st["xt", n, gp, rp][:].rearrange("q rl u p -> q rl p u"),
+            )
+
+        def q2(n, gp):
+            if gp == 0:
+                c2 = c2p.tile([P, 2, C], U32, tag="c2", name="c2", align_bytes=64)
+                s2x = c2p.tile([P, 2, C], U8, tag="s2x", name="s2x", align_bytes=64)
+                st["c2", n] = (c2, s2x)
+            c2, s2x = st["c2", n]
+            nc.vector.quantize_mx(
+                out=c2[:, gp, :].bitcast(FP8X4), scales=s2x[:, gp, :], in_=st["g2", n, gp][:]
+            )
+
+        def vmm(n):
             i = n % GRP
-            grp = n // GRP
-            mc, msc = mults[n]
-            c2, s2x = codes2[n]
             if i == 0:
-                state["v"] = [
+                st["v"] = [
                     ps_v.tile([P, 512], F32, tag="v%d" % hc, name="v_ps%d" % hc) for hc in range(2)
                 ]
-            v_ps = state["v"]
+            mc, msc = st["m", n]
+            c2, s2x = st["c2", n]
             for hc in range(2):
                 for gp in range(2):
                     nc.tensor.matmul_mx(
-                        out=v_ps[hc][:],
+                        out=st["v"][hc][:],
                         lhsT=mc[:, P * gp : P * gp + P].bitcast(FP8X4),
                         lhsT_scale=msc[:, P * gp : P * gp + P],
                         rhs=c2[:, gp, 512 * hc : 512 * hc + 512].bitcast(FP8X4),
                         rhs_scale=s2x[:, gp, 512 * hc : 512 * hc + 512],
                         start=(i == 0 and gp == 0),
-                        stop=(i == 3 and gp == 1),
+                        stop=(i == GRP - 1 and gp == 1),
                     )
-            if i != 3:
-                return
-            part = ps_xt.tile([P, GRP, 2], F32, tag="xt", name="part")
+
+        def ep_part(grp):
+            small = ps_zt.tile([P, 16], F32, tag="zT", name="small")
+            st["small"] = small
             for j in range(GRP):
                 for g in range(2):
                     nc.tensor.matmul(
-                        out=part[:, j, :],
-                        lhsT=multfs[n - 3 + j][:, 4 * g : 4 * g + 4, :].rearrange("q t k -> q (t k)"),
+                        out=small[:, 2 * j : 2 * j + 2],
+                        lhsT=st["multf", GRP * grp + j][:, 4 * g : 4 * g + 4, :].rearrange(
+                            "q t k -> q (t k)"
+                        ),
                         rhs=ones2[:],
                         start=(g == 0),
                         stop=(g == 1),
                     )
-            spread = epi.tile([P, GRP, K], F32, tag="spread", name="spread")
+
+        def ep_spread():
+            st["spread"] = epi.tile([P, GRP, K], F32, tag="spread", name="spread")
             nc.vector.tensor_tensor(
-                out=spread[:],
-                in0=part[:, :, 0:1].to_broadcast([P, GRP, K]),
+                out=st["spread"][:],
+                in0=st["small"][:, 0 : 2 * GRP : 2].unsqueeze(2).to_broadcast([P, GRP, K]),
                 in1=sel[:].unsqueeze(1).to_broadcast([P, GRP, K]),
                 op=ALU.mult,
             )
-            pss = ps_xt.tile([P, 2], F32, tag="xt", name="pss")
+
+        def ep_msum():
             nc.tensor.matmul(
-                out=pss[:],
-                lhsT=spread[:].rearrange("p i k -> p (i k)"),
+                out=st["small"][:, 8:10],
+                lhsT=st["spread"][:].rearrange("p i k -> p (i k)"),
                 rhs=ones2[:],
                 start=True,
                 stop=True,
             )
-            negms = epi.tile([P, 1], F32, tag="negms", name="negms")
-            nc.vector.tensor_scalar_mul(out=negms[:], in0=pss[:, 0:1], scalar1=-1.0)
-            v2 = epi.tile([P, C], F32, tag="v2", name="v2")
-            for hc in range(2):
-                nc.vector.scalar_tensor_tensor(
-                    out=v2[:, 512 * hc : 512 * hc + 512],
-                    in0=rep4[:, 512 * hc : 512 * hc + 512],
-                    scalar=negms[:, 0:1],
-                    in1=v_ps[hc][:],
-                    op0=ALU.mult,
-                    op1=ALU.add,
-                )
-            sq = epi.tile([P, C], BF16, tag="sq", name="sq")
-            ss = epi.tile([P, 1], F32, tag="ss", name="ss")
-            nc.scalar.activation(out=sq[:], in_=v2[:], func=ACT.Square, accum_out=ss[:])
-            ssc = epi.tile([P, 1], F32, tag="ssc", name="ssc")
-            nc.vector.tensor_scalar_max(out=ssc[:], in0=ss[:], scalar1=EPS * EPS)
-            rn1 = epi.tile([P, 1], F32, tag="rn1", name="rn1")
-            nc.gpsimd.tensor_tensor(out=rn1[:], in0=ssc[:], in1=mhalf[:], op=ALU.pow)
-            q2 = epi.tile([P, 2], F32, tag="q2", name="q2")
-            nc.vector.tensor_scalar(
-                out=q2[:],
-                in0=ss[:, 0:1].to_broadcast([P, 2]),
-                scalar1=rn1[:, 0:1],
-                scalar2=rn1[:, 0:1],
-                op0=ALU.mult,
-                op1=ALU.mult,
-            )
-            pst = ps_xt.tile([P, 2], F32, tag="xt", name="pst")
-            nc.tensor.matmul(out=pst[:], lhsT=bd[:], rhs=q2[:], start=True, stop=True)
-            totc = epi.tile([P, 1], F32, tag="totc", name="totc")
-            nc.vector.tensor_scalar_max(out=totc[:], in0=pst[:, 0:1], scalar1=EPS * EPS)
-            rn2 = epi.tile([P, 1], F32, tag="rn2", name="rn2")
-            nc.gpsimd.tensor_tensor(out=rn2[:], in0=totc[:], in1=mhalf[:], op=ALU.pow)
-            nc.vector.tensor_scalar(
-                out=v2[:],
-                in0=v2[:],
-                scalar1=rn1[:, 0:1],
-                scalar2=rn2[:, 0:1],
-                op0=ALU.mult,
-                op1=ALU.mult,
-            )
-            nc.sync.dma_start(
-                out=out[4 * grp : 4 * grp + 4, :].rearrange("i (k c) -> (i k) c", c=C),
-                in_=v2[:],
+
+        def ep_neg():
+            st["negms"] = epi.tile([P, 1], F32, tag="negms", name="negms")
+            nc.vector.tensor_scalar_mul(
+                out=st["negms"][:], in0=st["small"][:, 8:9], scalar1=-1.0
             )
 
-        for n in range(AHEAD):
-            stage_a(n)
-        stage_p(0)
-        for n in range(N_IMG + LAG):
-            if n < N_IMG:
-                stage_b(n)
-            if n >= LAG:
-                stage_d(n - LAG)
-            if n + AHEAD < N_IMG:
-                stage_a(n + AHEAD)
-            if n + 1 < N_IMG:
-                stage_p(n + 1)
-            if n < N_IMG and n % LNG == LNG - 1:
-                log_sums(n // LNG)
-            if n >= LAG:
-                stage_v(n - LAG)
+        def ep_v2(grp, hc):
+            if hc == 0:
+                st["v2", grp] = epi.tile([P, C], F32, tag="v2", name="v2")
+            nc.vector.scalar_tensor_tensor(
+                out=st["v2", grp][:, 512 * hc : 512 * hc + 512],
+                in0=rep4[:, 512 * hc : 512 * hc + 512],
+                scalar=st["negms"][:, 0:1],
+                in1=st["v"][hc][:],
+                op0=ALU.mult,
+                op1=ALU.add,
+            )
+
+        def ep_sq(grp):
+            sq = epi.tile([P, C], BF16, tag="sq", name="sq")
+            st["ss"] = epi.tile([P, 1], F32, tag="ss", name="ss")
+            nc.scalar.activation(
+                out=sq[:], in_=st["v2", grp][:], func=ACT.Square, accum_out=st["ss"][:]
+            )
+
+        def ep_rn1():
+            ssc = epi.tile([P, 1], F32, tag="ssc", name="ssc")
+            nc.vector.tensor_scalar_max(out=ssc[:], in0=st["ss"][:], scalar1=EPS * EPS)
+            st["rn1"] = epi.tile([P, 1], F32, tag="rn1", name="rn1")
+            nc.gpsimd.tensor_tensor(out=st["rn1"][:], in0=ssc[:], in1=mhalf[:], op=ALU.pow)
+
+        def ep_q2():
+            st["q2"] = epi.tile([P, 2], F32, tag="q2", name="q2")
+            nc.vector.tensor_scalar(
+                out=st["q2"][:],
+                in0=st["ss"][:, 0:1].to_broadcast([P, 2]),
+                scalar1=st["rn1"][:, 0:1],
+                scalar2=st["rn1"][:, 0:1],
+                op0=ALU.mult,
+                op1=ALU.mult,
+            )
+
+        def ep_tot():
+            st["tot"] = ps_zt.tile([P, 2], F32, tag="zT", name="tot")
+            nc.tensor.matmul(out=st["tot"][:], lhsT=bd[:], rhs=st["q2"][:], start=True, stop=True)
+
+        def ep_rn2():
+            totc = epi.tile([P, 1], F32, tag="totc", name="totc")
+            nc.vector.tensor_scalar_max(out=totc[:], in0=st["tot"][:, 0:1], scalar1=EPS * EPS)
+            st["rn2"] = epi.tile([P, 1], F32, tag="rn2", name="rn2")
+            nc.gpsimd.tensor_tensor(out=st["rn2"][:], in0=totc[:], in1=mhalf[:], op=ALU.pow)
+
+        def ep_scale(grp):
+            nc.vector.tensor_scalar(
+                out=st["v2", grp][:],
+                in0=st["v2", grp][:],
+                scalar1=st["rn1"][:, 0:1],
+                scalar2=st["rn2"][:, 0:1],
+                op0=ALU.mult,
+                op1=ALU.mult,
+            )
+
+        def ep_store(grp):
+            nc.sync.dma_start(
+                out=out[4 * grp : 4 * grp + 4, :].rearrange("i (k c) -> (i k) c", c=C),
+                in_=st["v2", grp][:],
+            )
+
+        def step(i):
+            end = N_IMG - 1
+            n = i if 0 <= i < N_IMG else None
+            nz = i + 1 if 0 <= i + 1 < N_IMG else None
+            p = i + 1 if 0 <= i + 1 < N_IMG else None
+            na = i + 2 if 0 <= i + 2 < N_IMG else None
+            js = [j for j in (i - 2,) if 0 <= j < end] + [end] * (i == end + 1)
+            jts = [j for j in (i - 3,) if 0 <= j < end] + [end] * (i == end + 2)
+            g1 = (i - 4) // GRP if i - 4 in range(3, end, GRP) else None
+            g2 = (i - 5) // GRP if i - 5 in range(3, end, GRP) else None
+            if i == end + 3:
+                g1 = LAST
+            if i == end + 4:
+                g2 = LAST
+            last = i - 1 if i - 1 in range(0, end, LNG) or i - 1 == end else None
+
+            if 2 <= i + 3 < N_IMG:
+                load(i + 3, 0)
+                load(i + 3, 1)
+            if n is not None:
+                soft_tiles(n)
+            if na is not None:
+                g1_tile(na, 0)
+            if p is not None:
+                g2_tile(p, 0)
+            if g1 is not None and g1 != LAST:
+                ep_part(g1)
+            if g2 is not None:
+                ep_tot()
+            if last is not None:
+                log_sums(last)
+
+            if n is not None:
+                max_s(n, 0)
+                max_k(n, 0)
+            if g1 is not None and g1 != LAST:
+                ep_spread()
+            if g2 is not None:
+                ep_rn2()
+            if nz is not None:
+                q1(nz, 1)
+            if n is not None:
+                sub_s(n, 0)
+            for r in range(4):
+                if p is not None:
+                    xtr(p, 0, r)
+                if r == 0 and g1 is not None and g1 != LAST:
+                    ep_msum()
+                    ep_neg()
+                if r == 1 and nz is not None:
+                    zmm(nz, 0)
+                if p is not None:
+                    xev(p, 0, r)
+                if r < 2 and na is not None:
+                    il_s(na, 0, r)
+                if r == 2 and nz is not None:
+                    zbt(nz, 0)
+            if n is not None:
+                max_s(n, 1)
+            for j in jts:
+                plus_one(j)
+            if n is not None:
+                max_k(n, 1)
+            for j in jts:
+                pair_mult(j)
+            if n is not None:
+                sub_s(n, 1)
+                exp_k(n, 0)
+                exp_k(n, 1)
+                exp_s(n)
+            if g1 is not None:
+                ep_v2(g1, 0)
+            for j in jts:
+                mult(j)
+            if g1 is not None:
+                ep_v2(g1, 1)
+            if end in jts:
+                ep_part(LAST)
+            if na is not None:
+                il_v(na, 0, 0)
+            for j in jts:
+                round_mult(j)
+            if end in jts:
+                ep_spread()
+                ep_msum()
+            if na is not None:
+                il_v(na, 0, 1)
+            for j in jts:
+                qm(j)
+            if end in jts:
+                ep_neg()
+            if i == -2:
+                prep_norm()
+                prep_w()
+
+            if na is not None:
+                g1_tile(na, 1)
+            if last is not None:
+                log_sum_exps(last)
+            if p is not None:
+                q2(p, 0)
+                g2_tile(p, 1)
+            for j in js:
+                log_prod(j)
+            if g2 is not None:
+                ep_scale(g2)
+            if nz is not None:
+                zmm(nz, 1)
+            for r in range(4):
+                if p is not None:
+                    xtr(p, 1, r)
+                    xev(p, 1, r)
+                if r == 0 and nz is not None:
+                    zbt(nz, 1)
+                if r < 2 and na is not None:
+                    il_s(na, 1, r)
+                if r == 1 and g1 is not None:
+                    ep_sq(g1)
+            for j in jts:
+                vmm(j)
+            if nz is not None:
+                ztr(nz, 0)
+                ztr(nz, 1)
+            if na is not None:
+                il_v(na, 1, 0)
+            if i == -2:
+                prep_wq()
+            if na is not None:
+                q1(na, 0)
+            if n is not None:
+                half_sum(n)
+            if g1 is not None:
+                ep_rn1()
+            if na is not None:
+                il_v(na, 1, 1)
+            if i == -2:
+                prep_b()
+            if n is not None:
+                sum_s(n)
+            if g1 is not None:
+                ep_q2()
+            if p is not None:
+                q2(p, 1)
+            for j in js:
+                exp_prod(j, 0)
+                exp_prod(j, 1)
+            if g2 is not None:
+                ep_store(g2)
+
+        for i in range(-2, N_IMG + 4):
+            step(i)

@@ -20,7 +20,8 @@ K = 32
 S4 = 4
 EPS = 1e-12
 WV0 = 344
-WV = 408
+WVL = 424
+WV = 424
 LNG = 2
 GRP = 4
 LAST = N_IMG // GRP - 1
@@ -152,12 +153,14 @@ def tile_sralnet_pa_t_kernel(tc, x, centroids, out):
             )
 
         def wv(n):
-            return WV0 if n < 2 else WV
+            return WV0 if n < 2 else WVL if n % 2 == 0 and n > 2 else WV
 
         def il_v(n, gp, g):
             regroup(nc.vector.tensor_copy, n, gp, g, 0, wv(n))
 
         def il_s(n, gp, g):
+            if wv(n) == 512:
+                return
             regroup(nc.scalar.copy, n, gp, g, wv(n), 512)
 
         def q1(n, gp):
@@ -218,8 +221,8 @@ def tile_sralnet_pa_t_kernel(tc, x, centroids, out):
             st["d", n] = dp.tile([P, S4, 8, K], F32, tag="d", name="d")
             st["e1", n] = smp.tile([P, 8, S4, K], BF16, tag="e1", name="e1")
             st["e2", n] = smp.tile([P, S4, 8, K], F32, tag="e2", name="e2")
-            lg, i = divmod(n + 1, LNG)
-            if i == 0 or n == 0:
+            lg, i = divmod(n, LNG)
+            if i == 0:
                 for name in ("sums", "maxes"):
                     st[name, lg] = sump.tile([P, LNG, 8 * S4 + 8 * K], F32, tag=name, name=name)
             st["sum", n] = over_k_and_s(st["sums", lg], i)
@@ -279,19 +282,25 @@ def tile_sralnet_pa_t_kernel(tc, x, centroids, out):
                 out=st["sum", n][1], in0=hs[:, 0], in1=hs[:, 1], op=ALU.add
             )
 
-        def both(name, last):
-            lg, i = divmod(last + 1, LNG)
-            first = 1 if last == 0 else 0
-            return st[name, lg][:, first : i + 1, :].rearrange("q i c -> q (i c)")
+        def sums_beside(n, beside):
+            gate = smp.tile([P, 1], F32, tag="gate", name="gate")
+            nc.gpsimd.tensor_copy(out=gate[:], in_=st["max", beside][1][:, 0, 0:1])
+            e2 = st["e2", n]
+            hs = smp.tile([P, 2, 8, K], F32, tag="hs", name="hs")
+            nc.gpsimd.tensor_tensor(out=hs[:], in0=e2[:, 0:2], in1=e2[:, 2:4], op=ALU.add)
+            nc.gpsimd.tensor_tensor(out=st["sum", n][1], in0=hs[:, 0], in1=hs[:, 1], op=ALU.add)
 
-        def log_sums(last):
-            flat = both("sums", last)
+        def log_sums(lg):
+            flat = st["sums", lg][:].rearrange("q i c -> q (i c)")
             nc.scalar.activation(out=flat, in_=flat, func=ACT.Ln)
 
-        def log_sum_exps(last):
-            flat = both("sums", last)
+        def log_sum_exps(lg):
+            flat = st["sums", lg][:].rearrange("q i c -> q (i c)")
             nc.vector.tensor_tensor(
-                out=flat, in0=both("maxes", last), in1=flat, op=ALU.subtract
+                out=flat,
+                in0=st["maxes", lg][:].rearrange("q i c -> q (i c)"),
+                in1=flat,
+                op=ALU.subtract,
             )
 
         def log_prod(n):
@@ -406,7 +415,7 @@ def tile_sralnet_pa_t_kernel(tc, x, centroids, out):
                     )
 
         def ep_part(grp):
-            small = ps_zt.tile([P, 16], F32, tag="zT", name="small")
+            small = ps_xt.tile([P, 16], F32, tag="xt", name="small")
             st["small"] = small
             for j in range(GRP):
                 for g in range(2):
@@ -456,24 +465,40 @@ def tile_sralnet_pa_t_kernel(tc, x, centroids, out):
                 op1=ALU.add,
             )
 
-        def ep_sq(grp):
-            sq = epi.tile([P, C], BF16, tag="sq", name="sq")
-            st["ss"] = epi.tile([P, 1], F32, tag="ss", name="ss")
+        def ep_sq(grp, hc):
+            if hc == 0:
+                st["sq"] = epi.tile([P, C], BF16, tag="sq", name="sq")
+                st["ss"] = epi.tile([P, 2], F32, tag="ss", name="ss")
+            half_c = slice(512 * hc, 512 * hc + 512)
             nc.scalar.activation(
-                out=sq[:], in_=st["v2", grp][:], func=ACT.Square, accum_out=st["ss"][:]
+                out=st["sq"][:, half_c],
+                in_=st["v2", grp][:, half_c],
+                func=ACT.Square,
+                accum_out=st["ss"][:, hc : hc + 1],
             )
 
         def ep_rn1():
             ssc = epi.tile([P, 1], F32, tag="ssc", name="ssc")
-            nc.vector.tensor_scalar_max(out=ssc[:], in0=st["ss"][:], scalar1=EPS * EPS)
+            nc.vector.tensor_scalar(
+                out=ssc[:],
+                in0=st["ss"][:, 0:1],
+                scalar1=st["ss"][:, 1:2],
+                scalar2=EPS * EPS,
+                op0=ALU.add,
+                op1=ALU.max,
+            )
             st["rn1"] = epi.tile([P, 1], F32, tag="rn1", name="rn1")
             nc.gpsimd.tensor_tensor(out=st["rn1"][:], in0=ssc[:], in1=mhalf[:], op=ALU.pow)
+            st["sst"] = epi.tile([P, 1], F32, tag="sst", name="sst")
+            nc.vector.tensor_tensor(
+                out=st["sst"][:], in0=st["ss"][:, 0:1], in1=st["ss"][:, 1:2], op=ALU.add
+            )
 
         def ep_q2():
             st["q2"] = epi.tile([P, 2], F32, tag="q2", name="q2")
             nc.vector.tensor_scalar(
                 out=st["q2"][:],
-                in0=st["ss"][:, 0:1].to_broadcast([P, 2]),
+                in0=st["sst"][:, 0:1].to_broadcast([P, 2]),
                 scalar1=st["rn1"][:, 0:1],
                 scalar2=st["rn1"][:, 0:1],
                 op0=ALU.mult,
@@ -481,7 +506,7 @@ def tile_sralnet_pa_t_kernel(tc, x, centroids, out):
             )
 
         def ep_tot():
-            st["tot"] = ps_zt.tile([P, 2], F32, tag="zT", name="tot")
+            st["tot"] = ps_xt.tile([P, 2], F32, tag="xt", name="tot")
             nc.tensor.matmul(out=st["tot"][:], lhsT=bd[:], rhs=st["q2"][:], start=True, stop=True)
 
         def ep_rn2():
@@ -490,39 +515,42 @@ def tile_sralnet_pa_t_kernel(tc, x, centroids, out):
             st["rn2"] = epi.tile([P, 1], F32, tag="rn2", name="rn2")
             nc.gpsimd.tensor_tensor(out=st["rn2"][:], in0=totc[:], in1=mhalf[:], op=ALU.pow)
 
-        def ep_scale(grp):
+        def ep_scale(grp, hc):
+            half_c = slice(512 * hc, 512 * hc + 512)
             nc.vector.tensor_scalar(
-                out=st["v2", grp][:],
-                in0=st["v2", grp][:],
+                out=st["v2", grp][:, half_c],
+                in0=st["v2", grp][:, half_c],
                 scalar1=st["rn1"][:, 0:1],
                 scalar2=st["rn2"][:, 0:1],
                 op0=ALU.mult,
                 op1=ALU.mult,
             )
 
-        def ep_store(grp):
+        def ep_store(grp, hc):
+            half_c = slice(512 * hc, 512 * hc + 512)
             nc.sync.dma_start(
-                out=out[4 * grp : 4 * grp + 4, :].rearrange("i (k c) -> (i k) c", c=C),
-                in_=st["v2", grp][:],
+                out=out[4 * grp : 4 * grp + 4, :].rearrange("i (k c) -> (i k) c", c=C)[:, half_c],
+                in_=st["v2", grp][:, half_c],
             )
 
-        def step(i):
-            end = N_IMG - 1
-            n = i if 0 <= i < N_IMG else None
-            nz = i + 1 if 0 <= i + 1 < N_IMG else None
-            p = i + 1 if 0 <= i + 1 < N_IMG else None
-            na = i + 2 if 0 <= i + 2 < N_IMG else None
-            js = [j for j in (i - 2,) if 0 <= j < end] + [end] * (i == end + 1)
-            jts = [j for j in (i - 3,) if 0 <= j < end] + [end] * (i == end + 2)
-            g1 = (i - 4) // GRP if i - 4 in range(3, end, GRP) else None
-            g2 = (i - 5) // GRP if i - 5 in range(3, end, GRP) else None
-            if i == end + 3:
-                g1 = LAST
-            if i == end + 4:
-                g2 = LAST
-            last = i - 1 if i - 1 in range(0, end, LNG) or i - 1 == end else None
+        end = N_IMG - 1
+        st["pl"] = None
 
-            if 2 <= i + 3 < N_IMG:
+        def step(i):
+            n = i if i >= 0 else None
+            nz = i + 1 if i >= -1 else None
+            p = i + 1 if -1 <= i else None
+            pl = st["pl"]
+            na = i + 2 if i + 2 <= end else None
+            j = i - 2 if i >= 2 else None
+            jt = i - 3 if i >= 3 else None
+            ends = range(GRP - 1, end, GRP)
+            g1 = (i - 4) // GRP if i - 4 in ends else None
+            g2 = (i - 5) // GRP if i - 5 in ends else None
+            g3 = (i - 6) // GRP if i - 6 in ends else None
+            lg = (i - 2) // LNG if i >= 2 and i % LNG == 0 else None
+
+            if 2 <= i + 3 <= end:
                 load(i + 3, 0)
                 load(i + 3, 1)
             if n is not None:
@@ -531,19 +559,15 @@ def tile_sralnet_pa_t_kernel(tc, x, centroids, out):
                 g1_tile(na, 0)
             if p is not None:
                 g2_tile(p, 0)
-            if g1 is not None and g1 != LAST:
-                ep_part(g1)
-            if g2 is not None:
+            if g3 is not None:
                 ep_tot()
-            if last is not None:
-                log_sums(last)
 
             if n is not None:
                 max_s(n, 0)
+                if n > 0:
+                    sums_beside(n - 1, n)
                 max_k(n, 0)
-            if g1 is not None and g1 != LAST:
-                ep_spread()
-            if g2 is not None:
+            if g3 is not None:
                 ep_rn2()
             if nz is not None:
                 q1(nz, 1)
@@ -552,69 +576,75 @@ def tile_sralnet_pa_t_kernel(tc, x, centroids, out):
             for r in range(4):
                 if p is not None:
                     xtr(p, 0, r)
-                if r == 0 and g1 is not None and g1 != LAST:
-                    ep_msum()
-                    ep_neg()
                 if r == 1 and nz is not None:
                     zmm(nz, 0)
                 if p is not None:
                     xev(p, 0, r)
                 if r < 2 and na is not None:
                     il_s(na, 0, r)
+                if r == 3 and lg is not None:
+                    log_sums(lg)
                 if r == 2 and nz is not None:
                     zbt(nz, 0)
+            if g1 is not None:
+                ep_part(g1)
             if n is not None:
                 max_s(n, 1)
-            for j in jts:
-                plus_one(j)
-            if n is not None:
                 max_k(n, 1)
-            for j in jts:
-                pair_mult(j)
+            if pl is not None:
+                q2(pl, 1)
             if n is not None:
                 sub_s(n, 1)
                 exp_k(n, 0)
                 exp_k(n, 1)
                 exp_s(n)
-            if g1 is not None:
-                ep_v2(g1, 0)
-            for j in jts:
-                mult(j)
-            if g1 is not None:
-                ep_v2(g1, 1)
-            if end in jts:
-                ep_part(LAST)
+            if jt is not None:
+                plus_one(jt)
             if na is not None:
                 il_v(na, 0, 0)
-            for j in jts:
-                round_mult(j)
-            if end in jts:
+            if g1 is not None:
                 ep_spread()
                 ep_msum()
+            if jt is not None:
+                pair_mult(jt)
             if na is not None:
                 il_v(na, 0, 1)
-            for j in jts:
-                qm(j)
-            if end in jts:
+            if g1 is not None:
                 ep_neg()
+            if jt is not None:
+                mult(jt)
             if i == -2:
                 prep_norm()
                 prep_w()
 
             if na is not None:
                 g1_tile(na, 1)
-            if last is not None:
-                log_sum_exps(last)
+            if lg is not None:
+                log_sum_exps(lg)
+            if jt is not None:
+                round_mult(jt)
+            if g3 is not None:
+                ep_scale(g3, 0)
+            if g1 is not None:
+                ep_v2(g1, 0)
             if p is not None:
                 q2(p, 0)
+            if p == end:
+                p = None
+            if p is not None:
                 g2_tile(p, 1)
-            for j in js:
+            if g1 is not None:
+                ep_v2(g1, 1)
+            if jt is not None:
+                qm(jt)
+            if j is not None:
                 log_prod(j)
-            if g2 is not None:
-                ep_scale(g2)
             if nz is not None:
                 zmm(nz, 1)
             for r in range(4):
+                if r == 2 and nz is not None:
+                    ztr(nz, 0)
+                    ztr(nz, 1)
                 if p is not None:
                     xtr(p, 1, r)
                     xev(p, 1, r)
@@ -622,38 +652,118 @@ def tile_sralnet_pa_t_kernel(tc, x, centroids, out):
                     zbt(nz, 1)
                 if r < 2 and na is not None:
                     il_s(na, 1, r)
-                if r == 1 and g1 is not None:
-                    ep_sq(g1)
-            for j in jts:
-                vmm(j)
-            if nz is not None:
-                ztr(nz, 0)
-                ztr(nz, 1)
+                if r < 2 and g2 is not None:
+                    ep_sq(g2, r)
+            st["pl"] = p
+            if j is not None:
+                exp_prod(j, 0)
+                exp_prod(j, 1)
+            if jt is not None:
+                vmm(jt)
             if na is not None:
                 il_v(na, 1, 0)
             if i == -2:
                 prep_wq()
             if na is not None:
                 q1(na, 0)
-            if n is not None:
-                half_sum(n)
-            if g1 is not None:
+            if g2 is not None:
                 ep_rn1()
             if na is not None:
                 il_v(na, 1, 1)
             if i == -2:
                 prep_b()
-            if n is not None:
-                sum_s(n)
-            if g1 is not None:
-                ep_q2()
-            if p is not None:
-                q2(p, 1)
-            for j in js:
-                exp_prod(j, 0)
-                exp_prod(j, 1)
             if g2 is not None:
-                ep_store(g2)
+                ep_q2()
+            if g3 is not None:
+                ep_scale(g3, 1)
+                ep_store(g3, 0)
+                ep_store(g3, 1)
 
-        for i in range(-2, N_IMG + 4):
+        def finish():
+            soft_tiles(end)
+            g2_tile(end, 1)
+            ep_part(LAST - 1)
+            max_s(end, 0)
+            sums_beside(end - 1, end)
+            max_k(end, 0)
+            max_s(end, 1)
+            max_k(end, 1)
+            exp_k(end, 0)
+            exp_k(end, 1)
+            sub_s(end, 0)
+            sub_s(end, 1)
+            exp_s(end)
+            log_prod(end - 2)
+            plus_one(end - 3)
+            ep_spread()
+            ep_msum()
+            pair_mult(end - 3)
+            ep_neg()
+            exp_prod(end - 2, 0)
+            exp_prod(end - 2, 1)
+            mult(end - 3)
+            half_sum(end)
+            round_mult(end - 3)
+            sum_s(end)
+            log_sums(end // LNG)
+            ep_v2(LAST - 1, 0)
+            ep_v2(LAST - 1, 1)
+            qm(end - 3)
+            plus_one(end - 2)
+            vmm(end - 3)
+            for r in range(4):
+                xtr(end, 1, r)
+                xev(end, 1, r)
+            log_sum_exps(end // LNG)
+            pair_mult(end - 2)
+            log_prod(end - 1)
+            mult(end - 2)
+            log_prod(end)
+            exp_prod(end - 1, 0)
+            exp_prod(end - 1, 1)
+            exp_prod(end, 0)
+            exp_prod(end, 1)
+            round_mult(end - 2)
+            q2(end, 1)
+            qm(end - 2)
+            vmm(end - 2)
+            plus_one(end - 1)
+            pair_mult(end - 1)
+            plus_one(end)
+            mult(end - 1)
+            pair_mult(end)
+            round_mult(end - 1)
+            mult(end)
+            qm(end - 1)
+            vmm(end - 1)
+            round_mult(end)
+            ep_part(LAST)
+            qm(end)
+            vmm(end)
+            ep_spread()
+            ep_msum()
+            ep_sq(LAST - 1, 0)
+            ep_sq(LAST - 1, 1)
+            ep_neg()
+            for hc in range(2):
+                ep_v2(LAST, hc)
+            ep_rn1()
+            ep_q2()
+            ep_tot()
+            ep_rn2()
+            for hc in range(2):
+                ep_scale(LAST - 1, hc)
+                ep_store(LAST - 1, hc)
+            for hc in range(2):
+                ep_sq(LAST, hc)
+            ep_rn1()
+            ep_q2()
+            ep_tot()
+            ep_rn2()
+            for hc in range(2):
+                ep_scale(LAST, hc)
+                ep_store(LAST, hc)
+
+        for i in range(-2, end):
             step(i)
+        finish()

@@ -20,8 +20,8 @@ K = 32
 S4 = 4
 EPS = 1e-12
 WV0 = 344
-WVL = 424
-WV = 424
+WVL = 440
+WV = 440
 LNG = 2
 GRP = 4
 LAST = N_IMG // GRP - 1
@@ -414,13 +414,13 @@ def tile_sralnet_pa_t_kernel(tc, x, centroids, out):
                         stop=(i == GRP - 1 and gp == 1),
                     )
 
-        def ep_part(grp):
-            small = ps_xt.tile([P, 16], F32, tag="xt", name="small")
-            st["small"] = small
-            for j in range(GRP):
+        def ep_part(grp, images=range(GRP)):
+            if 0 in images:
+                st["small"] = ps_xt.tile([P, 16], F32, tag="xt", name="small")
+            for j in images:
                 for g in range(2):
                     nc.tensor.matmul(
-                        out=small[:, 2 * j : 2 * j + 2],
+                        out=st["small"][:, 2 * j : 2 * j + 2],
                         lhsT=st["multf", GRP * grp + j][:, 4 * g : 4 * g + 4, :].rearrange(
                             "q t k -> q (t k)"
                         ),
@@ -586,6 +586,9 @@ def tile_sralnet_pa_t_kernel(tc, x, centroids, out):
                     log_sums(lg)
                 if r == 2 and nz is not None:
                     zbt(nz, 0)
+            if nz == end:
+                zmm(nz, 1)
+                zbt(nz, 1)
             if g1 is not None:
                 ep_part(g1)
             if n is not None:
@@ -639,7 +642,7 @@ def tile_sralnet_pa_t_kernel(tc, x, centroids, out):
                 qm(jt)
             if j is not None:
                 log_prod(j)
-            if nz is not None:
+            if nz is not None and nz < end:
                 zmm(nz, 1)
             for r in range(4):
                 if r == 2 and nz is not None:
@@ -648,7 +651,7 @@ def tile_sralnet_pa_t_kernel(tc, x, centroids, out):
                 if p is not None:
                     xtr(p, 1, r)
                     xev(p, 1, r)
-                if r == 0 and nz is not None:
+                if r == 0 and nz is not None and nz < end:
                     zbt(nz, 1)
                 if r < 2 and na is not None:
                     il_s(na, 1, r)
@@ -688,10 +691,10 @@ def tile_sralnet_pa_t_kernel(tc, x, centroids, out):
             max_k(end, 0)
             max_s(end, 1)
             max_k(end, 1)
-            exp_k(end, 0)
-            exp_k(end, 1)
             sub_s(end, 0)
             sub_s(end, 1)
+            exp_k(end, 0)
+            exp_k(end, 1)
             exp_s(end)
             log_prod(end - 2)
             plus_one(end - 3)
@@ -710,51 +713,55 @@ def tile_sralnet_pa_t_kernel(tc, x, centroids, out):
             ep_v2(LAST - 1, 1)
             qm(end - 3)
             plus_one(end - 2)
-            vmm(end - 3)
-            for r in range(4):
+            for r in range(3):
                 xtr(end, 1, r)
+            vmm(end - 3)
+            ep_sq(LAST - 1, 0)
+            ep_sq(LAST - 1, 1)
+            for r in range(3):
                 xev(end, 1, r)
             log_sum_exps(end // LNG)
             pair_mult(end - 2)
             log_prod(end - 1)
+            ep_rn1()
             mult(end - 2)
             log_prod(end)
             exp_prod(end - 1, 0)
             exp_prod(end - 1, 1)
+            ep_q2()
+            round_mult(end - 2)
+            xtr(end, 1, 3)
+            xev(end, 1, 3)
             exp_prod(end, 0)
             exp_prod(end, 1)
-            round_mult(end - 2)
-            q2(end, 1)
+            ep_tot()
             qm(end - 2)
             vmm(end - 2)
+            ep_rn2()
             plus_one(end - 1)
             pair_mult(end - 1)
-            plus_one(end)
+            q2(end, 1)
             mult(end - 1)
-            pair_mult(end)
+            ep_part(LAST, range(GRP - 1))
+            plus_one(end)
             round_mult(end - 1)
-            mult(end)
+            pair_mult(end)
             qm(end - 1)
+            mult(end)
+            ep_part(LAST, [GRP - 1])
             vmm(end - 1)
+            ep_scale(LAST - 1, 0)
             round_mult(end)
-            ep_part(LAST)
-            qm(end)
-            vmm(end)
             ep_spread()
             ep_msum()
-            ep_sq(LAST - 1, 0)
-            ep_sq(LAST - 1, 1)
+            qm(end)
+            vmm(end)
+            ep_scale(LAST - 1, 1)
+            ep_store(LAST - 1, 0)
+            ep_store(LAST - 1, 1)
             ep_neg()
             for hc in range(2):
                 ep_v2(LAST, hc)
-            ep_rn1()
-            ep_q2()
-            ep_tot()
-            ep_rn2()
-            for hc in range(2):
-                ep_scale(LAST - 1, hc)
-                ep_store(LAST - 1, hc)
-            for hc in range(2):
                 ep_sq(LAST, hc)
             ep_rn1()
             ep_q2()

@@ -20,8 +20,8 @@ K = 32
 S4 = 4
 EPS = 1e-12
 WV0 = 344
-WVL = 440
-WV = 440
+WVL = 384
+WV = 384
 LNG = 2
 GRP = 4
 LAST = N_IMG // GRP - 1
@@ -548,6 +548,7 @@ def tile_sralnet_pa_t_kernel(tc, x, centroids, out):
             g1 = (i - 4) // GRP if i - 4 in ends else None
             g2 = (i - 5) // GRP if i - 5 in ends else None
             g3 = (i - 6) // GRP if i - 6 in ends else None
+            g4 = (i - 7) // GRP if i - 7 in ends else None
             lg = (i - 2) // LNG if i >= 2 and i % LNG == 0 else None
 
             if 2 <= i + 3 <= end:
@@ -559,8 +560,6 @@ def tile_sralnet_pa_t_kernel(tc, x, centroids, out):
                 g1_tile(na, 0)
             if p is not None:
                 g2_tile(p, 0)
-            if g3 is not None:
-                ep_tot()
 
             if n is not None:
                 max_s(n, 0)
@@ -568,7 +567,7 @@ def tile_sralnet_pa_t_kernel(tc, x, centroids, out):
                     sums_beside(n - 1, n)
                 max_k(n, 0)
             if g3 is not None:
-                ep_rn2()
+                ep_rn1()
             if nz is not None:
                 q1(nz, 1)
             if n is not None:
@@ -626,8 +625,10 @@ def tile_sralnet_pa_t_kernel(tc, x, centroids, out):
                 log_sum_exps(lg)
             if jt is not None:
                 round_mult(jt)
+            if g4 is not None:
+                ep_scale(g4, 0)
             if g3 is not None:
-                ep_scale(g3, 0)
+                ep_q2()
             if g1 is not None:
                 ep_v2(g1, 0)
             if p is not None:
@@ -658,6 +659,8 @@ def tile_sralnet_pa_t_kernel(tc, x, centroids, out):
                 if r < 2 and g2 is not None:
                     ep_sq(g2, r)
             st["pl"] = p
+            if g3 is not None:
+                ep_tot()
             if j is not None:
                 exp_prod(j, 0)
                 exp_prod(j, 1)
@@ -669,18 +672,16 @@ def tile_sralnet_pa_t_kernel(tc, x, centroids, out):
                 prep_wq()
             if na is not None:
                 q1(na, 0)
-            if g2 is not None:
-                ep_rn1()
+            if g3 is not None:
+                ep_rn2()
             if na is not None:
                 il_v(na, 1, 1)
             if i == -2:
                 prep_b()
-            if g2 is not None:
-                ep_q2()
-            if g3 is not None:
-                ep_scale(g3, 1)
-                ep_store(g3, 0)
-                ep_store(g3, 1)
+            if g4 is not None:
+                ep_scale(g4, 1)
+                ep_store(g4, 0)
+                ep_store(g4, 1)
 
         def finish():
             soft_tiles(end)

@@ -20,8 +20,8 @@ K = 32
 S4 = 4
 EPS = 1e-12
 WV0 = 344
-WVL = 384
-WV = 384
+WVL = 416
+WV = 416
 LNG = 2
 GRP = 4
 LAST = N_IMG // GRP - 1
@@ -568,10 +568,13 @@ def tile_sralnet_pa_t_kernel(tc, x, centroids, out):
                 max_k(n, 0)
             if g3 is not None:
                 ep_rn1()
-            if nz is not None:
-                q1(nz, 1)
             if n is not None:
                 sub_s(n, 0)
+                max_s(n, 1)
+                max_k(n, 1)
+                sub_s(n, 1)
+            if nz is not None:
+                q1(nz, 1)
             for r in range(4):
                 if p is not None:
                     xtr(p, 0, r)
@@ -590,13 +593,9 @@ def tile_sralnet_pa_t_kernel(tc, x, centroids, out):
                 zbt(nz, 1)
             if g1 is not None:
                 ep_part(g1)
-            if n is not None:
-                max_s(n, 1)
-                max_k(n, 1)
             if pl is not None:
                 q2(pl, 1)
             if n is not None:
-                sub_s(n, 1)
                 exp_k(n, 0)
                 exp_k(n, 1)
                 exp_s(n)

@@ -20,8 +20,8 @@ K = 32
 S4 = 4
 EPS = 1e-12
 WV0 = 344
-WVL = 416
-WV = 416
+WG = 32
+WV = 432
 LNG = 2
 GRP = 4
 LAST = N_IMG // GRP - 1
@@ -35,8 +35,8 @@ def tile_sralnet_pa_t_kernel(tc, x, centroids, out):
         ctx.enter_context(tc.manual_schedule())
         const = ctx.enter_context(tc.tile_pool(name="const", bufs=1))
         rawp = ctx.enter_context(tc.tile_pool(name="rawp", bufs=6))
-        g1p = ctx.enter_context(tc.tile_pool(name="g1p", bufs=2))
-        c1p = ctx.enter_context(tc.tile_pool(name="c1p", bufs=3))
+        g1p = ctx.enter_context(tc.tile_pool(name="g1p", bufs=3))
+        c1p = ctx.enter_context(tc.tile_pool(name="c1p", bufs=2))
         g2p = ctx.enter_context(tc.tile_pool(name="g2p", bufs=2))
         c2p = ctx.enter_context(tc.tile_pool(name="c2p", bufs=5))
         zbp = ctx.enter_context(tc.tile_pool(name="zbp", bufs=2))
@@ -45,6 +45,7 @@ def tile_sralnet_pa_t_kernel(tc, x, centroids, out):
         sump = ctx.enter_context(tc.tile_pool(name="sump", bufs=2))
         mfp = ctx.enter_context(tc.tile_pool(name="mfp", bufs=5))
         epi = ctx.enter_context(tc.tile_pool(name="epi", bufs=2))
+        v2p = ctx.enter_context(tc.tile_pool(name="v2p", bufs=2))
         ps_zt = ctx.enter_context(tc.psum_pool(name="ps_zt", bufs=1))
         ps_z = ctx.enter_context(tc.psum_pool(name="ps_z", bufs=2))
         ps_xt = ctx.enter_context(tc.psum_pool(name="ps_xt", bufs=3))
@@ -131,7 +132,7 @@ def tile_sralnet_pa_t_kernel(tc, x, centroids, out):
             )
 
         def prep_norm():
-            junk0 = epi.tile([P, C], BF16, tag="sq", name="junk0")
+            junk0 = v2p.tile([P, C], BF16, tag="sq", name="junk0")
             css = const.tile([P, 1], F32, name="css")
             nc.scalar.activation(out=junk0[:], in_=c_sb[:], func=ACT.Square, accum_out=css[:])
             cn = const.tile([P, 1], F32, name="cn")
@@ -152,16 +153,20 @@ def tile_sralnet_pa_t_kernel(tc, x, centroids, out):
                 ),
             )
 
-        def wv(n):
-            return WV0 if n < 2 else WVL if n % 2 == 0 and n > 2 else WV
-
         def il_v(n, gp, g):
-            regroup(nc.vector.tensor_copy, n, gp, g, 0, wv(n))
+            regroup(nc.vector.tensor_copy, n, gp, g, 0, WV0 if n < 2 else WV)
 
         def il_s(n, gp, g):
-            if wv(n) == 512:
-                return
-            regroup(nc.scalar.copy, n, gp, g, wv(n), 512)
+            if n < 2 or WV + WG < 512:
+                regroup(nc.scalar.copy, n, gp, g, WV0 if n < 2 else WV + WG, 512)
+
+        def il_g(n, gp, g):
+            regroup(copy_g, n, gp, g, WV, WV + WG)
+
+        def copy_g(out, in_):
+            nc.gpsimd.tensor_scalar(
+                out=out, in0=in_, scalar1=1.0, scalar2=0.0, op0=ALU.mult, op1=ALU.add
+            )
 
         def q1(n, gp):
             c1 = c1p.tile([P, 2, 512], U32, tag="c1", name="c1", align_bytes=64)
@@ -282,9 +287,11 @@ def tile_sralnet_pa_t_kernel(tc, x, centroids, out):
                 out=st["sum", n][1], in0=hs[:, 0], in1=hs[:, 1], op=ALU.add
             )
 
-        def sums_beside(n, beside):
-            gate = smp.tile([P, 1], F32, tag="gate", name="gate")
-            nc.gpsimd.tensor_copy(out=gate[:], in_=st["max", beside][1][:, 0, 0:1])
+        def gate(n):
+            first = smp.tile([P, 1], F32, tag="first", name="first")
+            nc.gpsimd.tensor_copy(out=first[:], in_=st["max", n][1][:, 0, 0:1])
+
+        def sums(n):
             e2 = st["e2", n]
             hs = smp.tile([P, 2, 8, K], F32, tag="hs", name="hs")
             nc.gpsimd.tensor_tensor(out=hs[:], in0=e2[:, 0:2], in1=e2[:, 2:4], op=ALU.add)
@@ -293,6 +300,9 @@ def tile_sralnet_pa_t_kernel(tc, x, centroids, out):
         def log_sums(lg):
             flat = st["sums", lg][:].rearrange("q i c -> q (i c)")
             nc.scalar.activation(out=flat, in_=flat, func=ACT.Ln)
+
+        def load_exp():
+            nc.scalar.activation(out=warm2[:], in_=warm[:], func=ACT.Exp)
 
         def log_sum_exps(lg):
             flat = st["sums", lg][:].rearrange("q i c -> q (i c)")
@@ -329,9 +339,11 @@ def tile_sralnet_pa_t_kernel(tc, x, centroids, out):
                         scale=1.0,
                     )
 
-        def plus_one(n):
+        def plus_one(n, engine=nc.vector):
             hi = st["d", n][:, 2:4].rearrange("q s t k -> q (s t k)")
-            nc.vector.tensor_scalar_add(out=hi, in0=hi, scalar1=1.0)
+            engine.tensor_scalar(
+                out=hi, in0=hi, scalar1=1.0, scalar2=1.0, op0=ALU.mult, op1=ALU.add
+            )
 
         def pair_mult(n):
             lo = st["d", n][:, 0:2].rearrange("q s t k -> q (s t k)")
@@ -377,9 +389,9 @@ def tile_sralnet_pa_t_kernel(tc, x, centroids, out):
                         xt[:, rl, u, :], raw_w[:, 2 * rp + rl, P * u : P * u + P], ident_f[:]
                     )
 
-        def xev(n, gp, rp):
+        def xev(n, gp, rp, copy=nc.scalar.copy):
             g2w = st["g2", n, gp][:].bitcast(F32).rearrange("q (c u) -> q c u", u=2)
-            nc.scalar.copy(
+            copy(
                 out=g2w[:, 256 * rp : 256 * rp + 256, :].rearrange("q (rl p) u -> q rl p u", rl=2),
                 in_=st["xt", n, gp, rp][:].rearrange("q rl u p -> q rl p u"),
             )
@@ -455,7 +467,7 @@ def tile_sralnet_pa_t_kernel(tc, x, centroids, out):
 
         def ep_v2(grp, hc):
             if hc == 0:
-                st["v2", grp] = epi.tile([P, C], F32, tag="v2", name="v2")
+                st["v2", grp] = v2p.tile([P, C], F32, tag="v2", name="v2")
             nc.vector.scalar_tensor_tensor(
                 out=st["v2", grp][:, 512 * hc : 512 * hc + 512],
                 in0=rep4[:, 512 * hc : 512 * hc + 512],
@@ -467,7 +479,7 @@ def tile_sralnet_pa_t_kernel(tc, x, centroids, out):
 
         def ep_sq(grp, hc):
             if hc == 0:
-                st["sq"] = epi.tile([P, C], BF16, tag="sq", name="sq")
+                st["sq"] = v2p.tile([P, C], BF16, tag="sq", name="sq")
                 st["ss"] = epi.tile([P, 2], F32, tag="ss", name="ss")
             half_c = slice(512 * hc, 512 * hc + 512)
             nc.scalar.activation(
@@ -478,9 +490,9 @@ def tile_sralnet_pa_t_kernel(tc, x, centroids, out):
             )
 
         def ep_rn1():
-            ssc = epi.tile([P, 1], F32, tag="ssc", name="ssc")
+            st["ssc"] = epi.tile([P, 1], F32, tag="ssc", name="ssc")
             nc.vector.tensor_scalar(
-                out=ssc[:],
+                out=st["ssc"][:],
                 in0=st["ss"][:, 0:1],
                 scalar1=st["ss"][:, 1:2],
                 scalar2=EPS * EPS,
@@ -488,21 +500,21 @@ def tile_sralnet_pa_t_kernel(tc, x, centroids, out):
                 op1=ALU.max,
             )
             st["rn1"] = epi.tile([P, 1], F32, tag="rn1", name="rn1")
-            nc.gpsimd.tensor_tensor(out=st["rn1"][:], in0=ssc[:], in1=mhalf[:], op=ALU.pow)
-            st["sst"] = epi.tile([P, 1], F32, tag="sst", name="sst")
-            nc.vector.tensor_tensor(
-                out=st["sst"][:], in0=st["ss"][:, 0:1], in1=st["ss"][:, 1:2], op=ALU.add
-            )
+            nc.gpsimd.tensor_tensor(out=st["rn1"][:], in0=st["ssc"][:], in1=mhalf[:], op=ALU.pow)
 
         def ep_q2():
+            st["sst"] = epi.tile([P, 2], F32, tag="sst", name="sst")
+            nc.vector.tensor_tensor(
+                out=st["sst"][:],
+                in0=st["ss"][:, 0:1].to_broadcast([P, 2]),
+                in1=st["ss"][:, 1:2].to_broadcast([P, 2]),
+                op=ALU.add,
+            )
+            inv = epi.tile([P, 1], F32, tag="inv", name="inv")
+            nc.vector.reciprocal(out=inv[:], in_=st["ssc"][:])
             st["q2"] = epi.tile([P, 2], F32, tag="q2", name="q2")
-            nc.vector.tensor_scalar(
-                out=st["q2"][:],
-                in0=st["sst"][:, 0:1].to_broadcast([P, 2]),
-                scalar1=st["rn1"][:, 0:1],
-                scalar2=st["rn1"][:, 0:1],
-                op0=ALU.mult,
-                op1=ALU.mult,
+            nc.vector.tensor_scalar_mul(
+                out=st["q2"][:], in0=st["sst"][:], scalar1=inv[:, 0:1]
             )
 
         def ep_tot():
@@ -558,13 +570,19 @@ def tile_sralnet_pa_t_kernel(tc, x, centroids, out):
                 soft_tiles(n)
             if na is not None:
                 g1_tile(na, 0)
+                g1_tile(na, 1)
             if p is not None:
                 g2_tile(p, 0)
 
             if n is not None:
                 max_s(n, 0)
+                gate(n)
                 if n > 0:
-                    sums_beside(n - 1, n)
+                    sums(n - 1)
+                if na is not None:
+                    for gp in range(2):
+                        for g in range(2):
+                            il_g(na, gp, g)
                 max_k(n, 0)
             if g3 is not None:
                 ep_rn1()
@@ -618,8 +636,6 @@ def tile_sralnet_pa_t_kernel(tc, x, centroids, out):
                 prep_norm()
                 prep_w()
 
-            if na is not None:
-                g1_tile(na, 1)
             if lg is not None:
                 log_sum_exps(lg)
             if jt is not None:
@@ -687,7 +703,8 @@ def tile_sralnet_pa_t_kernel(tc, x, centroids, out):
             g2_tile(end, 1)
             ep_part(LAST - 1)
             max_s(end, 0)
-            sums_beside(end - 1, end)
+            gate(end)
+            sums(end - 1)
             max_k(end, 0)
             max_s(end, 1)
             max_k(end, 1)
@@ -709,57 +726,59 @@ def tile_sralnet_pa_t_kernel(tc, x, centroids, out):
             round_mult(end - 3)
             sum_s(end)
             log_sums(end // LNG)
+            load_exp()
             ep_v2(LAST - 1, 0)
             ep_v2(LAST - 1, 1)
+            ep_sq(LAST - 1, 0)
+            ep_sq(LAST - 1, 1)
             qm(end - 3)
-            plus_one(end - 2)
             for r in range(3):
                 xtr(end, 1, r)
             vmm(end - 3)
-            ep_sq(LAST - 1, 0)
-            ep_sq(LAST - 1, 1)
+            plus_one(end - 2)
             for r in range(3):
-                xev(end, 1, r)
+                xev(end, 1, r, nc.vector.tensor_copy)
             log_sum_exps(end // LNG)
             pair_mult(end - 2)
             log_prod(end - 1)
-            ep_rn1()
-            mult(end - 2)
             log_prod(end)
             exp_prod(end - 1, 0)
             exp_prod(end - 1, 1)
-            ep_q2()
-            round_mult(end - 2)
-            xtr(end, 1, 3)
-            xev(end, 1, 3)
             exp_prod(end, 0)
             exp_prod(end, 1)
-            ep_tot()
+            xtr(end, 1, 3)
+            mult(end - 2)
+            ep_rn1()
+            xev(end, 1, 3, nc.vector.tensor_copy)
+            round_mult(end - 2)
+            ep_part(LAST, range(GRP - 2))
+            plus_one(end - 1)
             qm(end - 2)
             vmm(end - 2)
-            ep_rn2()
-            plus_one(end - 1)
+            ep_q2()
             pair_mult(end - 1)
+            ep_tot()
             q2(end, 1)
             mult(end - 1)
-            ep_part(LAST, range(GRP - 1))
             plus_one(end)
             round_mult(end - 1)
+            ep_part(LAST, [GRP - 2])
             pair_mult(end)
             qm(end - 1)
+            ep_rn2()
             mult(end)
             ep_part(LAST, [GRP - 1])
-            vmm(end - 1)
             ep_scale(LAST - 1, 0)
-            round_mult(end)
             ep_spread()
             ep_msum()
+            round_mult(end)
+            vmm(end - 1)
+            ep_scale(LAST - 1, 1)
             qm(end)
             vmm(end)
-            ep_scale(LAST - 1, 1)
-            ep_store(LAST - 1, 0)
-            ep_store(LAST - 1, 1)
             ep_neg()
+            for hc in range(2):
+                ep_store(LAST - 1, hc)
             for hc in range(2):
                 ep_v2(LAST, hc)
                 ep_sq(LAST, hc)

@@ -20,7 +20,7 @@ K = 32
 S4 = 4
 EPS = 1e-12
 WV0 = 344
-WG = 32
+WG = 0
 WV = 432
 LNG = 2
 GRP = 4
@@ -35,7 +35,7 @@ def tile_sralnet_pa_t_kernel(tc, x, centroids, out):
         ctx.enter_context(tc.manual_schedule())
         const = ctx.enter_context(tc.tile_pool(name="const", bufs=1))
         rawp = ctx.enter_context(tc.tile_pool(name="rawp", bufs=6))
-        g1p = ctx.enter_context(tc.tile_pool(name="g1p", bufs=3))
+        g1p = ctx.enter_context(tc.tile_pool(name="g1p", bufs=2))
         c1p = ctx.enter_context(tc.tile_pool(name="c1p", bufs=2))
         g2p = ctx.enter_context(tc.tile_pool(name="g2p", bufs=2))
         c2p = ctx.enter_context(tc.tile_pool(name="c2p", bufs=5))
@@ -288,8 +288,8 @@ def tile_sralnet_pa_t_kernel(tc, x, centroids, out):
             )
 
         def gate(n):
-            first = smp.tile([P, 1], F32, tag="first", name="first")
-            nc.gpsimd.tensor_copy(out=first[:], in_=st["max", n][1][:, 0, 0:1])
+            first = smp.tile([P, 1], BF16, tag="first", name="first")
+            nc.gpsimd.tensor_copy(out=first[:], in_=st["g1", n + 1, 1][:, 1, 0, 0:1])
 
         def sums(n):
             e2 = st["e2", n]
@@ -339,11 +339,9 @@ def tile_sralnet_pa_t_kernel(tc, x, centroids, out):
                         scale=1.0,
                     )
 
-        def plus_one(n, engine=nc.vector):
+        def plus_one(n):
             hi = st["d", n][:, 2:4].rearrange("q s t k -> q (s t k)")
-            engine.tensor_scalar(
-                out=hi, in0=hi, scalar1=1.0, scalar2=1.0, op0=ALU.mult, op1=ALU.add
-            )
+            nc.vector.tensor_scalar_add(out=hi, in0=hi, scalar1=1.0)
 
         def pair_mult(n):
             lo = st["d", n][:, 0:2].rearrange("q s t k -> q (s t k)")
@@ -576,13 +574,9 @@ def tile_sralnet_pa_t_kernel(tc, x, centroids, out):
 
             if n is not None:
                 max_s(n, 0)
-                gate(n)
                 if n > 0:
+                    gate(n)
                     sums(n - 1)
-                if na is not None:
-                    for gp in range(2):
-                        for g in range(2):
-                            il_g(na, gp, g)
                 max_k(n, 0)
             if g3 is not None:
                 ep_rn1()
@@ -703,7 +697,6 @@ def tile_sralnet_pa_t_kernel(tc, x, centroids, out):
             g2_tile(end, 1)
             ep_part(LAST - 1)
             max_s(end, 0)
-            gate(end)
             sums(end - 1)
             max_k(end, 0)
             max_s(end, 1)

@@ -20,8 +20,8 @@ K = 32
 S4 = 4
 EPS = 1e-12
 WV0 = 344
-WG = 0
-WV = 432
+WVL = 440
+WV = 440
 LNG = 2
 GRP = 4
 LAST = N_IMG // GRP - 1
@@ -153,20 +153,15 @@ def tile_sralnet_pa_t_kernel(tc, x, centroids, out):
                 ),
             )
 
+        def wv(n):
+            return WV0 if n < 2 else WVL if n % LNG == 0 else WV
+
         def il_v(n, gp, g):
-            regroup(nc.vector.tensor_copy, n, gp, g, 0, WV0 if n < 2 else WV)
+            regroup(nc.vector.tensor_copy, n, gp, g, 0, wv(n))
 
         def il_s(n, gp, g):
-            if n < 2 or WV + WG < 512:
-                regroup(nc.scalar.copy, n, gp, g, WV0 if n < 2 else WV + WG, 512)
-
-        def il_g(n, gp, g):
-            regroup(copy_g, n, gp, g, WV, WV + WG)
-
-        def copy_g(out, in_):
-            nc.gpsimd.tensor_scalar(
-                out=out, in0=in_, scalar1=1.0, scalar2=0.0, op0=ALU.mult, op1=ALU.add
-            )
+            if wv(n) < 512:
+                regroup(nc.scalar.copy, n, gp, g, wv(n), 512)
 
         def q1(n, gp):
             c1 = c1p.tile([P, 2, 512], U32, tag="c1", name="c1", align_bytes=64)
@@ -339,39 +334,53 @@ def tile_sralnet_pa_t_kernel(tc, x, centroids, out):
                         scale=1.0,
                     )
 
-        def plus_one(n):
-            hi = st["d", n][:, 2:4].rearrange("q s t k -> q (s t k)")
-            nc.vector.tensor_scalar_add(out=hi, in0=hi, scalar1=1.0)
-
-        def pair_mult(n):
-            lo = st["d", n][:, 0:2].rearrange("q s t k -> q (s t k)")
-            hi = st["d", n][:, 2:4].rearrange("q s t k -> q (s t k)")
-            nc.vector.scalar_tensor_tensor(
-                out=lo, in0=lo, scalar=1.0, in1=hi, op0=ALU.add, op1=ALU.mult
-            )
-
-        def mult(n):
+        def low_high(n, half):
             a = st["d", n]
-            st["multf", n] = mfp.tile([P, 8, K], F32, tag="multf", name="multf")
+            ts = slice(0, 8) if half is None else slice(4 * half, 4 * half + 4)
+            return tuple(
+                a[:, s : s + 2, ts, :].rearrange("q s t k -> q s (t k)") for s in (0, 2)
+            )
+
+        def plus_one(n, half=None):
+            low, high = low_high(n, half)
+            nc.vector.tensor_scalar_add(out=high, in0=high, scalar1=1.0)
+
+        def pair_mult(n, half=None):
+            low, high = low_high(n, half)
+            nc.vector.scalar_tensor_tensor(
+                out=low, in0=low, scalar=1.0, in1=high, op0=ALU.add, op1=ALU.mult
+            )
+
+        def mult(n, half=None):
+            a = st["d", n]
+            if half != 1:
+                st["multf", n] = mfp.tile([P, 8, K], F32, tag="multf", name="multf")
+            ts = slice(0, 8) if half is None else slice(4 * half, 4 * half + 4)
             nc.vector.tensor_tensor(
-                out=st["multf", n][:], in0=a[:, 0], in1=a[:, 1], op=ALU.mult
+                out=st["multf", n][:, ts, :], in0=a[:, 0, ts, :], in1=a[:, 1, ts, :], op=ALU.mult
             )
 
-        def round_mult(n):
+        def round_mult(n, half=None):
             i = n % GRP
+            gs = slice(0, 2) if half is None else slice(half, half + 1)
+            ts = slice(0, 8) if half is None else slice(4 * half, 4 * half + 4)
             nc.vector.tensor_copy(
-                out=mb[i][:, :, K * i : K * i + K, :],
-                in_=st["multf", n][:].rearrange("q (g t) k -> q g k t", g=2),
+                out=mb[i][:, gs, K * i : K * i + K, :],
+                in_=st["multf", n][:, ts, :].rearrange("q (g t) k -> q g k t", t=4),
             )
 
-        def qm(n):
-            mc = smp.tile([P, 2 * P], U32, tag="mc", name="mc", align_bytes=64)
-            msc = smp.tile([P, 2 * P], U8, tag="msc", name="msc", align_bytes=64)
-            st["m", n] = (mc, msc)
+        def qm(n, half=None):
+            if half != 1:
+                mc = smp.tile([P, 2 * P], U32, tag="mc", name="mc", align_bytes=64)
+                msc = smp.tile([P, 2 * P], U8, tag="msc", name="msc", align_bytes=64)
+                st["m", n] = (mc, msc)
+            mc, msc = st["m", n]
+            gs = slice(0, 2) if half is None else slice(half, half + 1)
+            cols = slice(0, 2 * P) if half is None else slice(P * half, P * half + P)
             nc.vector.quantize_mx(
-                out=mc[:].bitcast(FP8X4),
-                scales=msc[:],
-                in_=mb[n % GRP][:].rearrange("q g c t -> q (g c t)"),
+                out=mc[:, cols].bitcast(FP8X4),
+                scales=msc[:, cols],
+                in_=mb[n % GRP][:, gs].rearrange("q g c t -> q (g c t)"),
             )
 
         def g2_tile(n, gp):
@@ -404,7 +413,7 @@ def tile_sralnet_pa_t_kernel(tc, x, centroids, out):
                 out=c2[:, gp, :].bitcast(FP8X4), scales=s2x[:, gp, :], in_=st["g2", n, gp][:]
             )
 
-        def vmm(n):
+        def vmm(n, halves=(0, 1)):
             i = n % GRP
             if i == 0:
                 st["v"] = [
@@ -412,8 +421,8 @@ def tile_sralnet_pa_t_kernel(tc, x, centroids, out):
                 ]
             mc, msc = st["m", n]
             c2, s2x = st["c2", n]
-            for hc in range(2):
-                for gp in range(2):
+            for gp in halves:
+                for hc in range(2):
                     nc.tensor.matmul_mx(
                         out=st["v"][hc][:],
                         lhsT=mc[:, P * gp : P * gp + P].bitcast(FP8X4),
@@ -600,15 +609,16 @@ def tile_sralnet_pa_t_kernel(tc, x, centroids, out):
                     log_sums(lg)
                 if r == 2 and nz is not None:
                     zbt(nz, 0)
-            if nz == end:
-                zmm(nz, 1)
-                zbt(nz, 1)
             if g1 is not None:
                 ep_part(g1)
             if pl is not None:
                 q2(pl, 1)
             if n is not None:
                 exp_k(n, 0)
+            if nz == end:
+                zmm(nz, 1)
+                zbt(nz, 1)
+            if n is not None:
                 exp_k(n, 1)
                 exp_s(n)
             if jt is not None:
@@ -715,22 +725,25 @@ def tile_sralnet_pa_t_kernel(tc, x, centroids, out):
             exp_prod(end - 2, 0)
             exp_prod(end - 2, 1)
             mult(end - 3)
+            for r in range(3):
+                xtr(end, 1, r)
+            for r in range(3):
+                xev(end, 1, r, nc.vector.tensor_copy)
             half_sum(end)
             round_mult(end - 3)
             sum_s(end)
             log_sums(end // LNG)
             load_exp()
+            xtr(end, 1, 3)
             ep_v2(LAST - 1, 0)
             ep_v2(LAST - 1, 1)
             ep_sq(LAST - 1, 0)
             ep_sq(LAST - 1, 1)
+            xev(end, 1, 3, nc.vector.tensor_copy)
             qm(end - 3)
-            for r in range(3):
-                xtr(end, 1, r)
             vmm(end - 3)
+            q2(end, 1)
             plus_one(end - 2)
-            for r in range(3):
-                xev(end, 1, r, nc.vector.tensor_copy)
             log_sum_exps(end // LNG)
             pair_mult(end - 2)
             log_prod(end - 1)
@@ -739,39 +752,50 @@ def tile_sralnet_pa_t_kernel(tc, x, centroids, out):
             exp_prod(end - 1, 1)
             exp_prod(end, 0)
             exp_prod(end, 1)
-            xtr(end, 1, 3)
             mult(end - 2)
             ep_rn1()
-            xev(end, 1, 3, nc.vector.tensor_copy)
+            ep_q2()
             round_mult(end - 2)
-            ep_part(LAST, range(GRP - 2))
             plus_one(end - 1)
             qm(end - 2)
+            dummy = ps_xt.tile([P, 512], F32, tag="xt", name="dummy")
+            for g in range(12):
+                nc.tensor.matmul(
+                    out=dummy[:],
+                    lhsT=ident_b[:],
+                    rhs=st["wg"][:, g % 2].rearrange("p m j -> p (m j)"),
+                    start=True,
+                    stop=True,
+                )
             vmm(end - 2)
-            ep_q2()
-            pair_mult(end - 1)
             ep_tot()
-            q2(end, 1)
+            pair_mult(end - 1)
+            plus_one(end, 0)
             mult(end - 1)
-            plus_one(end)
+            pair_mult(end, 0)
             round_mult(end - 1)
-            ep_part(LAST, [GRP - 2])
-            pair_mult(end)
+            plus_one(end, 1)
             qm(end - 1)
             ep_rn2()
-            mult(end)
-            ep_part(LAST, [GRP - 1])
+            ep_part(LAST, range(GRP - 2))
+            vmm(end - 1)
+            mult(end, 0)
+            pair_mult(end, 1)
+            round_mult(end, 0)
+            mult(end, 1)
+            ep_part(LAST, range(GRP - 2, GRP))
+            qm(end, 0)
+            vmm(end, (0,))
+            round_mult(end, 1)
             ep_scale(LAST - 1, 0)
+            qm(end, 1)
             ep_spread()
             ep_msum()
-            round_mult(end)
-            vmm(end - 1)
+            vmm(end, (1,))
             ep_scale(LAST - 1, 1)
-            qm(end)
-            vmm(end)
+            ep_store(LAST - 1, 0)
+            ep_store(LAST - 1, 1)
             ep_neg()
-            for hc in range(2):
-                ep_store(LAST - 1, hc)
             for hc in range(2):
                 ep_v2(LAST, hc)
                 ep_sq(LAST, hc)

@@ -20,8 +20,8 @@ K = 32
 S4 = 4
 EPS = 1e-12
 WV0 = 344
-WVL = 440
-WV = 440
+WVL = 460
+WV = 460
 LNG = 2
 GRP = 4
 LAST = N_IMG // GRP - 1
@@ -341,9 +341,11 @@ def tile_sralnet_pa_t_kernel(tc, x, centroids, out):
                 a[:, s : s + 2, ts, :].rearrange("q s t k -> q s (t k)") for s in (0, 2)
             )
 
-        def plus_one(n, half=None):
+        def plus_one(n, half=None, engine=nc.vector):
             low, high = low_high(n, half)
-            nc.vector.tensor_scalar_add(out=high, in0=high, scalar1=1.0)
+            engine.tensor_scalar(
+                out=high, in0=high, scalar1=1.0, scalar2=1.0, op0=ALU.mult, op1=ALU.add
+            )
 
         def pair_mult(n, half=None):
             low, high = low_high(n, half)
@@ -586,9 +588,13 @@ def tile_sralnet_pa_t_kernel(tc, x, centroids, out):
                 if n > 0:
                     gate(n)
                     sums(n - 1)
+                if jt is not None:
+                    plus_one(jt, engine=nc.gpsimd)
                 max_k(n, 0)
             if g3 is not None:
                 ep_rn1()
+            if g4 is not None:
+                ep_rn2()
             if n is not None:
                 sub_s(n, 0)
                 max_s(n, 1)
@@ -621,8 +627,6 @@ def tile_sralnet_pa_t_kernel(tc, x, centroids, out):
             if n is not None:
                 exp_k(n, 1)
                 exp_s(n)
-            if jt is not None:
-                plus_one(jt)
             if na is not None:
                 il_v(na, 0, 0)
             if g1 is not None:
@@ -691,8 +695,6 @@ def tile_sralnet_pa_t_kernel(tc, x, centroids, out):
                 prep_wq()
             if na is not None:
                 q1(na, 0)
-            if g3 is not None:
-                ep_rn2()
             if na is not None:
                 il_v(na, 1, 1)
             if i == -2:

from contextlib import ExitStack

import concourse.mybir as mybir
from concourse.masks import make_identity

F32 = mybir.dt.float32
BF16 = mybir.dt.bfloat16
U32 = mybir.dt.uint32
U8 = mybir.dt.uint8
FP8X4 = mybir.dt.float8_e4m3fn_x4
ALU = mybir.AluOpType
ACT = mybir.ActivationFunctionType
AX = mybir.AxisListType

P = 128
N_IMG = 16
C = 1024
PIX = 1024
K = 32
S4 = 4
EPS = 1e-12
WV0 = 344
WVL = 460
WV = 460
LNG = 2
GRP = 4
LAST = N_IMG // GRP - 1

FLOPS = 2 * N_IMG * C * PIX * (K * S4) + 2 * N_IMG * K * PIX * C


def tile_sralnet_pa_t_kernel(tc, x, centroids, out):
    nc = tc.nc
    with ExitStack() as ctx:
        ctx.enter_context(tc.manual_schedule())
        const = ctx.enter_context(tc.tile_pool(name="const", bufs=1))
        rawp = ctx.enter_context(tc.tile_pool(name="rawp", bufs=6))
        g1p = ctx.enter_context(tc.tile_pool(name="g1p", bufs=2))
        c1p = ctx.enter_context(tc.tile_pool(name="c1p", bufs=2))
        g2p = ctx.enter_context(tc.tile_pool(name="g2p", bufs=2))
        c2p = ctx.enter_context(tc.tile_pool(name="c2p", bufs=5))
        zbp = ctx.enter_context(tc.tile_pool(name="zbp", bufs=2))
        smp = ctx.enter_context(tc.tile_pool(name="smp", bufs=2))
        dp = ctx.enter_context(tc.tile_pool(name="dp", bufs=4))
        sump = ctx.enter_context(tc.tile_pool(name="sump", bufs=2))
        mfp = ctx.enter_context(tc.tile_pool(name="mfp", bufs=5))
        epi = ctx.enter_context(tc.tile_pool(name="epi", bufs=2))
        v2p = ctx.enter_context(tc.tile_pool(name="v2p", bufs=2))
        ps_zt = ctx.enter_context(tc.psum_pool(name="ps_zt", bufs=1))
        ps_z = ctx.enter_context(tc.psum_pool(name="ps_z", bufs=2))
        ps_xt = ctx.enter_context(tc.psum_pool(name="ps_xt", bufs=3))
        ps_v = ctx.enter_context(tc.psum_pool(name="ps_v", bufs=1))

        st = {}

        def load(n, gp):
            raw = rawp.tile([P, 8, 512], BF16, tag="raw", name="raw")
            st["raw", n, gp] = raw
            nc.sync.dma_start(
                out=raw[:],
                in_=x[n, :, 16 * gp : 16 * gp + 16, :].rearrange("(r p) h w -> p r (h w)", p=P),
            )

        def load_first():
            raw = rawp.tile([P, 8, 512], BF16, tag="raw", name="raw")
            st["raw", 0, 0] = raw
            for g in range(2):
                nc.sync.dma_start(
                    out=raw[:, 4 * g : 4 * g + 4, :],
                    in_=x[0, 512 * g : 512 * g + 512, 0:16, :].rearrange(
                        "(r p) h w -> p r (h w)", p=P
                    ),
                )

        load_first()
        c_sb = const.tile([P, C], BF16, name="c_sb")
        for s in range(S4):
            nc.sync.dma_start(out=c_sb[32 * s : 32 * s + 32, :], in_=centroids[:, s, :])
        load(0, 1)
        load(1, 0)
        load(1, 1)
        rep4 = const.tile([P, C], BF16, name="rep4")
        for i in range(4):
            nc.sync.dma_start(out=rep4[32 * i : 32 * i + 32, :], in_=centroids[:, 0, :])

        warm = const.tile([P, 1], F32, name="warm")
        nc.vector.memset(warm[:], 0.0)
        warm2 = const.tile([P, 1], F32, name="warm2")
        nc.scalar.activation(out=warm2[:], in_=warm[:], func=ACT.Exp)

        ident_b = const.tile([P, P], BF16, name="ident_b")
        make_identity(nc, ident_b[:])
        ident_f = const.tile([P, P], F32, name="ident_f")
        make_identity(nc, ident_f[:])
        half = const.tile([P, 1], F32, name="half")
        nc.vector.memset(half[:], 0.5)
        ones2 = const.tile([P, 2], F32, name="ones2")
        nc.vector.memset(ones2[:], 1.0)
        mhalf = const.tile([P, 1], F32, name="mhalf")
        nc.vector.memset(mhalf[:], -0.5)
        bd = const.tile([P, P], F32, name="bd")
        nc.vector.memset(bd[:], 0.0)
        for i in range(4):
            nc.vector.memset(bd[32 * i : 32 * i + 32, 32 * i : 32 * i + 32], 1.0)
        mb = [const.tile([P, 2, P, 4], BF16, name="mb%d" % i, align_bytes=64) for i in range(4)]
        for i in range(4):
            nc.vector.memset(mb[i][:], 0.0)
        sel = const.tile([P, K], F32, name="sel")
        nc.vector.tensor_reduce(
            out=sel[:], in_=ident_f[:].rearrange("p (b k) -> p k b", k=K), axis=AX.X, op=ALU.add
        )

        w_codes = const.tile([P, 2 * P], U32, name="w_codes", align_bytes=64)
        w_scales = const.tile([P, 2 * P], U8, name="w_scales", align_bytes=64)
        bvec = const.tile([P, 1], F32, name="bvec")

        def prep_w():
            pt = ps_xt.tile([P, 8, P], BF16, tag="xt", name="pt")
            for r in range(8):
                nc.tensor.transpose(pt[:, r, :], c_sb[:, P * r : P * r + P], ident_b[:])
            wg = const.tile([P, 2, P, 4], BF16, name="wg", align_bytes=64)
            nc.vector.tensor_scalar_mul(
                out=wg[:], in0=pt[:].rearrange("p (g j) m -> p g m j", j=4), scalar1=200.0
            )
            st["wg"] = wg

        def prep_wq():
            nc.vector.quantize_mx(
                out=w_codes[:].bitcast(FP8X4),
                scales=w_scales[:],
                in_=st["wg"][:].rearrange("p g m j -> p (g m j)"),
            )

        def prep_norm():
            junk0 = v2p.tile([P, C], BF16, tag="sq", name="junk0")
            css = const.tile([P, 1], F32, name="css")
            nc.scalar.activation(out=junk0[:], in_=c_sb[:], func=ACT.Square, accum_out=css[:])
            cn = const.tile([P, 1], F32, name="cn")
            nc.gpsimd.tensor_tensor(out=cn[:], in0=css[:], in1=half[:], op=ALU.pow)
            st["cn"] = cn

        def prep_b():
            nc.vector.tensor_scalar_mul(out=bvec[:], in0=st["cn"][:], scalar1=-100.0)

        def g1_tile(n, gp):
            st["g1", n, gp] = g1p.tile([P, 2, 512, 4], BF16, tag="g1", name="g1", align_bytes=64)

        def regroup(copy, n, gp, g, w0, w1):
            copy(
                out=st["g1", n, gp][:, g, w0:w1, :].rearrange("p (c i) t -> p c t i", i=4),
                in_=st["raw", n, gp][:, 4 * g : 4 * g + 4, w0:w1].rearrange(
                    "p t (c i) -> p c t i", i=4
                ),
            )

        def wv(n):
            return WV0 if n < 2 else WVL if n % LNG == 0 else WV

        def il_v(n, gp, g):
            regroup(nc.vector.tensor_copy, n, gp, g, 0, wv(n))

        def il_s(n, gp, g):
            if wv(n) < 512:
                regroup(nc.scalar.copy, n, gp, g, wv(n), 512)

        def q1(n, gp):
            c1 = c1p.tile([P, 2, 512], U32, tag="c1", name="c1", align_bytes=64)
            s1x = c1p.tile([P, 2, 512], U8, tag="s1x", name="s1x", align_bytes=64)
            st["c1", n, gp] = (c1, s1x)
            nc.vector.quantize_mx(
                out=c1[:].rearrange("p g w -> p (g w)").bitcast(FP8X4),
                scales=s1x[:].rearrange("p g w -> p (g w)"),
                in_=st["g1", n, gp][:].rearrange("p g w j -> p (g w j)"),
            )

        def zmm(n, gp):
            zt = ps_zt.tile([P, 512], F32, tag="zT", name="zt")
            st["zt", n, gp] = zt
            c1, s1x = st["c1", n, gp]
            for g in range(2):
                nc.tensor.matmul_mx(
                    out=zt[:],
                    lhsT=w_codes[:, P * g : P * g + P].bitcast(FP8X4),
                    lhsT_scale=w_scales[:, P * g : P * g + P],
                    rhs=c1[:, g, :].bitcast(FP8X4),
                    rhs_scale=s1x[:, g, :],
                    start=(g == 0),
                    stop=(g == 1),
                )

        def zbt(n, gp):
            if gp == 0:
                st["zb", n] = zbp.tile([P, PIX], F32, tag="zb", name="zb")
            nc.scalar.activation(
                out=st["zb", n][:, 512 * gp : 512 * gp + 512],
                in_=st["zt", n, gp][:],
                func=ACT.Identity,
                bias=bvec[:, 0:1],
                scale=1.0,
            )

        def ztr(n, gp):
            zp = ps_z.tile([P, 4, S4, K], F32, tag="z", name="zp")
            st["z", n, gp] = zp
            for u in range(2):
                for e in range(2):
                    wb = 2 * gp + u
                    nc.tensor.transpose(
                        zp[:, 2 * u + e].rearrange("q s k -> q (s k)"),
                        st["zb", n][:, 256 * wb + e : 256 * wb + 256 : 2],
                        ident_f[:],
                    )

        def over_k_and_s(tile, i):
            return (
                tile[:, i, 0 : 8 * S4].rearrange("q (t s) -> q t s", s=S4),
                tile[:, i, 8 * S4 :].rearrange("q (t k) -> q t k", k=K),
            )

        def soft_tiles(n):
            st["d", n] = dp.tile([P, S4, 8, K], F32, tag="d", name="d")
            st["e1", n] = smp.tile([P, 8, S4, K], BF16, tag="e1", name="e1")
            st["e2", n] = smp.tile([P, S4, 8, K], F32, tag="e2", name="e2")
            lg, i = divmod(n, LNG)
            if i == 0:
                for name in ("sums", "maxes"):
                    st[name, lg] = sump.tile([P, LNG, 8 * S4 + 8 * K], F32, tag=name, name=name)
            st["sum", n] = over_k_and_s(st["sums", lg], i)
            st["max", n] = over_k_and_s(st["maxes", lg], i)

        def max_s(n, gp):
            nc.vector.tensor_reduce(
                out=st["max", n][1][:, 4 * gp : 4 * gp + 4, :],
                in_=st["z", n, gp][:].rearrange("q t s k -> q t k s"),
                axis=AX.X,
                op=ALU.max,
            )

        def max_k(n, gp):
            nc.vector.tensor_reduce(
                out=st["max", n][0][:, 4 * gp : 4 * gp + 4, :],
                in_=st["z", n, gp][:],
                axis=AX.X,
                op=ALU.max,
                negate=True,
            )

        def sub_s(n, gp):
            ts = slice(4 * gp, 4 * gp + 4)
            nc.vector.tensor_tensor(
                out=st["d", n][:, :, ts, :].rearrange("q s t k -> q t s k"),
                in0=st["z", n, gp][:],
                in1=st["max", n][1][:, ts, :].unsqueeze(2).to_broadcast([P, 4, S4, K]),
                op=ALU.subtract,
            )

        def exp_k(n, gp):
            for t in range(4 * gp, 4 * gp + 4):
                for s in range(S4):
                    nc.scalar.activation(
                        out=st["e1", n][:, t, s, :],
                        in_=st["z", n, gp][:, t % 4, s, :],
                        func=ACT.Exp,
                        bias=st["max", n][0][:, t, s : s + 1],
                        scale=1.0,
                        accum_out=st["sum", n][0][:, t, s : s + 1],
                    )

        def exp_s(n):
            nc.scalar.activation(out=st["e2", n][:], in_=st["d", n][:], func=ACT.Exp)

        def half_sum(n):
            e2 = st["e2", n]
            st["hs", n] = smp.tile([P, 2, 8, K], F32, tag="hs", name="hs")
            nc.vector.tensor_tensor(
                out=st["hs", n][:], in0=e2[:, 0:2], in1=e2[:, 2:4], op=ALU.add
            )

        def sum_s(n):
            hs = st["hs", n]
            nc.vector.tensor_tensor(
                out=st["sum", n][1], in0=hs[:, 0], in1=hs[:, 1], op=ALU.add
            )

        def gate(n):
            first = smp.tile([P, 1], BF16, tag="first", name="first")
            nc.gpsimd.tensor_copy(out=first[:], in_=st["g1", n + 1, 1][:, 1, 0, 0:1])

        def sums(n):
            e2 = st["e2", n]
            hs = smp.tile([P, 2, 8, K], F32, tag="hs", name="hs")
            nc.gpsimd.tensor_tensor(out=hs[:], in0=e2[:, 0:2], in1=e2[:, 2:4], op=ALU.add)
            nc.gpsimd.tensor_tensor(out=st["sum", n][1], in0=hs[:, 0], in1=hs[:, 1], op=ALU.add)

        def log_sums(lg):
            flat = st["sums", lg][:].rearrange("q i c -> q (i c)")
            nc.scalar.activation(out=flat, in_=flat, func=ACT.Ln)

        def load_exp():
            nc.scalar.activation(out=warm2[:], in_=warm[:], func=ACT.Exp)

        def log_sum_exps(lg):
            flat = st["sums", lg][:].rearrange("q i c -> q (i c)")
            nc.vector.tensor_tensor(
                out=flat,
                in0=st["maxes", lg][:].rearrange("q i c -> q (i c)"),
                in1=flat,
                op=ALU.subtract,
            )

        def log_prod(n):
            a_flat = st["d", n][:].rearrange("q s t k -> q s (t k)")
            nc.vector.scalar_tensor_tensor(
                out=a_flat,
                in0=a_flat,
                scalar=2.0,
                in1=st["sum", n][1]
                .rearrange("q t k -> q (t k)")
                .unsqueeze(1)
                .to_broadcast([P, S4, 8 * K]),
                op0=ALU.mult,
                op1=ALU.add,
            )

        def exp_prod(n, gp):
            a = st["d", n]
            for t in range(4 * gp, 4 * gp + 4):
                for s in range(S4):
                    nc.scalar.activation(
                        out=a[:, s, t, :],
                        in_=a[:, s, t, :],
                        func=ACT.Exp,
                        bias=st["sum", n][0][:, t, s : s + 1],
                        scale=1.0,
                    )

        def low_high(n, half):
            a = st["d", n]
            ts = slice(0, 8) if half is None else slice(4 * half, 4 * half + 4)
            return tuple(
                a[:, s : s + 2, ts, :].rearrange("q s t k -> q s (t k)") for s in (0, 2)
            )

        def plus_one(n, half=None, engine=nc.vector):
            low, high = low_high(n, half)
            engine.tensor_scalar(
                out=high, in0=high, scalar1=1.0, scalar2=1.0, op0=ALU.mult, op1=ALU.add
            )

        def pair_mult(n, half=None):
            low, high = low_high(n, half)
            nc.vector.scalar_tensor_tensor(
                out=low, in0=low, scalar=1.0, in1=high, op0=ALU.add, op1=ALU.mult
            )

        def mult(n, half=None):
            a = st["d", n]
            if half != 1:
                st["multf", n] = mfp.tile([P, 8, K], F32, tag="multf", name="multf")
            ts = slice(0, 8) if half is None else slice(4 * half, 4 * half + 4)
            nc.vector.tensor_tensor(
                out=st["multf", n][:, ts, :], in0=a[:, 0, ts, :], in1=a[:, 1, ts, :], op=ALU.mult
            )

        def round_mult(n, half=None):
            i = n % GRP
            gs = slice(0, 2) if half is None else slice(half, half + 1)
            ts = slice(0, 8) if half is None else slice(4 * half, 4 * half + 4)
            nc.vector.tensor_copy(
                out=mb[i][:, gs, K * i : K * i + K, :],
                in_=st["multf", n][:, ts, :].rearrange("q (g t) k -> q g k t", t=4),
            )

        def qm(n, half=None):
            if half != 1:
                mc = smp.tile([P, 2 * P], U32, tag="mc", name="mc", align_bytes=64)
                msc = smp.tile([P, 2 * P], U8, tag="msc", name="msc", align_bytes=64)
                st["m", n] = (mc, msc)
            mc, msc = st["m", n]
            gs = slice(0, 2) if half is None else slice(half, half + 1)
            cols = slice(0, 2 * P) if half is None else slice(P * half, P * half + P)
            nc.vector.quantize_mx(
                out=mc[:, cols].bitcast(FP8X4),
                scales=msc[:, cols],
                in_=mb[n % GRP][:, gs].rearrange("q g c t -> q (g c t)"),
            )

        def g2_tile(n, gp):
            st["g2", n, gp] = g2p.tile([P, 4 * C], BF16, tag="g2", name="g2", align_bytes=64)

        def xtr(n, gp, rp):
            raw_w = st["raw", n, gp][:].bitcast(F32)
            xt = ps_xt.tile([P, 2, 2, P], F32, tag="xt", name="xt")
            st["xt", n, gp, rp] = xt
            for rl in range(2):
                for u in range(2):
                    nc.tensor.transpose(
                        xt[:, rl, u, :], raw_w[:, 2 * rp + rl, P * u : P * u + P], ident_f[:]
                    )

        def xev(n, gp, rp, copy=nc.scalar.copy):
            g2w = st["g2", n, gp][:].bitcast(F32).rearrange("q (c u) -> q c u", u=2)
            copy(
                out=g2w[:, 256 * rp : 256 * rp + 256, :].rearrange("q (rl p) u -> q rl p u", rl=2),
                in_=st["xt", n, gp, rp][:].rearrange("q rl u p -> q rl p u"),
            )

        def q2(n, gp):
            if gp == 0:
                c2 = c2p.tile([P, 2, C], U32, tag="c2", name="c2", align_bytes=64)
                s2x = c2p.tile([P, 2, C], U8, tag="s2x", name="s2x", align_bytes=64)
                st["c2", n] = (c2, s2x)
            c2, s2x = st["c2", n]
            nc.vector.quantize_mx(
                out=c2[:, gp, :].bitcast(FP8X4), scales=s2x[:, gp, :], in_=st["g2", n, gp][:]
            )

        def vmm(n, halves=(0, 1)):
            i = n % GRP
            if i == 0:
                st["v"] = [
                    ps_v.tile([P, 512], F32, tag="v%d" % hc, name="v_ps%d" % hc) for hc in range(2)
                ]
            mc, msc = st["m", n]
            c2, s2x = st["c2", n]
            for gp in halves:
                for hc in range(2):
                    nc.tensor.matmul_mx(
                        out=st["v"][hc][:],
                        lhsT=mc[:, P * gp : P * gp + P].bitcast(FP8X4),
                        lhsT_scale=msc[:, P * gp : P * gp + P],
                        rhs=c2[:, gp, 512 * hc : 512 * hc + 512].bitcast(FP8X4),
                        rhs_scale=s2x[:, gp, 512 * hc : 512 * hc + 512],
                        start=(i == 0 and gp == 0),
                        stop=(i == GRP - 1 and gp == 1),
                    )

        def ep_part(grp, images=range(GRP)):
            if 0 in images:
                st["small"] = ps_xt.tile([P, 16], F32, tag="xt", name="small")
            for j in images:
                for g in range(2):
                    nc.tensor.matmul(
                        out=st["small"][:, 2 * j : 2 * j + 2],
                        lhsT=st["multf", GRP * grp + j][:, 4 * g : 4 * g + 4, :].rearrange(
                            "q t k -> q (t k)"
                        ),
                        rhs=ones2[:],
                        start=(g == 0),
                        stop=(g == 1),
                    )

        def ep_spread():
            st["spread"] = epi.tile([P, GRP, K], F32, tag="spread", name="spread")
            nc.vector.tensor_tensor(
                out=st["spread"][:],
                in0=st["small"][:, 0 : 2 * GRP : 2].unsqueeze(2).to_broadcast([P, GRP, K]),
                in1=sel[:].unsqueeze(1).to_broadcast([P, GRP, K]),
                op=ALU.mult,
            )

        def ep_msum():
            nc.tensor.matmul(
                out=st["small"][:, 8:10],
                lhsT=st["spread"][:].rearrange("p i k -> p (i k)"),
                rhs=ones2[:],
                start=True,
                stop=True,
            )

        def ep_neg():
            st["negms"] = epi.tile([P, 1], F32, tag="negms", name="negms")
            nc.vector.tensor_scalar_mul(
                out=st["negms"][:], in0=st["small"][:, 8:9], scalar1=-1.0
            )

        def ep_v2(grp, hc):
            if hc == 0:
                st["v2", grp] = v2p.tile([P, C], F32, tag="v2", name="v2")
            nc.vector.scalar_tensor_tensor(
                out=st["v2", grp][:, 512 * hc : 512 * hc + 512],
                in0=rep4[:, 512 * hc : 512 * hc + 512],
                scalar=st["negms"][:, 0:1],
                in1=st["v"][hc][:],
                op0=ALU.mult,
                op1=ALU.add,
            )

        def ep_sq(grp, hc):
            if hc == 0:
                st["sq"] = v2p.tile([P, C], BF16, tag="sq", name="sq")
                st["ss"] = epi.tile([P, 2], F32, tag="ss", name="ss")
            half_c = slice(512 * hc, 512 * hc + 512)
            nc.scalar.activation(
                out=st["sq"][:, half_c],
                in_=st["v2", grp][:, half_c],
                func=ACT.Square,
                accum_out=st["ss"][:, hc : hc + 1],
            )

        def ep_rn1():
            st["ssc"] = epi.tile([P, 1], F32, tag="ssc", name="ssc")
            nc.vector.tensor_scalar(
                out=st["ssc"][:],
                in0=st["ss"][:, 0:1],
                scalar1=st["ss"][:, 1:2],
                scalar2=EPS * EPS,
                op0=ALU.add,
                op1=ALU.max,
            )
            st["rn1"] = epi.tile([P, 1], F32, tag="rn1", name="rn1")
            nc.gpsimd.tensor_tensor(out=st["rn1"][:], in0=st["ssc"][:], in1=mhalf[:], op=ALU.pow)

        def ep_q2():
            st["sst"] = epi.tile([P, 2], F32, tag="sst", name="sst")
            nc.vector.tensor_tensor(
                out=st["sst"][:],
                in0=st["ss"][:, 0:1].to_broadcast([P, 2]),
                in1=st["ss"][:, 1:2].to_broadcast([P, 2]),
                op=ALU.add,
            )
            inv = epi.tile([P, 1], F32, tag="inv", name="inv")
            nc.vector.reciprocal(out=inv[:], in_=st["ssc"][:])
            st["q2"] = epi.tile([P, 2], F32, tag="q2", name="q2")
            nc.vector.tensor_scalar_mul(
                out=st["q2"][:], in0=st["sst"][:], scalar1=inv[:, 0:1]
            )

        def ep_tot():
            st["tot"] = ps_xt.tile([P, 2], F32, tag="xt", name="tot")
            nc.tensor.matmul(out=st["tot"][:], lhsT=bd[:], rhs=st["q2"][:], start=True, stop=True)

        def ep_rn2():
            totc = epi.tile([P, 1], F32, tag="totc", name="totc")
            nc.vector.tensor_scalar_max(out=totc[:], in0=st["tot"][:, 0:1], scalar1=EPS * EPS)
            st["rn2"] = epi.tile([P, 1], F32, tag="rn2", name="rn2")
            nc.gpsimd.tensor_tensor(out=st["rn2"][:], in0=totc[:], in1=mhalf[:], op=ALU.pow)

        def ep_scale(grp, hc):
            half_c = slice(512 * hc, 512 * hc + 512)
            nc.vector.tensor_scalar(
                out=st["v2", grp][:, half_c],
                in0=st["v2", grp][:, half_c],
                scalar1=st["rn1"][:, 0:1],
                scalar2=st["rn2"][:, 0:1],
                op0=ALU.mult,
                op1=ALU.mult,
            )

        def ep_store(grp, hc):
            half_c = slice(512 * hc, 512 * hc + 512)
            nc.sync.dma_start(
                out=out[4 * grp : 4 * grp + 4, :].rearrange("i (k c) -> (i k) c", c=C)[:, half_c],
                in_=st["v2", grp][:, half_c],
            )

        end = N_IMG - 1
        st["pl"] = None

        def step(i):
            n = i if i >= 0 else None
            nz = i + 1 if i >= -1 else None
            p = i + 1 if -1 <= i else None
            pl = st["pl"]
            na = i + 2 if i + 2 <= end else None
            j = i - 2 if i >= 2 else None
            jt = i - 3 if i >= 3 else None
            ends = range(GRP - 1, end, GRP)
            g1 = (i - 4) // GRP if i - 4 in ends else None
            g2 = (i - 5) // GRP if i - 5 in ends else None
            g3 = (i - 6) // GRP if i - 6 in ends else None
            g4 = (i - 7) // GRP if i - 7 in ends else None
            lg = (i - 2) // LNG if i >= 2 and i % LNG == 0 else None

            if 2 <= i + 3 <= end:
                load(i + 3, 0)
                load(i + 3, 1)
            if n is not None:
                soft_tiles(n)
            if na is not None:
                g1_tile(na, 0)
                g1_tile(na, 1)
            if p is not None:
                g2_tile(p, 0)

            if n is not None:
                max_s(n, 0)
                if n > 0:
                    gate(n)
                    sums(n - 1)
                if jt is not None:
                    plus_one(jt, engine=nc.gpsimd)
                max_k(n, 0)
            if g3 is not None:
                ep_rn1()
            if g4 is not None:
                ep_rn2()
            if n is not None:
                sub_s(n, 0)
                max_s(n, 1)
                max_k(n, 1)
                sub_s(n, 1)
            if nz is not None:
                q1(nz, 1)
            for r in range(4):
                if p is not None:
                    xtr(p, 0, r)
                if r == 1 and nz is not None:
                    zmm(nz, 0)
                if p is not None:
                    xev(p, 0, r)
                if r < 2 and na is not None:
                    il_s(na, 0, r)
                if r == 3 and lg is not None:
                    log_sums(lg)
                if r == 2 and nz is not None:
                    zbt(nz, 0)
            if g1 is not None:
                ep_part(g1)
            if pl is not None:
                q2(pl, 1)
            if n is not None:
                exp_k(n, 0)
            if nz == end:
                zmm(nz, 1)
                zbt(nz, 1)
            if n is not None:
                exp_k(n, 1)
                exp_s(n)
            if na is not None:
                il_v(na, 0, 0)
            if g1 is not None:
                ep_spread()
                ep_msum()
            if jt is not None:
                pair_mult(jt)
            if na is not None:
                il_v(na, 0, 1)
            if g1 is not None:
                ep_neg()
            if jt is not None:
                mult(jt)
            if i == -2:
                prep_norm()
                prep_w()

            if lg is not None:
                log_sum_exps(lg)
            if jt is not None:
                round_mult(jt)
            if g4 is not None:
                ep_scale(g4, 0)
            if g3 is not None:
                ep_q2()
            if g1 is not None:
                ep_v2(g1, 0)
            if p is not None:
                q2(p, 0)
            if p == end:
                p = None
            if p is not None:
                g2_tile(p, 1)
            if g1 is not None:
                ep_v2(g1, 1)
            if jt is not None:
                qm(jt)
            if j is not None:
                log_prod(j)
            if nz is not None and nz < end:
                zmm(nz, 1)
            for r in range(4):
                if r == 2 and nz is not None:
                    ztr(nz, 0)
                    ztr(nz, 1)
                if p is not None:
                    xtr(p, 1, r)
                    xev(p, 1, r)
                if r == 0 and nz is not None and nz < end:
                    zbt(nz, 1)
                if r < 2 and na is not None:
                    il_s(na, 1, r)
                if r < 2 and g2 is not None:
                    ep_sq(g2, r)
            st["pl"] = p
            if g3 is not None:
                ep_tot()
            if j is not None:
                exp_prod(j, 0)
                exp_prod(j, 1)
            if jt is not None:
                vmm(jt)
            if na is not None:
                il_v(na, 1, 0)
            if i == -2:
                prep_wq()
            if na is not None:
                q1(na, 0)
            if na is not None:
                il_v(na, 1, 1)
            if i == -2:
                prep_b()
            if g4 is not None:
                ep_scale(g4, 1)
                ep_store(g4, 0)
                ep_store(g4, 1)

        def finish():
            soft_tiles(end)
            g2_tile(end, 1)
            ep_part(LAST - 1)
            max_s(end, 0)
            sums(end - 1)
            max_k(end, 0)
            max_s(end, 1)
            max_k(end, 1)
            sub_s(end, 0)
            sub_s(end, 1)
            exp_k(end, 0)
            exp_k(end, 1)
            exp_s(end)
            log_prod(end - 2)
            plus_one(end - 3)
            ep_spread()
            ep_msum()
            pair_mult(end - 3)
            ep_neg()
            exp_prod(end - 2, 0)
            exp_prod(end - 2, 1)
            mult(end - 3)
            for r in range(3):
                xtr(end, 1, r)
            for r in range(3):
                xev(end, 1, r, nc.vector.tensor_copy)
            half_sum(end)
            round_mult(end - 3)
            sum_s(end)
            log_sums(end // LNG)
            load_exp()
            xtr(end, 1, 3)
            ep_v2(LAST - 1, 0)
            ep_v2(LAST - 1, 1)
            ep_sq(LAST - 1, 0)
            ep_sq(LAST - 1, 1)
            xev(end, 1, 3, nc.vector.tensor_copy)
            qm(end - 3)
            vmm(end - 3)
            q2(end, 1)
            plus_one(end - 2)
            log_sum_exps(end // LNG)
            pair_mult(end - 2)
            log_prod(end - 1)
            log_prod(end)
            exp_prod(end - 1, 0)
            exp_prod(end - 1, 1)
            exp_prod(end, 0)
            exp_prod(end, 1)
            mult(end - 2)
            ep_rn1()
            ep_q2()
            round_mult(end - 2)
            plus_one(end - 1)
            qm(end - 2)
            dummy = ps_xt.tile([P, 512], F32, tag="xt", name="dummy")
            for g in range(12):
                nc.tensor.matmul(
                    out=dummy[:],
                    lhsT=ident_b[:],
                    rhs=st["wg"][:, g % 2].rearrange("p m j -> p (m j)"),
                    start=True,
                    stop=True,
                )
            vmm(end - 2)
            ep_tot()
            pair_mult(end - 1)
            plus_one(end, 0)
            mult(end - 1)
            pair_mult(end, 0)
            round_mult(end - 1)
            plus_one(end, 1)
            qm(end - 1)
            ep_rn2()
            ep_part(LAST, range(GRP - 2))
            vmm(end - 1)
            mult(end, 0)
            pair_mult(end, 1)
            round_mult(end, 0)
            mult(end, 1)
            ep_part(LAST, range(GRP - 2, GRP))
            qm(end, 0)
            vmm(end, (0,))
            round_mult(end, 1)
            ep_scale(LAST - 1, 0)
            qm(end, 1)
            ep_spread()
            ep_msum()
            vmm(end, (1,))
            ep_scale(LAST - 1, 1)
            ep_store(LAST - 1, 0)
            ep_store(LAST - 1, 1)
            ep_neg()
            for hc in range(2):
                ep_v2(LAST, hc)
                ep_sq(LAST, hc)
            ep_rn1()
            ep_q2()
            ep_tot()
            ep_rn2()
            for hc in range(2):
                ep_scale(LAST, hc)
                ep_store(LAST, hc)

        for i in range(-2, end):
            step(i)
        finish()
